import numpy as np
import ml_dtypes


def mxq(x, axis, fmt="e4m3"):
    dtype, down = {"e4m3": (ml_dtypes.float8_e4m3fn, 7), "e5m2": (ml_dtypes.float8_e5m2, 14)}[fmt]
    v = np.moveaxis(np.asarray(x, np.float32).astype(ml_dtypes.bfloat16).astype(np.float64), axis, -1)
    blocks = v.reshape(v.shape[:-1] + (-1, 32))
    amax = np.abs(blocks).max(-1, keepdims=True)
    byte = np.maximum(np.where(amax > 0, np.frexp(amax)[1] - 1 + 127, 0) - down, 1)
    scale = np.exp2(byte - 127.0)
    codes = (blocks / scale).astype(np.float32).astype(dtype).astype(np.float64)
    return np.moveaxis((codes * scale).reshape(v.shape), -1, axis)


WIDE = False


def mx_kscale(k):
    if not WIDE:
        return np.ones(k)
    levels = np.array([10, -10, 5, -5, 0])
    a = np.random.permutation(np.resize(levels, k // 512 * 4)).reshape(k // 512, 4)
    idx = np.arange(k)
    return np.exp2(a[idx // 512, idx % 128 // 32])


BF16 = ml_dtypes.bfloat16


def bf(x):
    return np.asarray(x, np.float32).astype(BF16)


def f64(x):
    return np.asarray(x).astype(np.float64)


B, T_IN, T_OUT, N, FEAT, HID, OUT, GRID_SIZE, SPLINE_ORDER = 2, 128, 128, 512, 8, 512, 64, 5, 3
M = B * N
KX = T_IN * FEAT
KY = T_OUT * FEAT
CAT = HID + HID
COEF = GRID_SIZE + SPLINE_ORDER
KS = HID * COEF
GRID_LO, GRID_HI = -1.0, 1.0


def silu(v):
    return v / (1.0 + np.exp(-v))


def make_grid():
    step = (GRID_HI - GRID_LO) / GRID_SIZE
    return np.arange(-SPLINE_ORDER, GRID_SIZE + SPLINE_ORDER + 1) * step + GRID_LO


def b_splines(x, grid):
    x = x[..., None]
    bases = np.where((x >= grid[:-1]) & (x < grid[1:]), 1.0, 0.0)
    for k in range(1, SPLINE_ORDER + 1):
        left = (x - grid[:-(k + 1)]) / (grid[k:-1] - grid[:-(k + 1)])
        right = (grid[k + 1:] - x) / (grid[k + 1:] - grid[1:-k])
        bases = left * bases[..., :-1] + right * bases[..., 1:]
    return bases


def setup_inputs():
    sx, sy = mx_kscale(KX), mx_kscale(KY)
    return {
        "X": bf(np.random.standard_normal((B, T_IN, N, FEAT)) * sx.reshape(T_IN, 1, FEAT)),
        "Y": bf(np.random.standard_normal((B, T_OUT, N, FEAT)) * sy.reshape(T_OUT, 1, FEAT)),
        "Wx": bf(np.random.standard_normal((HID, KX)) / np.sqrt(KX) / sx),
        "bx": bf(np.random.standard_normal(HID) * 0.3),
        "Wy": bf(np.random.standard_normal((HID, KY)) / np.sqrt(KY) / sy),
        "by": bf(np.random.standard_normal(HID) * 0.3),
        "base_w": bf(np.random.standard_normal((OUT, CAT)) * 3.0 / np.sqrt(CAT)),
        "spline_w": bf(np.random.standard_normal((OUT, CAT, COEF))),
        "spline_scaler": bf(np.random.standard_normal((OUT, CAT)) * 1.5 / np.sqrt(CAT)),
    }


def reference(X, Y, Wx, bx, Wy, by, base_w, spline_w, spline_scaler):
    Xf = f64(X).transpose(0, 2, 1, 3).reshape(M, KX)
    Yf = f64(Y).transpose(0, 2, 1, 3).reshape(M, KY)
    Hx = np.tanh((mxq(Xf, 1, "e4m3") @ mxq(f64(Wx), 1, "e4m3").T) + f64(bx))
    Hy = np.tanh((mxq(Yf, 1, "e4m3") @ mxq(f64(Wy), 1, "e4m3").T) + f64(by))
    grid = make_grid()
    act = np.stack([silu(Hx), silu(Hy)])
    bases = np.stack([b_splines(Hx, grid).reshape(M, KS), b_splines(Hy, grid).reshape(M, KS)])
    bw = f64(base_w)
    bw2 = np.stack([bw[:, :HID], bw[:, HID:]])
    sw = f64(spline_w) * f64(spline_scaler)[..., None]
    sw2 = np.stack([sw[:, :HID].reshape(OUT, KS), sw[:, HID:].reshape(OUT, KS)])
    base_out = (mxq(act, 2, "e4m3") @ mxq(bw2, 2, "e4m3").transpose(0, 2, 1)).sum(0)
    spline_out = (mxq(bases, 2, "e4m3") @ mxq(sw2, 2, "e4m3").transpose(0, 2, 1)).sum(0)
    return (base_out + spline_out).reshape(B, N, OUT)

@@ -1,0 +1,321 @@
+import math
+from contextlib import ExitStack
+
+import concourse.mybir as mybir
+from concourse.masks import make_identity
+
+F32 = mybir.dt.float32
+BF16 = mybir.dt.bfloat16
+U32 = mybir.dt.uint32
+U8 = mybir.dt.uint8
+FP8X4 = mybir.dt.float8_e4m3fn_x4
+ACTF = mybir.ActivationFunctionType
+ALU = mybir.AluOpType
+
+P = 128
+FLOPS = 2 * 2 * 1024 * 1024 * 512 + 2 * 1024 * 64 * (1024 + 8192)
+MC = 256
+CW = 4 * MC
+KFAM = ((0, 6, 4, 2), (7, 5, 3, 1))
+ACT_W = 256
+
+
+def central_constants():
+    a0 = -0.7
+    for i in range(80):
+        a0 = a0 - (a0 ** 3 - 2.0 * a0 ** 2 + 4.0 / 3.0) / (3.0 * a0 ** 2 - 4.0 * a0)
+    b = a0 - 2.0
+    return a0, b / 2.0, a0 * b - b * b / 4.0
+
+
+def tile_refiner_pa_kernel(tc, X, Y, Wx, bx, Wy, by, base_w, spline_w, spline_scaler, out):
+    nc = tc.nc
+    a0, hb, cp = central_constants()
+    r6 = 1.0 / math.sqrt(6.0)
+    rc = math.sqrt(2.5 / 6.0)
+    bias_vals = (-0.5, 0.5, -2.0, -1.0, -2.0 * r6, hb, 1.0 + hb, -a0 / 2.0, (1.0 - a0) / 2.0)
+    (B_M05, B_P05, B_M2, B_M1, B_M2R6, B_HB, B_1HB, B_L1, B_L2) = range(9)
+
+    with ExitStack() as ctx:
+        keep = ctx.enter_context(tc.tile_pool(name="keep", bufs=1))
+        prep = ctx.enter_context(tc.tile_pool(name="prep", bufs=1))
+        work = ctx.enter_context(tc.tile_pool(name="work", bufs=2))
+        psum = ctx.enter_context(tc.psum_pool(name="psum", bufs=1))
+
+        ident_f = keep.tile([P, P], F32, name="ident_f")
+        make_identity(nc, ident_f[:])
+        ident_b = keep.tile([P, P], BF16, name="ident_b")
+        make_identity(nc, ident_b[:])
+        ones = keep.tile([P, 8], F32, name="ones")
+        nc.vector.memset(ones[:], 1.0)
+        cb = keep.tile([P, 16], F32, name="cb")
+        for i, v in enumerate(bias_vals):
+            nc.scalar.activation(out=cb[:, i : i + 1], in_=ones[:, 0:1], func=ACTF.Copy, scale=v)
+
+        def cbias(i):
+            return cb[:, i : i + 1]
+
+        brow = keep.tile([P, P], BF16, name="brow")
+        nc.vector.memset(brow[:], 0.0)
+        nc.sync.dma_start(out=brow[0:4, :], in_=bx.rearrange("(r c) -> r c", c=P))
+        nc.sync.dma_start(out=brow[4:8, :], in_=by.rearrange("(r c) -> r c", c=P))
+
+        def load_w(w, nm):
+            wr = prep.tile([P, 4096], BF16, name=nm, tag="raw", bufs=3)
+            nc.sync.dma_start(out=wr[:].rearrange("p (j k) -> p j k", j=4), in_=w.rearrange("(j p) k -> p j k", p=P))
+            return wr
+
+        def load_x(x, b, nm):
+            xr = prep.tile([P, 4096], BF16, name=nm, tag="raw", bufs=3)
+            src = x[b].rearrange("(a c) n f -> c a (n f)", c=16)
+            for cl in range(4):
+                for s in range(4):
+                    nc.sync.dma_start(out=xr[32 * cl + s : 32 * cl + 32 : 4, :], in_=src[4 * cl + s])
+            return xr
+
+        w_raw = [None, None]
+        x_raw = {}
+        w_raw[0] = load_w(Wx, "wxr")
+        x_raw[(0, 0)] = load_x(X, 0, "x0r")
+        w_raw[1] = load_w(Wy, "wyr")
+        scr = prep.tile([P, 512], BF16, name="scr")
+        bwr = prep.tile([P, 512], BF16, name="bwr")
+        for sg in range(2):
+            rows = slice(64 * sg, 64 * sg + 64)
+            cols = slice(512 * sg, 512 * sg + 512)
+            nc.sync.dma_start(out=scr[rows, :], in_=spline_scaler[:, cols])
+            nc.sync.dma_start(out=bwr[rows, :], in_=base_w[:, cols])
+
+        pb0 = psum.tile([P, P], BF16, name="pb0", tag="s1", bufs=5)
+        nc.tensor.transpose(pb0[:], brow[:], ident_b[:])
+        bias = keep.tile([P, 8], F32, name="bias")
+        nc.vector.tensor_copy(out=bias[:], in_=pb0[:, 0:8])
+
+        w_codes = []
+        w_scales = []
+
+        def prep_w(sg):
+            wrw = w_raw[sg][:].bitcast(F32).rearrange("p (j a c s f) -> p j f c a s", j=4, a=8, c=4, s=4, f=4)
+            wg = prep.tile([P, 2048], F32, name="wg%d" % sg, tag="grp", bufs=2, align_bytes=64)
+            wtg = prep.tile([P, 4096], BF16, name="wtg%d" % sg, tag="grp", bufs=2, align_bytes=64)
+            wtw = wtg[:].bitcast(F32)
+            for j in range(4):
+                nc.vector.tensor_copy(
+                    out=wg[:, 512 * j : 512 * j + 512].rearrange("p (f c a s) -> p f c a s", f=4, c=4, a=8, s=4),
+                    in_=wrw[:, j],
+                )
+            for j in range(4):
+                pt = psum.tile([P, 512], F32, name="ptw%d%d" % (sg, j), tag="s1", bufs=5)
+                for f in range(4):
+                    nc.tensor.transpose(pt[:, P * f : P * f + P], wg[:, 512 * j + P * f : 512 * j + P * f + P], ident_f[:])
+                nc.scalar.copy(
+                    out=wtw[:, 512 * j : 512 * j + 512].rearrange("p (h i e) -> p h i e", h=2, e=2),
+                    in_=pt[:].rearrange("p (h e i) -> p h i e", h=2, e=2),
+                )
+            wc = keep.tile([P, 1024], U32, name="wc%d" % sg, align_bytes=64)
+            ws = keep.tile([P, 1024], U8, name="ws%d" % sg, align_bytes=64)
+            nc.vector.quantize_mx(out=wc[:].bitcast(FP8X4), scales=ws[:], in_=wtg[:])
+            w_codes.append(wc)
+            w_scales.append(ws)
+
+        swc = keep.tile([P, 9 * P], U32, name="swc", align_bytes=64)
+        sws = keep.tile([P, 9 * P], U8, name="sws", align_bytes=64)
+
+        def load_sw():
+            swr = prep.tile([P, 4096], BF16, name="swr", tag="raw", bufs=3)
+            for sg in range(2):
+                nc.sync.dma_start(
+                    out=swr[64 * sg : 64 * sg + 64, :],
+                    in_=spline_w[:, 512 * sg : 512 * sg + 512, :].rearrange("o i k -> o (i k)"),
+                )
+            return swr
+
+        def prep_sw(swr):
+            swg = prep.tile([P, 2048], F32, name="swg", tag="grp", bufs=2, align_bytes=64)
+            nc.vector.tensor_copy(
+                out=swg[:].rearrange("p (k i) -> p k i", k=4),
+                in_=swr[:].bitcast(F32).rearrange("p (i k) -> p k i", k=4),
+            )
+            swt = prep.tile([P, 9 * 512], BF16, name="swt", align_bytes=64)
+            psc = psum.tile([P, 512], BF16, name="psc", tag="s1", bufs=5)
+            pbw = psum.tile([P, 512], BF16, name="pbw", tag="s1", bufs=5)
+            for j in range(4):
+                nc.tensor.transpose(psc[:, P * j : P * j + P], scr[:, P * j : P * j + P], ident_b[:])
+            for j in range(4):
+                nc.tensor.transpose(pbw[:, P * j : P * j + P], bwr[:, P * j : P * j + P], ident_b[:])
+            sct = prep.tile([P, 512], BF16, name="sct")
+            nc.scalar.copy(out=sct[:], in_=psc[:])
+            nc.scalar.copy(
+                out=swt[:, 8 * 512 : 9 * 512].rearrange("p (q j) -> p q j", j=4),
+                in_=pbw[:].rearrange("p (j q) -> p q j", j=4),
+            )
+            swp = prep.tile([P, 4096], BF16, name="swp", tag="grp", bufs=2, align_bytes=64)
+            for kk in range(4):
+                pt = psum.tile([P, 512], F32, name="pts%d" % kk, tag="s1", bufs=5)
+                for j in range(4):
+                    nc.tensor.transpose(pt[:, P * j : P * j + P], swg[:, 512 * kk + P * j : 512 * kk + P * j + P], ident_f[:])
+                pairs = pt[:].bitcast(BF16).rearrange("p (w e) -> p e w", e=2)
+                for e in range(2):
+                    k = 2 * kk + e
+                    plane = 4 * (k % 2) + KFAM[k % 2].index(k)
+                    nc.vector.tensor_tensor(out=swp[:, 512 * plane : 512 * plane + 512], in0=pairs[:, e], in1=sct[:], op=ALU.mult)
+            for fam in range(2):
+                nc.vector.tensor_copy(
+                    out=swt[:, 0:4096].rearrange("p (t f q j) -> p f t q j", t=4, f=2, j=4)[:, fam],
+                    in_=swp[:].rearrange("p (f j t q) -> p f t q j", f=2, j=4, t=4)[:, fam],
+                )
+            nc.vector.quantize_mx(out=swc[:, 0:1024].bitcast(FP8X4), scales=sws[:, 0:1024], in_=swt[:, 0:4096])
+            nc.vector.quantize_mx(out=swc[:, 1024:1152].bitcast(FP8X4), scales=sws[:, 1024:1152], in_=swt[:, 4096:4608])
+
+        def prep_x(sg, b, h):
+            xg = work.tile([P, 2048], BF16, name="xg", align_bytes=64)
+            nc.vector.tensor_copy(
+                out=xg[:].bitcast(F32).rearrange("p (h n w) -> p h n w", h=2, w=2),
+                in_=x_raw[(sg, b)][:].bitcast(F32).rearrange("p (n h w) -> p h n w", h=2, w=2)[:, :, MC * h : MC * h + MC, :],
+            )
+            xc = work.tile([P, 512], U32, name="xc", align_bytes=64)
+            xs = work.tile([P, 512], U8, name="xs", align_bytes=64)
+            nc.vector.quantize_mx(out=xc[:].bitcast(FP8X4), scales=xs[:], in_=xg[:])
+            return xc, xs
+
+        def stage1(sg, xc, xs):
+            xt = work.tile([P, CW], F32, name="xt")
+            for jj in range(2):
+                ps = psum.tile([P, 512], F32, name="ps1", tag="s1", bufs=5)
+                for j2 in range(2):
+                    j = 2 * jj + j2
+                    for half in range(2):
+                        wcol = slice(256 * j + P * half, 256 * j + P * half + P)
+                        xcol = slice(MC * half, MC * half + MC)
+                        nc.tensor.matmul_mx(
+                            out=ps[:, MC * j2 : MC * j2 + MC],
+                            lhsT=w_codes[sg][:, wcol].bitcast(FP8X4),
+                            lhsT_scale=w_scales[sg][:, wcol],
+                            rhs=xc[:, xcol].bitcast(FP8X4),
+                            rhs_scale=xs[:, xcol],
+                            start=(half == 0),
+                            stop=(half == 1),
+                        )
+                for j2 in range(2):
+                    j = 2 * jj + j2
+                    nc.scalar.activation(
+                        out=xt[:, MC * j : MC * j + MC],
+                        in_=ps[:, MC * j2 : MC * j2 + MC],
+                        func=ACTF.Tanh,
+                        bias=bias[:, 4 * sg + j : 4 * sg + j + 1],
+                        scale=1.0,
+                    )
+            return xt
+
+        def act(nm, src, func, scale, bi, tag, bufs):
+            t = work.tile([P, CW], F32, name=nm, tag=tag, bufs=bufs)
+            if bi is None:
+                nc.scalar.activation(out=t[:], in_=src[:], func=func, scale=scale)
+            else:
+                nc.scalar.activation(out=t[:], in_=src[:], func=func, bias=cbias(bi), scale=scale)
+            return t
+
+        def product(dst, in0, scalar, in1):
+            nc.vector.scalar_tensor_tensor(out=dst, in0=in0[:], scalar=scalar, in1=in1[:], op0=ALU.add, op1=ALU.mult)
+
+        def interleave(dst, planes, width, scale):
+            o = dst.rearrange("p (c i j) -> p c j i", i=4, j=4)
+            s = planes.rearrange("p j (c i) -> p c j i", i=4)
+            cut = (width - ACT_W) // 4 if scale == 1.0 else width // 4
+            if scale == 1.0:
+                nc.vector.tensor_scalar(out=o[:, 0:cut], in0=s[:, 0:cut], scalar1=0.0, scalar2=None, op0=ALU.max)
+                nc.scalar.activation(out=o[:, cut : width // 4], in_=s[:, cut : width // 4], func=ACTF.Relu)
+            else:
+                nc.vector.tensor_scalar(out=o, in0=s, scalar1=scale, scalar2=None, op0=ALU.mult)
+
+        def bases(x):
+            codes = work.tile([P, 9 * MC], U32, name="codes", align_bytes=64)
+            scl = work.tile([P, 9 * MC], U8, name="scl", align_bytes=64)
+            pl = [work.tile([P, 4, CW], BF16, name="pl%d" % f, tag="pl", bufs=3, align_bytes=64) for f in range(2)]
+
+            f1 = act("f1", x, ACTF.Abs, 2.5, B_M05, "f1", 2)
+            g2 = act("g2", f1, ACTF.Abs, 1.0, B_M2, "fold", 2)
+            s4 = act("s4", g2, ACTF.Square, r6, None, "sq", 3)
+            product(pl[0][:, 0, :], f1, -2.0, s4)
+            s6 = act("s6", f1, ACTF.Square, rc, None, "sq", 3)
+            product(pl[0][:, 1, :], x, -0.2, s6)
+            a3 = act("a3", x, ACTF.Abs, 2.5, B_P05, "a3", 2)
+            s3 = act("s3", a3, ACTF.Square, r6, B_M2R6, "sq", 3)
+            product(pl[1][:, 0, :], a3, -2.0, s3)
+            s5 = act("s5", a3, ACTF.Square, rc, None, "sq", 3)
+            product(pl[1][:, 1, :], x, 0.2, s5)
+            vb = act("vb", g2, ACTF.Abs, 1.0, B_M1, "fold", 2)
+            caps = []
+            for f, (sc_q, b_q, sc_l, b_l) in enumerate(((-1.0, B_1HB, -0.5, B_L2), (1.0, B_HB, 0.5, B_L1))):
+                q = act("q%d" % f, vb, ACTF.Square, sc_q, b_q, "sq", 3)
+                lin = act("l%d" % f, vb, ACTF.Identity, sc_l, b_l, "lin", 2)
+                cap = work.tile([P, CW], BF16, name="cap%d" % f, align_bytes=64)
+                product(cap[:], q, cp, lin)
+                caps.append(cap)
+            th = act("th", x, ACTF.Tanh, 0.5, None, "sq", 3)
+            s2 = work.tile([P, CW], BF16, name="s2", align_bytes=64)
+            product(s2[:], th, 1.0, x)
+
+            for f in range(2):
+                nc.vector.tensor_scalar(out=pl[f][:, 2:4, :], in0=pl[f][:, 0:2, :], scalar1=-1.0, scalar2=None, op0=ALU.mult)
+                nc.vector.tensor_tensor(
+                    out=pl[f][:, 1:4, :],
+                    in0=pl[f][:, 1:4, :],
+                    in1=caps[f][:].unsqueeze(1).to_broadcast([P, 3, CW]),
+                    op=ALU.min,
+                )
+                fam = work.tile([P, 4 * CW], BF16, name="fam", align_bytes=64)
+                interleave(fam[:], pl[f][:], CW, 1.0)
+                cols = slice(CW * f, CW * f + CW)
+                nc.vector.quantize_mx(out=codes[:, cols].bitcast(FP8X4), scales=scl[:, cols], in_=fam[:])
+            sil = work.tile([P, CW], BF16, name="sil", align_bytes=64)
+            interleave(sil[:], s2[:].rearrange("p (j m) -> p j m", j=4), MC, 0.5)
+            cols = slice(2 * CW, 2 * CW + MC)
+            nc.vector.quantize_mx(out=codes[:, cols].bitcast(FP8X4), scales=scl[:, cols], in_=sil[:])
+            return codes, scl
+
+        def stage2(codes, scl):
+            acc = psum.tile([P, 512], F32, name="acc", tag="acc", bufs=3)
+            for mt in range(2):
+                for step in range(9):
+                    f, j = step // 4, step % 4
+                    m0 = 2 * CW + P * mt if step == 8 else CW * f + MC * j + P * mt
+                    q0 = 8 * P if step == 8 else P * (2 * j + f)
+                    nc.tensor.matmul_mx(
+                        out=acc[:, P * mt : P * mt + P],
+                        lhsT=codes[:, m0 : m0 + P].bitcast(FP8X4),
+                        lhsT_scale=scl[:, m0 : m0 + P],
+                        rhs=swc[:, q0 : q0 + P].bitcast(FP8X4),
+                        rhs_scale=sws[:, q0 : q0 + P],
+                        start=(step == 0),
+                        stop=(step == 8),
+                    )
+            return acc[:, 0:256].rearrange("p (t q) -> p t q", t=2)
+
+        prep_w(0)
+        x_raw[(1, 0)] = load_x(Y, 0, "y0r")
+        first = prep_x(0, 0, 0)
+        prep_w(1)
+        sw_raw = load_sw()
+        prep_sw(sw_raw)
+        x_raw[(0, 1)] = load_x(X, 1, "x1r")
+        for b in range(2):
+            for h in range(2):
+                part = None
+                for sg in range(2):
+                    xc, xs = first if (b, h, sg) == (0, 0, 0) else prep_x(sg, b, h)
+                    if (b, h, sg) == (0, 1, 0):
+                        x_raw[(1, 1)] = load_x(Y, 1, "y1r")
+                    x = stage1(sg, xc, xs)
+                    codes, scl = bases(x)
+                    res = stage2(codes, scl)
+                    if sg == 0:
+                        part = work.tile([P, 2, 64], F32, name="part")
+                        nc.scalar.copy(out=part[:], in_=res[:, :, 0:64])
+                    else:
+                        total = work.tile([P, 2, 64], F32, name="total")
+                        nc.vector.tensor_tensor(out=total[:], in0=res[:, :, 64:128], in1=part[:], op=ALU.add)
+                        nc.sync.dma_start(
+                            out=out[b, MC * h : MC * h + MC, :].rearrange("(t p) o -> p t o", p=P),
+                            in_=total[:],
+                        )

@@ -16,8 +16,9 @@ P = 128
 FLOPS = 2 * 2 * 1024 * 1024 * 512 + 2 * 1024 * 64 * (1024 + 8192)
 MC = 256
 CW = 4 * MC
+NCH = 8
 KFAM = ((0, 6, 4, 2), (7, 5, 3, 1))
-ACT_W = 256
+ACT_W = 320
 
 
 def central_constants():
@@ -41,6 +42,10 @@ def tile_refiner_pa_kernel(tc, X, Y, Wx, bx, Wy, by, base_w, spline_w, spline_sc
         prep = ctx.enter_context(tc.tile_pool(name="prep", bufs=1))
         work = ctx.enter_context(tc.tile_pool(name="work", bufs=2))
         psum = ctx.enter_context(tc.psum_pool(name="psum", bufs=1))
+        ctx.enter_context(tc.manual_schedule())
+
+        def bank(nm, dt):
+            return psum.tile([P, 512], dt, name=nm, tag="s1", bufs=4)
 
         ident_f = keep.tile([P, P], F32, name="ident_f")
         make_identity(nc, ident_f[:])
@@ -48,78 +53,30 @@ def tile_refiner_pa_kernel(tc, X, Y, Wx, bx, Wy, by, base_w, spline_w, spline_sc
         make_identity(nc, ident_b[:])
         ones = keep.tile([P, 8], F32, name="ones")
         nc.vector.memset(ones[:], 1.0)
+        brow = keep.tile([P, P], BF16, name="brow")
+        nc.vector.memset(brow[:], 0.0)
         cb = keep.tile([P, 16], F32, name="cb")
+        warm = keep.tile([P, 8], F32, name="warm")
+        nc.scalar.activation(out=warm[:, 0:1], in_=ones[:, 0:1], func=ACTF.Tanh)
         for i, v in enumerate(bias_vals):
             nc.scalar.activation(out=cb[:, i : i + 1], in_=ones[:, 0:1], func=ACTF.Copy, scale=v)
 
         def cbias(i):
             return cb[:, i : i + 1]
 
-        brow = keep.tile([P, P], BF16, name="brow")
-        nc.vector.memset(brow[:], 0.0)
-        nc.sync.dma_start(out=brow[0:4, :], in_=bx.rearrange("(r c) -> r c", c=P))
-        nc.sync.dma_start(out=brow[4:8, :], in_=by.rearrange("(r c) -> r c", c=P))
-
         def load_w(w, nm):
             wr = prep.tile([P, 4096], BF16, name=nm, tag="raw", bufs=3)
             nc.sync.dma_start(out=wr[:].rearrange("p (j k) -> p j k", j=4), in_=w.rearrange("(j p) k -> p j k", p=P))
             return wr
 
-        def load_x(x, b, nm):
-            xr = prep.tile([P, 4096], BF16, name=nm, tag="raw", bufs=3)
+        def load_x(x, b, xr, lo, hi):
             src = x[b].rearrange("(a c) n f -> c a (n f)", c=16)
             for cl in range(4):
                 for s in range(4):
-                    nc.sync.dma_start(out=xr[32 * cl + s : 32 * cl + 32 : 4, :], in_=src[4 * cl + s])
-            return xr
+                    nc.sync.dma_start(out=xr[32 * cl + s : 32 * cl + 32 : 4, lo:hi], in_=src[4 * cl + s][:, lo:hi])
 
-        w_raw = [None, None]
-        x_raw = {}
-        w_raw[0] = load_w(Wx, "wxr")
-        x_raw[(0, 0)] = load_x(X, 0, "x0r")
-        w_raw[1] = load_w(Wy, "wyr")
-        scr = prep.tile([P, 512], BF16, name="scr")
-        bwr = prep.tile([P, 512], BF16, name="bwr")
-        for sg in range(2):
-            rows = slice(64 * sg, 64 * sg + 64)
-            cols = slice(512 * sg, 512 * sg + 512)
-            nc.sync.dma_start(out=scr[rows, :], in_=spline_scaler[:, cols])
-            nc.sync.dma_start(out=bwr[rows, :], in_=base_w[:, cols])
-
-        pb0 = psum.tile([P, P], BF16, name="pb0", tag="s1", bufs=5)
-        nc.tensor.transpose(pb0[:], brow[:], ident_b[:])
-        bias = keep.tile([P, 8], F32, name="bias")
-        nc.vector.tensor_copy(out=bias[:], in_=pb0[:, 0:8])
-
-        w_codes = []
-        w_scales = []
-
-        def prep_w(sg):
-            wrw = w_raw[sg][:].bitcast(F32).rearrange("p (j a c s f) -> p j f c a s", j=4, a=8, c=4, s=4, f=4)
-            wg = prep.tile([P, 2048], F32, name="wg%d" % sg, tag="grp", bufs=2, align_bytes=64)
-            wtg = prep.tile([P, 4096], BF16, name="wtg%d" % sg, tag="grp", bufs=2, align_bytes=64)
-            wtw = wtg[:].bitcast(F32)
-            for j in range(4):
-                nc.vector.tensor_copy(
-                    out=wg[:, 512 * j : 512 * j + 512].rearrange("p (f c a s) -> p f c a s", f=4, c=4, a=8, s=4),
-                    in_=wrw[:, j],
-                )
-            for j in range(4):
-                pt = psum.tile([P, 512], F32, name="ptw%d%d" % (sg, j), tag="s1", bufs=5)
-                for f in range(4):
-                    nc.tensor.transpose(pt[:, P * f : P * f + P], wg[:, 512 * j + P * f : 512 * j + P * f + P], ident_f[:])
-                nc.scalar.copy(
-                    out=wtw[:, 512 * j : 512 * j + 512].rearrange("p (h i e) -> p h i e", h=2, e=2),
-                    in_=pt[:].rearrange("p (h e i) -> p h i e", h=2, e=2),
-                )
-            wc = keep.tile([P, 1024], U32, name="wc%d" % sg, align_bytes=64)
-            ws = keep.tile([P, 1024], U8, name="ws%d" % sg, align_bytes=64)
-            nc.vector.quantize_mx(out=wc[:].bitcast(FP8X4), scales=ws[:], in_=wtg[:])
-            w_codes.append(wc)
-            w_scales.append(ws)
-
-        swc = keep.tile([P, 9 * P], U32, name="swc", align_bytes=64)
-        sws = keep.tile([P, 9 * P], U8, name="sws", align_bytes=64)
+        def raw_tile(nm):
+            return prep.tile([P, 4096], BF16, name=nm, tag="raw", bufs=3)
 
         def load_sw():
             swr = prep.tile([P, 4096], BF16, name="swr", tag="raw", bufs=3)
@@ -130,58 +87,146 @@ def tile_refiner_pa_kernel(tc, X, Y, Wx, bx, Wy, by, base_w, spline_w, spline_sc
                 )
             return swr
 
-        def prep_sw(swr):
+        w_raw = [None, None]
+        w_grp = [None, None]
+        w_tg = [None, None]
+        w_codes = [None, None]
+        w_scales = [None, None]
+
+        def w_regroup(sg):
+            wrw = w_raw[sg][:].bitcast(F32).rearrange("p (j a c s f) -> p j f c a s", j=4, a=8, c=4, s=4, f=4)
+            wg = prep.tile([P, 2048], F32, name="wg%d" % sg, tag="grp", bufs=2, align_bytes=64)
+            for j in range(4):
+                nc.vector.tensor_copy(
+                    out=wg[:, 512 * j : 512 * j + 512].rearrange("p (f c a s) -> p f c a s", f=4, c=4, a=8, s=4),
+                    in_=wrw[:, j],
+                )
+            w_grp[sg] = wg
+
+        def w_transpose(sg):
+            wg = w_grp[sg]
+            wtg = prep.tile([P, 4096], BF16, name="wtg%d" % sg, tag="grp", bufs=2, align_bytes=64)
+            wtw = wtg[:].bitcast(F32)
+            for j in range(4):
+                pt = bank("ptw%d%d" % (sg, j), F32)
+                for f in range(4):
+                    nc.tensor.transpose(pt[:, P * f : P * f + P], wg[:, 512 * j + P * f : 512 * j + P * f + P], ident_f[:])
+                mover = nc.scalar.copy if sg == 0 else nc.vector.tensor_copy
+                mover(
+                    out=wtw[:, 512 * j : 512 * j + 512].rearrange("p (h i e) -> p h i e", h=2, e=2),
+                    in_=pt[:].rearrange("p (h e i) -> p h i e", h=2, e=2),
+                )
+            w_tg[sg] = wtg
+
+        def w_quant(sg, lo, hi):
+            if lo == 0:
+                w_codes[sg] = keep.tile([P, 1024], U32, name="wc%d" % sg, align_bytes=64)
+                w_scales[sg] = keep.tile([P, 1024], U8, name="ws%d" % sg, align_bytes=64)
+            nc.vector.quantize_mx(
+                out=w_codes[sg][:, 256 * lo : 256 * hi].bitcast(FP8X4),
+                scales=w_scales[sg][:, 256 * lo : 256 * hi],
+                in_=w_tg[sg][:, 1024 * lo : 1024 * hi],
+            )
+
+        scr = prep.tile([P, 512], BF16, name="scr")
+        bwr = prep.tile([P, 512], BF16, name="bwr")
+        sct = prep.tile([P, 512], BF16, name="sct")
+        bwt = [prep.tile([P, 512], BF16, name="bwt%d" % v, align_bytes=64) for v in range(2)]
+        swc = [keep.tile([P, 9 * P], U32, name="swc%d" % v, align_bytes=64) for v in range(2)]
+        sws = [keep.tile([P, 9 * P], U8, name="sws%d" % v, align_bytes=64) for v in range(2)]
+        sw_state = {}
+
+        def load_small():
+            for sg in range(2):
+                rows = slice(64 * sg, 64 * sg + 64)
+                cols = slice(512 * sg, 512 * sg + 512)
+                nc.sync.dma_start(out=scr[rows, :], in_=spline_scaler[:, cols])
+                nc.sync.dma_start(out=bwr[rows, :], in_=base_w[:, cols])
+
+        def sw_small():
+            psc = bank("psc", BF16)
+            pbw = bank("pbw", BF16)
+            for j in range(4):
+                nc.tensor.transpose(psc[:, P * j : P * j + P], scr[:, P * j : P * j + P], ident_b[:])
+            for j in range(4):
+                nc.tensor.transpose(pbw[:, P * j : P * j + P], bwr[:, P * j : P * j + P], ident_b[:])
+            nc.vector.tensor_copy(out=sct[:], in_=psc[:])
+            nc.vector.tensor_copy(out=bwt[0][:].rearrange("p (q j) -> p q j", j=4), in_=pbw[:].rearrange("p (j q) -> p q j", j=4))
+            for hq in range(2):
+                nc.vector.tensor_copy(
+                    out=bwt[1][:].rearrange("p (h q j) -> p h q j", h=2, j=4)[:, 1 - hq],
+                    in_=pbw[:].rearrange("p (j h q) -> p h q j", j=4, h=2)[:, hq],
+                )
+
+        def sw_regroup(swr):
             swg = prep.tile([P, 2048], F32, name="swg", tag="grp", bufs=2, align_bytes=64)
             nc.vector.tensor_copy(
                 out=swg[:].rearrange("p (k i) -> p k i", k=4),
                 in_=swr[:].bitcast(F32).rearrange("p (i k) -> p k i", k=4),
             )
-            swt = prep.tile([P, 9 * 512], BF16, name="swt", align_bytes=64)
-            psc = psum.tile([P, 512], BF16, name="psc", tag="s1", bufs=5)
-            pbw = psum.tile([P, 512], BF16, name="pbw", tag="s1", bufs=5)
-            for j in range(4):
-                nc.tensor.transpose(psc[:, P * j : P * j + P], scr[:, P * j : P * j + P], ident_b[:])
-            for j in range(4):
-                nc.tensor.transpose(pbw[:, P * j : P * j + P], bwr[:, P * j : P * j + P], ident_b[:])
-            sct = prep.tile([P, 512], BF16, name="sct")
-            nc.scalar.copy(out=sct[:], in_=psc[:])
-            nc.scalar.copy(
-                out=swt[:, 8 * 512 : 9 * 512].rearrange("p (q j) -> p q j", j=4),
-                in_=pbw[:].rearrange("p (j q) -> p q j", j=4),
-            )
-            swp = prep.tile([P, 4096], BF16, name="swp", tag="grp", bufs=2, align_bytes=64)
-            for kk in range(4):
-                pt = psum.tile([P, 512], F32, name="pts%d" % kk, tag="s1", bufs=5)
-                for j in range(4):
-                    nc.tensor.transpose(pt[:, P * j : P * j + P], swg[:, 512 * kk + P * j : 512 * kk + P * j + P], ident_f[:])
-                pairs = pt[:].bitcast(BF16).rearrange("p (w e) -> p e w", e=2)
-                for e in range(2):
-                    k = 2 * kk + e
-                    plane = 4 * (k % 2) + KFAM[k % 2].index(k)
-                    nc.vector.tensor_tensor(out=swp[:, 512 * plane : 512 * plane + 512], in0=pairs[:, e], in1=sct[:], op=ALU.mult)
-            for fam in range(2):
-                nc.vector.tensor_copy(
-                    out=swt[:, 0:4096].rearrange("p (t f q j) -> p f t q j", t=4, f=2, j=4)[:, fam],
-                    in_=swp[:].rearrange("p (f j t q) -> p f t q j", f=2, j=4, t=4)[:, fam],
-                )
-            nc.vector.quantize_mx(out=swc[:, 0:1024].bitcast(FP8X4), scales=sws[:, 0:1024], in_=swt[:, 0:4096])
-            nc.vector.quantize_mx(out=swc[:, 1024:1152].bitcast(FP8X4), scales=sws[:, 1024:1152], in_=swt[:, 4096:4608])
+            sw_state["swg"] = swg
 
-        def prep_x(sg, b, h):
-            xg = work.tile([P, 2048], BF16, name="xg", align_bytes=64)
+        def sw_transpose(kk):
+            swg = sw_state["swg"]
+            pt = bank("pts%d" % kk, F32)
+            for j in range(4):
+                nc.tensor.transpose(pt[:, P * j : P * j + P], swg[:, 512 * kk + P * j : 512 * kk + P * j + P], ident_f[:])
+            sw_state[kk] = pt
+
+        def sw_products(kk):
+            if kk == 0:
+                sw_state["swp"] = prep.tile([P, 4096], BF16, name="swp", tag="grp", bufs=2, align_bytes=64)
+            swp = sw_state["swp"]
+            pairs = sw_state[kk][:].bitcast(BF16).rearrange("p (w e) -> p e w", e=2)
+            for e in range(2):
+                k = 2 * kk + e
+                plane = 4 * (k % 2) + KFAM[k % 2].index(k)
+                nc.vector.tensor_tensor(out=swp[:, 512 * plane : 512 * plane + 512], in0=pairs[:, e], in1=sct[:], op=ALU.mult)
+
+        def sw_finish(v):
+            swp = sw_state["swp"]
+            swt = prep.tile([P, 4096], BF16, name="swt%d" % v, tag="swt", bufs=1, align_bytes=64)
+            for fam in range(2):
+                if v == 0:
+                    nc.vector.tensor_copy(
+                        out=swt[:].rearrange("p (t f q j) -> p f t q j", t=4, f=2, j=4)[:, fam],
+                        in_=swp[:].rearrange("p (f j t q) -> p f t q j", f=2, j=4, t=4)[:, fam],
+                    )
+                else:
+                    for hq in range(2):
+                        nc.vector.tensor_copy(
+                            out=swt[:].rearrange("p (t f h q j) -> p f h t q j", t=4, f=2, h=2, j=4)[:, fam, 1 - hq],
+                            in_=swp[:].rearrange("p (f j t h q) -> p f h t q j", f=2, j=4, t=4, h=2)[:, fam, hq],
+                        )
+            nc.vector.quantize_mx(out=swc[v][:, 0:1024].bitcast(FP8X4), scales=sws[v][:, 0:1024], in_=swt[:])
+            nc.vector.quantize_mx(out=swc[v][:, 1024:1152].bitcast(FP8X4), scales=sws[v][:, 1024:1152], in_=bwt[v][:])
+
+        x_raw = {}
+        st = [{} for c in range(NCH)]
+        acc = {}
+
+        def where(c):
+            return c // 4, (c // 2) % 2, c % 2
+
+        def x_prep(c):
+            b, h, sg = where(c)
+            xg = work.tile([P, 2048], BF16, name="xg", bufs=1, align_bytes=64)
             nc.vector.tensor_copy(
                 out=xg[:].bitcast(F32).rearrange("p (h n w) -> p h n w", h=2, w=2),
                 in_=x_raw[(sg, b)][:].bitcast(F32).rearrange("p (n h w) -> p h n w", h=2, w=2)[:, :, MC * h : MC * h + MC, :],
             )
-            xc = work.tile([P, 512], U32, name="xc", align_bytes=64)
-            xs = work.tile([P, 512], U8, name="xs", align_bytes=64)
+            xc = work.tile([P, 512], U32, name="xc", bufs=3, align_bytes=64)
+            xs = work.tile([P, 512], U8, name="xs", bufs=3, align_bytes=64)
             nc.vector.quantize_mx(out=xc[:].bitcast(FP8X4), scales=xs[:], in_=xg[:])
-            return xc, xs
+            st[c]["xc"] = xc
+            st[c]["xs"] = xs
 
-        def stage1(sg, xc, xs):
-            xt = work.tile([P, CW], F32, name="xt")
+        def m1(c):
+            sg = c % 2
+            xc, xs = st[c]["xc"], st[c]["xs"]
+            st[c]["ps"] = []
             for jj in range(2):
-                ps = psum.tile([P, 512], F32, name="ps1", tag="s1", bufs=5)
+                ps = bank("ps1", F32)
                 for j2 in range(2):
                     j = 2 * jj + j2
                     for half in range(2):
@@ -196,126 +241,249 @@ def tile_refiner_pa_kernel(tc, X, Y, Wx, bx, Wy, by, base_w, spline_w, spline_sc
                             start=(half == 0),
                             stop=(half == 1),
                         )
-                for j2 in range(2):
-                    j = 2 * jj + j2
-                    nc.scalar.activation(
-                        out=xt[:, MC * j : MC * j + MC],
-                        in_=ps[:, MC * j2 : MC * j2 + MC],
-                        func=ACTF.Tanh,
-                        bias=bias[:, 4 * sg + j : 4 * sg + j + 1],
-                        scale=1.0,
-                    )
-            return xt
+                st[c]["ps"].append(ps)
 
-        def act(nm, src, func, scale, bi, tag, bufs):
+        def tanh(c):
+            sg = c % 2
+            x = work.tile([P, CW], F32, name="x", bufs=4)
+            for j in range(4):
+                nc.scalar.activation(
+                    out=x[:, MC * j : MC * j + MC],
+                    in_=st[c]["ps"][j // 2][:, MC * (j % 2) : MC * (j % 2) + MC],
+                    func=ACTF.Tanh,
+                    bias=bias[:, 4 * sg + j : 4 * sg + j + 1],
+                    scale=1.0,
+                )
+            st[c]["x"] = x
+
+        def act(c, nm, src, func, scale, bi, tag, bufs):
             t = work.tile([P, CW], F32, name=nm, tag=tag, bufs=bufs)
             if bi is None:
-                nc.scalar.activation(out=t[:], in_=src[:], func=func, scale=scale)
+                nc.scalar.activation(out=t[:], in_=st[c][src][:], func=func, scale=scale)
             else:
-                nc.scalar.activation(out=t[:], in_=src[:], func=func, bias=cbias(bi), scale=scale)
-            return t
+                nc.scalar.activation(out=t[:], in_=st[c][src][:], func=func, bias=cbias(bi), scale=scale)
+            st[c][nm] = t
 
-        def product(dst, in0, scalar, in1):
-            nc.vector.scalar_tensor_tensor(out=dst, in0=in0[:], scalar=scalar, in1=in1[:], op0=ALU.add, op1=ALU.mult)
+        def product(c, dst, in0, scalar, in1):
+            nc.vector.scalar_tensor_tensor(
+                out=dst, in0=st[c][in0][:], scalar=scalar, in1=st[c][in1][:], op0=ALU.add, op1=ALU.mult
+            )
 
-        def interleave(dst, planes, width, scale):
-            o = dst.rearrange("p (c i j) -> p c j i", i=4, j=4)
-            s = planes.rearrange("p j (c i) -> p c j i", i=4)
-            cut = (width - ACT_W) // 4 if scale == 1.0 else width // 4
-            if scale == 1.0:
-                nc.vector.tensor_scalar(out=o[:, 0:cut], in0=s[:, 0:cut], scalar1=0.0, scalar2=None, op0=ALU.max)
-                nc.scalar.activation(out=o[:, cut : width // 4], in_=s[:, cut : width // 4], func=ACTF.Relu)
+        def a_even(c):
+            act(c, "f1", "x", ACTF.Abs, 2.5, B_M05, "f1", 2)
+            act(c, "g2", "f1", ACTF.Abs, 1.0, B_M2, "fold", 2)
+            act(c, "s4", "g2", ACTF.Square, r6, None, "sq", 4)
+            act(c, "s6", "f1", ACTF.Square, rc, None, "sq", 4)
+            act(c, "vb", "g2", ACTF.Abs, 1.0, B_M1, "fold", 2)
+
+        def a_odd(c):
+            act(c, "a3", "x", ACTF.Abs, 2.5, B_P05, "a3", 2)
+            act(c, "s3", "a3", ACTF.Square, r6, B_M2R6, "sq", 4)
+            act(c, "s5", "a3", ACTF.Square, rc, None, "sq", 4)
+
+        def a_cap(c, f):
+            if f == 0:
+                act(c, "q0", "vb", ACTF.Square, -1.0, B_1HB, "sq", 4)
+                act(c, "l0", "vb", ACTF.Identity, -0.5, B_L2, "lin", 2)
             else:
-                nc.vector.tensor_scalar(out=o, in0=s, scalar1=scale, scalar2=None, op0=ALU.mult)
+                act(c, "q1", "vb", ACTF.Square, 1.0, B_HB, "sq", 4)
+                act(c, "l1", "vb", ACTF.Identity, 0.5, B_L1, "lin", 2)
 
-        def bases(x):
-            codes = work.tile([P, 9 * MC], U32, name="codes", align_bytes=64)
-            scl = work.tile([P, 9 * MC], U8, name="scl", align_bytes=64)
-            pl = [work.tile([P, 4, CW], BF16, name="pl%d" % f, tag="pl", bufs=3, align_bytes=64) for f in range(2)]
+        def q_family(c, f):
+            pl = work.tile([P, 4, CW], BF16, name="pl%d" % f, tag="pl", bufs=3, align_bytes=64)
+            st[c]["pl%d" % f] = pl
+            if f == 0:
+                product(c, pl[:, 0, :], "f1", -2.0, "s4")
+                product(c, pl[:, 1, :], "x", -0.2, "s6")
+            else:
+                product(c, pl[:, 0, :], "a3", -2.0, "s3")
+                product(c, pl[:, 1, :], "x", 0.2, "s5")
 
-            f1 = act("f1", x, ACTF.Abs, 2.5, B_M05, "f1", 2)
-            g2 = act("g2", f1, ACTF.Abs, 1.0, B_M2, "fold", 2)
-            s4 = act("s4", g2, ACTF.Square, r6, None, "sq", 3)
-            product(pl[0][:, 0, :], f1, -2.0, s4)
-            s6 = act("s6", f1, ACTF.Square, rc, None, "sq", 3)
-            product(pl[0][:, 1, :], x, -0.2, s6)
-            a3 = act("a3", x, ACTF.Abs, 2.5, B_P05, "a3", 2)
-            s3 = act("s3", a3, ACTF.Square, r6, B_M2R6, "sq", 3)
-            product(pl[1][:, 0, :], a3, -2.0, s3)
-            s5 = act("s5", a3, ACTF.Square, rc, None, "sq", 3)
-            product(pl[1][:, 1, :], x, 0.2, s5)
-            vb = act("vb", g2, ACTF.Abs, 1.0, B_M1, "fold", 2)
-            caps = []
-            for f, (sc_q, b_q, sc_l, b_l) in enumerate(((-1.0, B_1HB, -0.5, B_L2), (1.0, B_HB, 0.5, B_L1))):
-                q = act("q%d" % f, vb, ACTF.Square, sc_q, b_q, "sq", 3)
-                lin = act("l%d" % f, vb, ACTF.Identity, sc_l, b_l, "lin", 2)
-                cap = work.tile([P, CW], BF16, name="cap%d" % f, align_bytes=64)
-                product(cap[:], q, cp, lin)
-                caps.append(cap)
-            th = act("th", x, ACTF.Tanh, 0.5, None, "sq", 3)
-            s2 = work.tile([P, CW], BF16, name="s2", align_bytes=64)
-            product(s2[:], th, 1.0, x)
+        def q_cap(c, f):
+            cap = work.tile([P, CW], BF16, name="cap%d" % f, align_bytes=64)
+            st[c]["cap%d" % f] = cap
+            product(c, cap[:], "q%d" % f, cp, "l%d" % f)
 
-            for f in range(2):
-                nc.vector.tensor_scalar(out=pl[f][:, 2:4, :], in0=pl[f][:, 0:2, :], scalar1=-1.0, scalar2=None, op0=ALU.mult)
-                nc.vector.tensor_tensor(
-                    out=pl[f][:, 1:4, :],
-                    in0=pl[f][:, 1:4, :],
-                    in1=caps[f][:].unsqueeze(1).to_broadcast([P, 3, CW]),
-                    op=ALU.min,
-                )
-                fam = work.tile([P, 4 * CW], BF16, name="fam", align_bytes=64)
-                interleave(fam[:], pl[f][:], CW, 1.0)
-                cols = slice(CW * f, CW * f + CW)
-                nc.vector.quantize_mx(out=codes[:, cols].bitcast(FP8X4), scales=scl[:, cols], in_=fam[:])
+        def views(dst, planes):
+            return dst.rearrange("p (c i j) -> p c j i", i=4, j=4), planes.rearrange("p j (c i) -> p c j i", i=4)
+
+        CUT = (CW - ACT_W) // 4
+
+        def lattice(c, f):
+            pl = st[c]["pl%d" % f]
+            nc.vector.tensor_scalar(out=pl[:, 2:4, :], in0=pl[:, 0:2, :], scalar1=-1.0, scalar2=None, op0=ALU.mult)
+            nc.vector.tensor_tensor(
+                out=pl[:, 1:4, :],
+                in0=pl[:, 1:4, :],
+                in1=st[c]["cap%d" % f][:].unsqueeze(1).to_broadcast([P, 3, CW]),
+                op=ALU.min,
+            )
+            fam = work.tile([P, 4 * CW], BF16, name="fam", align_bytes=64)
+            st[c]["fam%d" % f] = fam
+            o, s = views(fam[:], pl[:])
+            nc.vector.tensor_scalar(out=o[:, 0:CUT], in0=s[:, 0:CUT], scalar1=0.0, scalar2=None, op0=ALU.max)
+
+        def relu_share(c, f):
+            o, s = views(st[c]["fam%d" % f][:], st[c]["pl%d" % f][:])
+            nc.scalar.activation(out=o[:, CUT : CW // 4], in_=s[:, CUT : CW // 4], func=ACTF.Relu)
+
+        def quant_family(c, f):
+            if f == 0:
+                st[c]["codes"] = work.tile([P, 2 * CW], U32, name="codes", align_bytes=64)
+                st[c]["scl"] = work.tile([P, 2 * CW], U8, name="scl", align_bytes=64)
+            cols = slice(CW * f, CW * f + CW)
+            nc.vector.quantize_mx(
+                out=st[c]["codes"][:, cols].bitcast(FP8X4), scales=st[c]["scl"][:, cols], in_=st[c]["fam%d" % f][:]
+            )
+
+        def silu(c):
             sil = work.tile([P, CW], BF16, name="sil", align_bytes=64)
-            interleave(sil[:], s2[:].rearrange("p (j m) -> p j m", j=4), MC, 0.5)
-            cols = slice(2 * CW, 2 * CW + MC)
-            nc.vector.quantize_mx(out=codes[:, cols].bitcast(FP8X4), scales=scl[:, cols], in_=sil[:])
-            return codes, scl
+            o, s = views(sil[:], st[c]["x"][:].rearrange("p (j m) -> p j m", j=4))
+            nc.scalar.activation(out=o, in_=s, func=ACTF.Silu)
+            st[c]["sil"] = sil
 
-        def stage2(codes, scl):
-            acc = psum.tile([P, 512], F32, name="acc", tag="acc", bufs=3)
-            for mt in range(2):
-                for step in range(9):
-                    f, j = step // 4, step % 4
-                    m0 = 2 * CW + P * mt if step == 8 else CW * f + MC * j + P * mt
-                    q0 = 8 * P if step == 8 else P * (2 * j + f)
-                    nc.tensor.matmul_mx(
-                        out=acc[:, P * mt : P * mt + P],
-                        lhsT=codes[:, m0 : m0 + P].bitcast(FP8X4),
-                        lhsT_scale=scl[:, m0 : m0 + P],
-                        rhs=swc[:, q0 : q0 + P].bitcast(FP8X4),
-                        rhs_scale=sws[:, q0 : q0 + P],
-                        start=(step == 0),
-                        stop=(step == 8),
-                    )
-            return acc[:, 0:256].rearrange("p (t q) -> p t q", t=2)
+        def quant_silu(c):
+            bc = work.tile([P, MC], U32, name="bc", bufs=4, align_bytes=64)
+            bs = work.tile([P, MC], U8, name="bs", bufs=4, align_bytes=64)
+            nc.vector.quantize_mx(out=bc[:].bitcast(FP8X4), scales=bs[:], in_=st[c]["sil"][:])
+            st[c]["bc"] = bc
+            st[c]["bs"] = bs
 
-        prep_w(0)
-        x_raw[(1, 0)] = load_x(Y, 0, "y0r")
-        first = prep_x(0, 0, 0)
-        prep_w(1)
-        sw_raw = load_sw()
-        prep_sw(sw_raw)
-        x_raw[(0, 1)] = load_x(X, 1, "x1r")
-        for b in range(2):
-            for h in range(2):
-                part = None
-                for sg in range(2):
-                    xc, xs = first if (b, h, sg) == (0, 0, 0) else prep_x(sg, b, h)
-                    if (b, h, sg) == (0, 1, 0):
-                        x_raw[(1, 1)] = load_x(Y, 1, "y1r")
-                    x = stage1(sg, xc, xs)
-                    codes, scl = bases(x)
-                    res = stage2(codes, scl)
-                    if sg == 0:
-                        part = work.tile([P, 2, 64], F32, name="part")
-                        nc.scalar.copy(out=part[:], in_=res[:, :, 0:64])
-                    else:
-                        total = work.tile([P, 2, 64], F32, name="total")
-                        nc.vector.tensor_tensor(out=total[:], in0=res[:, :, 64:128], in1=part[:], op=ALU.add)
-                        nc.sync.dma_start(
-                            out=out[b, MC * h : MC * h + MC, :].rearrange("(t p) o -> p t o", p=P),
-                            in_=total[:],
+        def mx2(c, mt, lhs, lhs_s, m0, q0, start, stop):
+            v = c % 2
+            nc.tensor.matmul_mx(
+                out=acc[(c // 2, mt)][:, 0:P],
+                lhsT=lhs[:, m0 : m0 + P].bitcast(FP8X4),
+                lhsT_scale=lhs_s[:, m0 : m0 + P],
+                rhs=swc[v][:, q0 : q0 + P].bitcast(FP8X4),
+                rhs_scale=sws[v][:, q0 : q0 + P],
+                start=start,
+                stop=stop,
+            )
+
+        def m2_spline(c, last):
+            if c % 2 == 0:
+                for mt in range(2):
+                    acc[(c // 2, mt)] = psum.tile([P, 512], F32, name="acc", tag="acc", bufs=4)
+            for f in range(2):
+                for mt in range(2):
+                    for j in range(4):
+                        mx2(
+                            c, mt, st[c]["codes"], st[c]["scl"], CW * f + MC * j + P * mt, P * (2 * j + f),
+                            c % 2 == 0 and f == 0 and j == 0, last and f == 1 and j == 3,
                         )
+
+        def m2_base(c, last):
+            for mt in range(2):
+                mx2(c, mt, st[c]["bc"], st[c]["bs"], P * mt, 8 * P, False, last)
+
+        def store(g):
+            b, h = g // 2, g % 2
+            for mt in range(2):
+                ob = work.tile([P, 64], F32, name="ob", bufs=4)
+                nc.scalar.copy(out=ob[:], in_=acc[(g, mt)][:, 0:64])
+                r0 = MC * h + P * mt
+                nc.sync.dma_start(out=out[b, r0 : r0 + P, :], in_=ob[:])
+
+        nc.sync.dma_start(out=brow[0:4, :], in_=bx.rearrange("(r c) -> r c", c=P))
+        nc.sync.dma_start(out=brow[4:8, :], in_=by.rearrange("(r c) -> r c", c=P))
+        w_raw[0] = load_w(Wx, "wxr")
+        x_raw[(0, 0)] = raw_tile("x0r")
+        load_x(X, 0, x_raw[(0, 0)], 0, 2048)
+        w_raw[1] = load_w(Wy, "wyr")
+        load_small()
+        load_x(X, 0, x_raw[(0, 0)], 2048, 4096)
+
+        pb0 = bank("pb0", BF16)
+        nc.tensor.transpose(pb0[:, 0:P], brow[:], ident_b[:])
+        bias = keep.tile([P, 8], F32, name="bias")
+        nc.vector.tensor_copy(out=bias[:], in_=pb0[:, 0:8])
+
+        w_regroup(0)
+        x_raw[(1, 0)] = raw_tile("y0r")
+        load_x(Y, 0, x_raw[(1, 0)], 0, 4096)
+        w_transpose(0)
+        w_quant(0, 0, 2)
+        x_prep(0)
+        w_quant(0, 2, 4)
+        m1(0)
+        tanh(0)
+        a_odd(0)
+        w_regroup(1)
+        sw_raw = load_sw()
+        w_transpose(1)
+        w_quant(1, 0, 4)
+        q_family(0, 1)
+        a_even(0)
+        q_family(0, 0)
+        sw_small()
+        a_cap(0, 0)
+        a_cap(0, 1)
+        x_prep(1)
+        m1(1)
+        q_cap(0, 0)
+        x_prep(2)
+        m1(2)
+        q_cap(0, 1)
+        tanh(1)
+        tanh(2)
+        x_prep(3)
+        m1(3)
+        tanh(3)
+        for k in range(4):
+            silu(k)
+        sw_regroup(sw_raw)
+        x_raw[(0, 1)] = raw_tile("x1r")
+        load_x(X, 1, x_raw[(0, 1)], 0, 4096)
+        for kk in range(4):
+            sw_transpose(kk)
+            sw_products(kk)
+        sw_finish(0)
+        sw_finish(1)
+        x_raw[(1, 1)] = raw_tile("y1r")
+        load_x(Y, 1, x_raw[(1, 1)], 0, 4096)
+        for k in range(4):
+            quant_silu(k)
+
+        for c in range(1, NCH + 1):
+            live = c < NCH
+            if live and c >= 4:
+                tanh(c)
+            if live:
+                a_even(c)
+                a_cap(c, 0)
+            lattice(c - 1, 0)
+            relu_share(c - 1, 0)
+            if live:
+                q_family(c, 0)
+                q_cap(c, 0)
+                a_odd(c)
+                a_cap(c, 1)
+            lattice(c - 1, 1)
+            relu_share(c - 1, 1)
+            if c == NCH:
+                for k in range(4, NCH):
+                    quant_silu(k)
+                m2_base(4, False)
+                m2_base(5, True)
+                store(2)
+                m2_base(6, False)
+                m2_base(7, False)
+            quant_family(c - 1, 0)
+            if live:
+                q_family(c, 1)
+                q_cap(c, 1)
+            quant_family(c - 1, 1)
+            m2_spline(c - 1, c == NCH)
+            if c - 1 in (1, 3):
+                m2_base(c - 2, False)
+                m2_base(c - 1, True)
+            if c - 1 in (2, 4):
+                store((c - 2) // 2)
+            if c + 3 < NCH:
+                x_prep(c + 3)
+                m1(c + 3)
+            if c == NCH - 1:
+                for k in range(4, NCH):
+                    silu(k)
+        store(3)

@@ -18,7 +18,8 @@ MC = 256
 CW = 4 * MC
 NCH = 8
 KFAM = ((0, 6, 4, 2), (7, 5, 3, 1))
-ACT_W = 320
+ACT_W_LAST = 640
+ACT_W = 256
 
 
 def central_constants():
@@ -103,11 +104,12 @@ def tile_refiner_pa_kernel(tc, X, Y, Wx, bx, Wy, by, base_w, spline_w, spline_sc
                 )
             w_grp[sg] = wg
 
-        def w_transpose(sg):
+        def w_transpose(sg, lo, hi):
             wg = w_grp[sg]
-            wtg = prep.tile([P, 4096], BF16, name="wtg%d" % sg, tag="grp", bufs=2, align_bytes=64)
-            wtw = wtg[:].bitcast(F32)
-            for j in range(4):
+            if lo == 0:
+                w_tg[sg] = prep.tile([P, 4096], BF16, name="wtg%d" % sg, tag="grp", bufs=2, align_bytes=64)
+            wtw = w_tg[sg][:].bitcast(F32)
+            for j in range(lo, hi):
                 pt = bank("ptw%d%d" % (sg, j), F32)
                 for f in range(4):
                     nc.tensor.transpose(pt[:, P * f : P * f + P], wg[:, 512 * j + P * f : 512 * j + P * f + P], ident_f[:])
@@ -116,7 +118,6 @@ def tile_refiner_pa_kernel(tc, X, Y, Wx, bx, Wy, by, base_w, spline_w, spline_sc
                     out=wtw[:, 512 * j : 512 * j + 512].rearrange("p (h i e) -> p h i e", h=2, e=2),
                     in_=pt[:].rearrange("p (h e i) -> p h i e", h=2, e=2),
                 )
-            w_tg[sg] = wtg
 
         def w_quant(sg, lo, hi):
             if lo == 0:
@@ -159,7 +160,7 @@ def tile_refiner_pa_kernel(tc, X, Y, Wx, bx, Wy, by, base_w, spline_w, spline_sc
                 )
 
         def sw_regroup(swr):
-            swg = prep.tile([P, 2048], F32, name="swg", tag="grp", bufs=2, align_bytes=64)
+            swg = prep.tile([P, 2048], F32, name="swg", tag="swt", bufs=1, align_bytes=64)
             nc.vector.tensor_copy(
                 out=swg[:].rearrange("p (k i) -> p k i", k=4),
                 in_=swr[:].bitcast(F32).rearrange("p (i k) -> p k i", k=4),
@@ -175,7 +176,7 @@ def tile_refiner_pa_kernel(tc, X, Y, Wx, bx, Wy, by, base_w, spline_w, spline_sc
 
         def sw_products(kk):
             if kk == 0:
-                sw_state["swp"] = prep.tile([P, 4096], BF16, name="swp", tag="grp", bufs=2, align_bytes=64)
+                sw_state["swp"] = work.tile([P, 4096], BF16, name="swp", tag="pl", bufs=3, align_bytes=64)
             swp = sw_state["swp"]
             pairs = sw_state[kk][:].bitcast(BF16).rearrange("p (w e) -> p e w", e=2)
             for e in range(2):
@@ -208,13 +209,17 @@ def tile_refiner_pa_kernel(tc, X, Y, Wx, bx, Wy, by, base_w, spline_w, spline_sc
         def where(c):
             return c // 4, (c // 2) % 2, c % 2
 
-        def x_prep(c):
+        def x_copy(c):
             b, h, sg = where(c)
             xg = work.tile([P, 2048], BF16, name="xg", bufs=1, align_bytes=64)
+            st[c]["xg"] = xg
             nc.vector.tensor_copy(
                 out=xg[:].bitcast(F32).rearrange("p (h n w) -> p h n w", h=2, w=2),
                 in_=x_raw[(sg, b)][:].bitcast(F32).rearrange("p (n h w) -> p h n w", h=2, w=2)[:, :, MC * h : MC * h + MC, :],
             )
+
+        def x_quant(c):
+            xg = st[c]["xg"]
             xc = work.tile([P, 512], U32, name="xc", bufs=3, align_bytes=64)
             xs = work.tile([P, 512], U8, name="xs", bufs=3, align_bytes=64)
             nc.vector.quantize_mx(out=xc[:].bitcast(FP8X4), scales=xs[:], in_=xg[:])
@@ -269,63 +274,79 @@ def tile_refiner_pa_kernel(tc, X, Y, Wx, bx, Wy, by, base_w, spline_w, spline_sc
                 out=dst, in0=st[c][in0][:], scalar=scalar, in1=st[c][in1][:], op0=ALU.add, op1=ALU.mult
             )
 
-        def a_even(c):
-            act(c, "f1", "x", ACTF.Abs, 2.5, B_M05, "f1", 2)
-            act(c, "g2", "f1", ACTF.Abs, 1.0, B_M2, "fold", 2)
-            act(c, "s4", "g2", ACTF.Square, r6, None, "sq", 4)
-            act(c, "s6", "f1", ACTF.Square, rc, None, "sq", 4)
-            act(c, "vb", "g2", ACTF.Abs, 1.0, B_M1, "fold", 2)
+        A_OPS = {
+            "f1": ("x", ACTF.Abs, 2.5, B_M05, "f1", 2),
+            "a3": ("x", ACTF.Abs, 2.5, B_P05, "a3", 2),
+            "g2": ("f1", ACTF.Abs, 1.0, B_M2, "fold", 2),
+            "vb": ("g2", ACTF.Abs, 1.0, B_M1, "fold", 2),
+            "s4": ("g2", ACTF.Square, r6, None, "sq", 4),
+            "s6": ("f1", ACTF.Square, rc, None, "sq", 4),
+            "s3": ("a3", ACTF.Square, r6, B_M2R6, "sq", 4),
+            "s5": ("a3", ACTF.Square, rc, None, "sq", 4),
+            "q0": ("vb", ACTF.Square, -1.0, B_1HB, "sq", 4),
+            "l0": ("vb", ACTF.Identity, -0.5, B_L2, "lin", 2),
+            "q1": ("vb", ACTF.Square, 1.0, B_HB, "sq", 4),
+            "l1": ("vb", ACTF.Identity, 0.5, B_L1, "lin", 2),
+        }
 
-        def a_odd(c):
-            act(c, "a3", "x", ACTF.Abs, 2.5, B_P05, "a3", 2)
-            act(c, "s3", "a3", ACTF.Square, r6, B_M2R6, "sq", 4)
-            act(c, "s5", "a3", ACTF.Square, rc, None, "sq", 4)
+        def aops(c, names):
+            for nm in names:
+                src, func, scale, bi, tag, bufs = A_OPS[nm]
+                act(c, nm, src, func, scale, bi, tag, bufs)
 
-        def a_cap(c, f):
-            if f == 0:
-                act(c, "q0", "vb", ACTF.Square, -1.0, B_1HB, "sq", 4)
-                act(c, "l0", "vb", ACTF.Identity, -0.5, B_L2, "lin", 2)
+        V_OPS = {
+            "P4": (0, 0, "f1", -2.0, "s4"),
+            "L6": (0, 1, "x", -0.2, "s6"),
+            "P3": (1, 0, "a3", -2.0, "s3"),
+            "L5": (1, 1, "x", 0.2, "s5"),
+            "C0": (0, None, "q0", cp, "l0"),
+            "C1": (1, None, "q1", cp, "l1"),
+        }
+
+        def vop(c, nm):
+            f, plane, in0, scalar, in1 = V_OPS[nm]
+            if plane is None:
+                cap = work.tile([P, CW], BF16, name="cap%d" % f, align_bytes=64)
+                st[c]["cap%d" % f] = cap
+                product(c, cap[:], in0, scalar, in1)
             else:
-                act(c, "q1", "vb", ACTF.Square, 1.0, B_HB, "sq", 4)
-                act(c, "l1", "vb", ACTF.Identity, 0.5, B_L1, "lin", 2)
-
-        def q_family(c, f):
-            pl = work.tile([P, 4, CW], BF16, name="pl%d" % f, tag="pl", bufs=3, align_bytes=64)
-            st[c]["pl%d" % f] = pl
-            if f == 0:
-                product(c, pl[:, 0, :], "f1", -2.0, "s4")
-                product(c, pl[:, 1, :], "x", -0.2, "s6")
-            else:
-                product(c, pl[:, 0, :], "a3", -2.0, "s3")
-                product(c, pl[:, 1, :], "x", 0.2, "s5")
-
-        def q_cap(c, f):
-            cap = work.tile([P, CW], BF16, name="cap%d" % f, align_bytes=64)
-            st[c]["cap%d" % f] = cap
-            product(c, cap[:], "q%d" % f, cp, "l%d" % f)
+                key = "pl%d" % f
+                if key not in st[c]:
+                    st[c][key] = work.tile([P, 4, CW], BF16, name=key, tag="pl", bufs=3, align_bytes=64)
+                product(c, st[c][key][:, plane, :], in0, scalar, in1)
 
         def views(dst, planes):
             return dst.rearrange("p (c i j) -> p c j i", i=4, j=4), planes.rearrange("p j (c i) -> p c j i", i=4)
 
-        CUT = (CW - ACT_W) // 4
+        def cut(c):
+            return (CW - (ACT_W_LAST if c == NCH - 1 else ACT_W)) // 4
 
-        def lattice(c, f):
+        def neg(c, f):
             pl = st[c]["pl%d" % f]
             nc.vector.tensor_scalar(out=pl[:, 2:4, :], in0=pl[:, 0:2, :], scalar1=-1.0, scalar2=None, op0=ALU.mult)
+
+        def cap_min(c, f):
+            pl = st[c]["pl%d" % f]
             nc.vector.tensor_tensor(
                 out=pl[:, 1:4, :],
                 in0=pl[:, 1:4, :],
                 in1=st[c]["cap%d" % f][:].unsqueeze(1).to_broadcast([P, 3, CW]),
                 op=ALU.min,
             )
-            fam = work.tile([P, 4 * CW], BF16, name="fam", align_bytes=64)
-            st[c]["fam%d" % f] = fam
-            o, s = views(fam[:], pl[:])
-            nc.vector.tensor_scalar(out=o[:, 0:CUT], in0=s[:, 0:CUT], scalar1=0.0, scalar2=None, op0=ALU.max)
+
+        def fam_views(c, f):
+            key = "fam%d" % f
+            if key not in st[c]:
+                st[c][key] = work.tile([P, 4 * CW], BF16, name="fam", align_bytes=64)
+            return views(st[c][key][:], st[c]["pl%d" % f][:])
+
+        def weave(c, f):
+            o, s = fam_views(c, f)
+            nc.vector.tensor_scalar(out=o[:, 0 : cut(c)], in0=s[:, 0 : cut(c)], scalar1=0.0, scalar2=None, op0=ALU.max)
 
         def relu_share(c, f):
-            o, s = views(st[c]["fam%d" % f][:], st[c]["pl%d" % f][:])
-            nc.scalar.activation(out=o[:, CUT : CW // 4], in_=s[:, CUT : CW // 4], func=ACTF.Relu)
+            o, s = fam_views(c, f)
+            nc.scalar.activation(out=o[:, cut(c) : CW // 4], in_=s[:, cut(c) : CW // 4], func=ACTF.Relu)
 
         def quant_family(c, f):
             if f == 0:
@@ -337,7 +358,7 @@ def tile_refiner_pa_kernel(tc, X, Y, Wx, bx, Wy, by, base_w, spline_w, spline_sc
             )
 
         def silu(c):
-            sil = work.tile([P, CW], BF16, name="sil", align_bytes=64)
+            sil = work.tile([P, CW], BF16, name="sil", bufs=4, align_bytes=64)
             o, s = views(sil[:], st[c]["x"][:].rearrange("p (j m) -> p j m", j=4))
             nc.scalar.activation(out=o, in_=s, func=ACTF.Silu)
             st[c]["sil"] = sil
@@ -389,45 +410,47 @@ def tile_refiner_pa_kernel(tc, X, Y, Wx, bx, Wy, by, base_w, spline_w, spline_sc
         nc.sync.dma_start(out=brow[4:8, :], in_=by.rearrange("(r c) -> r c", c=P))
         w_raw[0] = load_w(Wx, "wxr")
         x_raw[(0, 0)] = raw_tile("x0r")
-        load_x(X, 0, x_raw[(0, 0)], 0, 2048)
+        load_x(X, 0, x_raw[(0, 0)], 0, 4096)
         w_raw[1] = load_w(Wy, "wyr")
         load_small()
-        load_x(X, 0, x_raw[(0, 0)], 2048, 4096)
-
-        pb0 = bank("pb0", BF16)
-        nc.tensor.transpose(pb0[:, 0:P], brow[:], ident_b[:])
-        bias = keep.tile([P, 8], F32, name="bias")
-        nc.vector.tensor_copy(out=bias[:], in_=pb0[:, 0:8])
 
         w_regroup(0)
         x_raw[(1, 0)] = raw_tile("y0r")
         load_x(Y, 0, x_raw[(1, 0)], 0, 4096)
-        w_transpose(0)
+        pb0 = bank("pb0", BF16)
+        nc.tensor.transpose(pb0[:, 0:P], brow[:], ident_b[:])
+        bias = keep.tile([P, 8], F32, name="bias")
+        nc.vector.tensor_copy(out=bias[:], in_=pb0[:, 0:8])
+        w_transpose(0, 0, 4)
         w_quant(0, 0, 2)
-        x_prep(0)
+        x_copy(0)
         w_quant(0, 2, 4)
+        x_quant(0)
         m1(0)
         tanh(0)
-        a_odd(0)
+        aops(0, ("a3", "f1", "s3", "g2", "s5", "s6", "vb", "s4", "q0", "l0", "q1", "l1"))
         w_regroup(1)
         sw_raw = load_sw()
-        w_transpose(1)
+        w_transpose(1, 0, 4)
         w_quant(1, 0, 4)
-        q_family(0, 1)
-        a_even(0)
-        q_family(0, 0)
+        vop(0, "P3")
         sw_small()
-        a_cap(0, 0)
-        a_cap(0, 1)
-        x_prep(1)
+        vop(0, "L5")
+        x_copy(2)
+        vop(0, "L6")
+        x_quant(2)
+        vop(0, "P4")
+        x_copy(1)
+        vop(0, "C0")
+        x_quant(1)
         m1(1)
-        q_cap(0, 0)
-        x_prep(2)
         m1(2)
-        q_cap(0, 1)
+        vop(0, "C1")
         tanh(1)
         tanh(2)
-        x_prep(3)
+        x_copy(3)
+        neg(0, 0)
+        x_quant(3)
         m1(3)
         tanh(3)
         for k in range(4):
@@ -435,9 +458,17 @@ def tile_refiner_pa_kernel(tc, X, Y, Wx, bx, Wy, by, base_w, spline_w, spline_sc
         sw_regroup(sw_raw)
         x_raw[(0, 1)] = raw_tile("x1r")
         load_x(X, 1, x_raw[(0, 1)], 0, 4096)
+        cap_min(0, 0)
+        neg(0, 1)
         for kk in range(4):
             sw_transpose(kk)
-            sw_products(kk)
+        weave(0, 0)
+        sw_products(0)
+        cap_min(0, 1)
+        sw_products(1)
+        weave(0, 1)
+        sw_products(2)
+        sw_products(3)
         sw_finish(0)
         sw_finish(1)
         x_raw[(1, 1)] = raw_tile("y1r")
@@ -446,21 +477,36 @@ def tile_refiner_pa_kernel(tc, X, Y, Wx, bx, Wy, by, base_w, spline_w, spline_sc
             quant_silu(k)
 
         for c in range(1, NCH + 1):
+            p = c - 1
             live = c < NCH
-            if live and c >= 4:
-                tanh(c)
+            nxt = c + 3 < NCH
             if live:
-                a_even(c)
-                a_cap(c, 0)
-            lattice(c - 1, 0)
-            relu_share(c - 1, 0)
+                if c >= 4:
+                    tanh(c)
+                aops(c, ("f1", "a3", "g2", "s6", "vb", "s4"))
+            if c > 1:
+                neg(p, 0)
             if live:
-                q_family(c, 0)
-                q_cap(c, 0)
-                a_odd(c)
-                a_cap(c, 1)
-            lattice(c - 1, 1)
-            relu_share(c - 1, 1)
+                vop(c, "L6")
+            if c > 1:
+                cap_min(p, 0)
+            relu_share(p, 0)
+            if live:
+                aops(c, ("s5", "q0", "s3", "l0"))
+                vop(c, "P4")
+            if c > 1:
+                weave(p, 0)
+                neg(p, 1)
+            if nxt:
+                x_copy(c + 3)
+            if c > 1:
+                cap_min(p, 1)
+            relu_share(p, 1)
+            if live:
+                aops(c, ("q1", "l1"))
+                vop(c, "L5")
+            if c > 1:
+                weave(p, 1)
             if c == NCH:
                 for k in range(4, NCH):
                     quant_silu(k)
@@ -469,20 +515,23 @@ def tile_refiner_pa_kernel(tc, X, Y, Wx, bx, Wy, by, base_w, spline_w, spline_sc
                 store(2)
                 m2_base(6, False)
                 m2_base(7, False)
-            quant_family(c - 1, 0)
+            quant_family(p, 0)
             if live:
-                q_family(c, 1)
-                q_cap(c, 1)
-            quant_family(c - 1, 1)
-            m2_spline(c - 1, c == NCH)
-            if c - 1 in (1, 3):
-                m2_base(c - 2, False)
-                m2_base(c - 1, True)
-            if c - 1 in (2, 4):
-                store((c - 2) // 2)
-            if c + 3 < NCH:
-                x_prep(c + 3)
+                vop(c, "P3")
+            if nxt:
+                x_quant(c + 3)
                 m1(c + 3)
+            if live:
+                vop(c, "C0")
+            quant_family(p, 1)
+            m2_spline(p, c == NCH)
+            if live:
+                vop(c, "C1")
+            if p in (1, 3):
+                m2_base(p - 1, False)
+                m2_base(p, True)
+            if p in (2, 4):
+                store((p - 1) // 2)
             if c == NCH - 1:
                 for k in range(4, NCH):
                     silu(k)

@@ -11,6 +11,7 @@ U8 = mybir.dt.uint8
 FP8X4 = mybir.dt.float8_e4m3fn_x4
 ACTF = mybir.ActivationFunctionType
 ALU = mybir.AluOpType
+AX = mybir.AxisListType
 
 P = 128
 FLOPS = 2 * 2 * 1024 * 1024 * 512 + 2 * 1024 * 64 * (1024 + 8192)
@@ -18,8 +19,6 @@ MC = 256
 CW = 4 * MC
 NCH = 8
 KFAM = ((0, 6, 4, 2), (7, 5, 3, 1))
-ACT_W_LAST = 640
-ACT_W = 256
 
 
 def central_constants():
@@ -35,7 +34,7 @@ def tile_refiner_pa_kernel(tc, X, Y, Wx, bx, Wy, by, base_w, spline_w, spline_sc
     a0, hb, cp = central_constants()
     r6 = 1.0 / math.sqrt(6.0)
     rc = math.sqrt(2.5 / 6.0)
-    bias_vals = (-0.5, 0.5, -2.0, -1.0, -2.0 * r6, hb, 1.0 + hb, -a0 / 2.0, (1.0 - a0) / 2.0)
+    bias_vals = (-0.5, 0.5, -2.0, -1.0, -2.0 * r6, hb, 1.0 + hb, a0 / 2.0, (a0 - 1.0) / 2.0)
     (B_M05, B_P05, B_M2, B_M1, B_M2R6, B_HB, B_1HB, B_L1, B_L2) = range(9)
 
     with ExitStack() as ctx:
@@ -46,7 +45,7 @@ def tile_refiner_pa_kernel(tc, X, Y, Wx, bx, Wy, by, base_w, spline_w, spline_sc
         ctx.enter_context(tc.manual_schedule())
 
         def bank(nm, dt):
-            return psum.tile([P, 512], dt, name=nm, tag="s1", bufs=4)
+            return psum.tile([P, 512], dt, name=nm, tag="s1", bufs=6)
 
         ident_f = keep.tile([P, P], F32, name="ident_f")
         make_identity(nc, ident_f[:])
@@ -58,29 +57,40 @@ def tile_refiner_pa_kernel(tc, X, Y, Wx, bx, Wy, by, base_w, spline_w, spline_sc
         nc.vector.memset(brow[:], 0.0)
         cb = keep.tile([P, 16], F32, name="cb")
         warm = keep.tile([P, 8], F32, name="warm")
-        nc.scalar.activation(out=warm[:, 0:1], in_=ones[:, 0:1], func=ACTF.Tanh)
+        nc.scalar.activation(out=warm[:, 0:1], in_=ones[:, 0:1], func=ACTF.Silu)
         for i, v in enumerate(bias_vals):
             nc.scalar.activation(out=cb[:, i : i + 1], in_=ones[:, 0:1], func=ACTF.Copy, scale=v)
 
         def cbias(i):
             return cb[:, i : i + 1]
 
+        low = keep.tile([P, 1], F32, name="low")
+        nc.vector.tensor_reduce(
+            out=low[:], in_=ident_f[:].rearrange("p (g e r) -> p e g r", e=2, r=4)[:, 0], axis=AX.XY, op=ALU.add
+        )
+        sgn = keep.tile([P, 2], F32, name="sgn")
+        nc.vector.tensor_scalar(out=sgn[:, 0:1], in0=low[:], scalar1=2.0, scalar2=-1.0, op0=ALU.mult, op1=ALU.add)
+        nc.vector.tensor_scalar(out=sgn[:, 1:2], in0=low[:], scalar1=-2.0, scalar2=1.0, op0=ALU.mult, op1=ALU.add)
+
+        def raw_tile(nm):
+            return prep.tile([P, 4096], BF16, name=nm, tag="raw", bufs=5)
+
         def load_w(w, nm):
-            wr = prep.tile([P, 4096], BF16, name=nm, tag="raw", bufs=3)
-            nc.sync.dma_start(out=wr[:].rearrange("p (j k) -> p j k", j=4), in_=w.rearrange("(j p) k -> p j k", p=P))
+            wr = raw_tile(nm)
+            for j in range(4):
+                nc.sync.dma_start(out=wr[:, 1024 * j : 1024 * j + 1024], in_=w[P * j : P * j + P, :])
             return wr
 
-        def load_x(x, b, xr, lo, hi):
+        def load_x(x, b, nm):
+            xr = raw_tile(nm)
             src = x[b].rearrange("(a c) n f -> c a (n f)", c=16)
             for cl in range(4):
                 for s in range(4):
-                    nc.sync.dma_start(out=xr[32 * cl + s : 32 * cl + 32 : 4, lo:hi], in_=src[4 * cl + s][:, lo:hi])
-
-        def raw_tile(nm):
-            return prep.tile([P, 4096], BF16, name=nm, tag="raw", bufs=3)
+                    nc.sync.dma_start(out=xr[32 * cl + s : 32 * cl + 32 : 4, :], in_=src[4 * cl + s])
+            return xr
 
         def load_sw():
-            swr = prep.tile([P, 4096], BF16, name="swr", tag="raw", bufs=3)
+            swr = raw_tile("swr")
             for sg in range(2):
                 nc.sync.dma_start(
                     out=swr[64 * sg : 64 * sg + 64, :],
@@ -91,33 +101,36 @@ def tile_refiner_pa_kernel(tc, X, Y, Wx, bx, Wy, by, base_w, spline_w, spline_sc
         w_raw = [None, None]
         w_grp = [None, None]
         w_tg = [None, None]
+        w_pt = {}
         w_codes = [None, None]
         w_scales = [None, None]
 
-        def w_regroup(sg):
-            wrw = w_raw[sg][:].bitcast(F32).rearrange("p (j a c s f) -> p j f c a s", j=4, a=8, c=4, s=4, f=4)
-            wg = prep.tile([P, 2048], F32, name="wg%d" % sg, tag="grp", bufs=2, align_bytes=64)
-            for j in range(4):
-                nc.vector.tensor_copy(
-                    out=wg[:, 512 * j : 512 * j + 512].rearrange("p (f c a s) -> p f c a s", f=4, c=4, a=8, s=4),
-                    in_=wrw[:, j],
-                )
-            w_grp[sg] = wg
+        def grp_tile(nm, cols, dt):
+            return prep.tile([P, cols], dt, name=nm, tag="grp", bufs=3, align_bytes=64)
 
-        def w_transpose(sg, lo, hi):
+        def w_regroup(sg, j, copier):
+            if w_grp[sg] is None:
+                w_grp[sg] = grp_tile("wg%d" % sg, 2048, F32)
+            wrw = w_raw[sg][:].bitcast(F32).rearrange("p (j a c s f) -> p j f c a s", j=4, a=8, c=4, s=4, f=4)
+            copier(
+                out=w_grp[sg][:, 512 * j : 512 * j + 512].rearrange("p (f c a s) -> p f c a s", f=4, c=4, a=8, s=4),
+                in_=wrw[:, j],
+            )
+
+        def w_transpose(sg, j):
             wg = w_grp[sg]
-            if lo == 0:
-                w_tg[sg] = prep.tile([P, 4096], BF16, name="wtg%d" % sg, tag="grp", bufs=2, align_bytes=64)
-            wtw = w_tg[sg][:].bitcast(F32)
-            for j in range(lo, hi):
-                pt = bank("ptw%d%d" % (sg, j), F32)
-                for f in range(4):
-                    nc.tensor.transpose(pt[:, P * f : P * f + P], wg[:, 512 * j + P * f : 512 * j + P * f + P], ident_f[:])
-                mover = nc.scalar.copy if sg == 0 else nc.vector.tensor_copy
-                mover(
-                    out=wtw[:, 512 * j : 512 * j + 512].rearrange("p (h i e) -> p h i e", h=2, e=2),
-                    in_=pt[:].rearrange("p (h e i) -> p h i e", h=2, e=2),
-                )
+            pt = bank("ptw%d%d" % (sg, j), F32)
+            for f in range(4):
+                nc.tensor.transpose(pt[:, P * f : P * f + P], wg[:, 512 * j + P * f : 512 * j + P * f + P], ident_f[:])
+            w_pt[(sg, j)] = pt
+
+        def w_evac(sg, j, copier):
+            if w_tg[sg] is None:
+                w_tg[sg] = grp_tile("wtg%d" % sg, 4096, BF16)
+            copier(
+                out=w_tg[sg][:].bitcast(F32)[:, 512 * j : 512 * j + 512].rearrange("p (h i e) -> p h i e", h=2, e=2),
+                in_=w_pt[(sg, j)][:].rearrange("p (h e i) -> p h i e", h=2, e=2),
+            )
 
         def w_quant(sg, lo, hi):
             if lo == 0:
@@ -132,9 +145,9 @@ def tile_refiner_pa_kernel(tc, X, Y, Wx, bx, Wy, by, base_w, spline_w, spline_sc
         scr = prep.tile([P, 512], BF16, name="scr")
         bwr = prep.tile([P, 512], BF16, name="bwr")
         sct = prep.tile([P, 512], BF16, name="sct")
-        bwt = [prep.tile([P, 512], BF16, name="bwt%d" % v, align_bytes=64) for v in range(2)]
-        swc = [keep.tile([P, 9 * P], U32, name="swc%d" % v, align_bytes=64) for v in range(2)]
-        sws = [keep.tile([P, 9 * P], U8, name="sws%d" % v, align_bytes=64) for v in range(2)]
+        bwt = prep.tile([P, 512], BF16, name="bwt", align_bytes=64)
+        swc = keep.tile([P, 9 * P], U32, name="swc", align_bytes=64)
+        sws = keep.tile([P, 9 * P], U8, name="sws", align_bytes=64)
         sw_state = {}
 
         def load_small():
@@ -145,26 +158,28 @@ def tile_refiner_pa_kernel(tc, X, Y, Wx, bx, Wy, by, base_w, spline_w, spline_sc
                 nc.sync.dma_start(out=bwr[rows, :], in_=base_w[:, cols])
 
         def sw_small():
-            psc = bank("psc", BF16)
-            pbw = bank("pbw", BF16)
+            sw_state["psc"] = psc = bank("psc", BF16)
+            sw_state["pbw"] = pbw = bank("pbw", BF16)
             for j in range(4):
                 nc.tensor.transpose(psc[:, P * j : P * j + P], scr[:, P * j : P * j + P], ident_b[:])
             for j in range(4):
                 nc.tensor.transpose(pbw[:, P * j : P * j + P], bwr[:, P * j : P * j + P], ident_b[:])
-            nc.vector.tensor_copy(out=sct[:], in_=psc[:])
-            nc.vector.tensor_copy(out=bwt[0][:].rearrange("p (q j) -> p q j", j=4), in_=pbw[:].rearrange("p (j q) -> p q j", j=4))
-            for hq in range(2):
-                nc.vector.tensor_copy(
-                    out=bwt[1][:].rearrange("p (h q j) -> p h q j", h=2, j=4)[:, 1 - hq],
-                    in_=pbw[:].rearrange("p (j h q) -> p h q j", j=4, h=2)[:, hq],
-                )
 
-        def sw_regroup(swr):
-            swg = prep.tile([P, 2048], F32, name="swg", tag="swt", bufs=1, align_bytes=64)
-            nc.vector.tensor_copy(
-                out=swg[:].rearrange("p (k i) -> p k i", k=4),
-                in_=swr[:].bitcast(F32).rearrange("p (i k) -> p k i", k=4),
+        def sw_small_evac():
+            psc, pbw = sw_state["psc"], sw_state["pbw"]
+            nc.vector.tensor_scalar(
+                out=sct[:].rearrange("p (q j) -> p q j", j=4), in0=psc[:].rearrange("p (j q) -> p q j", j=4),
+                scalar1=-1.0, scalar2=None, op0=ALU.mult,
             )
+            nc.vector.tensor_copy(out=bwt[:].rearrange("p (q j) -> p q j", j=4), in_=pbw[:].rearrange("p (j q) -> p q j", j=4))
+
+        def sw_regroup(swr, copier):
+            swg = grp_tile("swg", 2048, F32)
+            o = swg[:].rearrange("p (k g e r) -> p e k g r", k=4, e=2, r=4)
+            s = swr[:].bitcast(F32).rearrange("p (g e r k) -> p e k g r", e=2, r=4, k=4)
+            copier(out=o[:, 0], in_=s[:, 0])
+            copier(out=o[:, 1, 0:2], in_=s[:, 1, 2:4])
+            copier(out=o[:, 1, 2:4], in_=s[:, 1, 0:2])
             sw_state["swg"] = swg
 
         def sw_transpose(kk):
@@ -176,52 +191,43 @@ def tile_refiner_pa_kernel(tc, X, Y, Wx, bx, Wy, by, base_w, spline_w, spline_sc
 
         def sw_products(kk):
             if kk == 0:
-                sw_state["swp"] = work.tile([P, 4096], BF16, name="swp", tag="pl", bufs=3, align_bytes=64)
-            swp = sw_state["swp"]
-            pairs = sw_state[kk][:].bitcast(BF16).rearrange("p (w e) -> p e w", e=2)
+                sw_state["swt"] = grp_tile("swt", 4096, BF16)
+            pairs = sw_state[kk][:].bitcast(BF16).rearrange("p (j q e) -> p e q j", j=4, e=2)
             for e in range(2):
                 k = 2 * kk + e
                 plane = 4 * (k % 2) + KFAM[k % 2].index(k)
-                nc.vector.tensor_tensor(out=swp[:, 512 * plane : 512 * plane + 512], in0=pairs[:, e], in1=sct[:], op=ALU.mult)
+                nc.vector.tensor_tensor(
+                    out=sw_state["swt"][:, 512 * plane : 512 * plane + 512].rearrange("p (q j) -> p q j", j=4),
+                    in0=pairs[:, e], in1=sct[:].rearrange("p (q j) -> p q j", j=4), op=ALU.mult,
+                )
 
-        def sw_finish(v):
-            swp = sw_state["swp"]
-            swt = prep.tile([P, 4096], BF16, name="swt%d" % v, tag="swt", bufs=1, align_bytes=64)
-            for fam in range(2):
-                if v == 0:
-                    nc.vector.tensor_copy(
-                        out=swt[:].rearrange("p (t f q j) -> p f t q j", t=4, f=2, j=4)[:, fam],
-                        in_=swp[:].rearrange("p (f j t q) -> p f t q j", f=2, j=4, t=4)[:, fam],
-                    )
-                else:
-                    for hq in range(2):
-                        nc.vector.tensor_copy(
-                            out=swt[:].rearrange("p (t f h q j) -> p f h t q j", t=4, f=2, h=2, j=4)[:, fam, 1 - hq],
-                            in_=swp[:].rearrange("p (f j t h q) -> p f h t q j", f=2, j=4, t=4, h=2)[:, fam, hq],
-                        )
-            nc.vector.quantize_mx(out=swc[v][:, 0:1024].bitcast(FP8X4), scales=sws[v][:, 0:1024], in_=swt[:])
-            nc.vector.quantize_mx(out=swc[v][:, 1024:1152].bitcast(FP8X4), scales=sws[v][:, 1024:1152], in_=bwt[v][:])
+        def sw_quant():
+            nc.vector.quantize_mx(out=swc[:, 0:1024].bitcast(FP8X4), scales=sws[:, 0:1024], in_=sw_state["swt"][:])
+
+        def bw_quant():
+            nc.vector.quantize_mx(out=swc[:, 1024:1152].bitcast(FP8X4), scales=sws[:, 1024:1152], in_=bwt[:])
 
         x_raw = {}
         st = [{} for c in range(NCH)]
         acc = {}
+        obx = {}
 
         def where(c):
             return c // 4, (c // 2) % 2, c % 2
 
-        def x_copy(c):
+        def x_copy(c, copier):
             b, h, sg = where(c)
             xg = work.tile([P, 2048], BF16, name="xg", bufs=1, align_bytes=64)
             st[c]["xg"] = xg
-            nc.vector.tensor_copy(
+            copier(
                 out=xg[:].bitcast(F32).rearrange("p (h n w) -> p h n w", h=2, w=2),
                 in_=x_raw[(sg, b)][:].bitcast(F32).rearrange("p (n h w) -> p h n w", h=2, w=2)[:, :, MC * h : MC * h + MC, :],
             )
 
         def x_quant(c):
             xg = st[c]["xg"]
-            xc = work.tile([P, 512], U32, name="xc", bufs=3, align_bytes=64)
-            xs = work.tile([P, 512], U8, name="xs", bufs=3, align_bytes=64)
+            xc = work.tile([P, 512], U32, name="xc", bufs=2, align_bytes=64)
+            xs = work.tile([P, 512], U8, name="xs", bufs=2, align_bytes=64)
             nc.vector.quantize_mx(out=xc[:].bitcast(FP8X4), scales=xs[:], in_=xg[:])
             st[c]["xc"] = xc
             st[c]["xs"] = xs
@@ -250,7 +256,7 @@ def tile_refiner_pa_kernel(tc, X, Y, Wx, bx, Wy, by, base_w, spline_w, spline_sc
 
         def tanh(c):
             sg = c % 2
-            x = work.tile([P, CW], F32, name="x", bufs=4)
+            x = work.tile([P, CW], F32, name="x", bufs=2)
             for j in range(4):
                 nc.scalar.activation(
                     out=x[:, MC * j : MC * j + MC],
@@ -259,34 +265,47 @@ def tile_refiner_pa_kernel(tc, X, Y, Wx, bx, Wy, by, base_w, spline_w, spline_sc
                     bias=bias[:, 4 * sg + j : 4 * sg + j + 1],
                     scale=1.0,
                 )
-            st[c]["x"] = x
+            st[c]["xj"] = x
+
+        def weave(c):
+            st[c]["x"] = []
+            for half in range(2):
+                xi = bank("xi", F32)
+                nc.tensor.matmul(
+                    out=xi[:], lhsT=ident_f[:],
+                    rhs=st[c]["xj"][:].rearrange("p (j h m) -> p h m j", j=4, h=2)[:, half],
+                    start=True, stop=True,
+                )
+                st[c]["x"].append(xi)
+
+        def halves(c, src, dst):
+            t = st[c][src]
+            if src != "x":
+                return [(t[:], dst)]
+            return [(t[half][:], dst[:, 512 * half : 512 * half + 512]) for half in range(2)]
 
         def act(c, nm, src, func, scale, bi, tag, bufs):
             t = work.tile([P, CW], F32, name=nm, tag=tag, bufs=bufs)
-            if bi is None:
-                nc.scalar.activation(out=t[:], in_=st[c][src][:], func=func, scale=scale)
-            else:
-                nc.scalar.activation(out=t[:], in_=st[c][src][:], func=func, bias=cbias(bi), scale=scale)
+            for s, o in halves(c, src, t[:]):
+                if bi is None:
+                    nc.scalar.activation(out=o, in_=s, func=func, scale=scale)
+                else:
+                    nc.scalar.activation(out=o, in_=s, func=func, bias=cbias(bi), scale=scale)
             st[c][nm] = t
-
-        def product(c, dst, in0, scalar, in1):
-            nc.vector.scalar_tensor_tensor(
-                out=dst, in0=st[c][in0][:], scalar=scalar, in1=st[c][in1][:], op0=ALU.add, op1=ALU.mult
-            )
 
         A_OPS = {
             "f1": ("x", ACTF.Abs, 2.5, B_M05, "f1", 2),
             "a3": ("x", ACTF.Abs, 2.5, B_P05, "a3", 2),
             "g2": ("f1", ACTF.Abs, 1.0, B_M2, "fold", 2),
             "vb": ("g2", ACTF.Abs, 1.0, B_M1, "fold", 2),
-            "s4": ("g2", ACTF.Square, r6, None, "sq", 4),
-            "s6": ("f1", ACTF.Square, rc, None, "sq", 4),
-            "s3": ("a3", ACTF.Square, r6, B_M2R6, "sq", 4),
-            "s5": ("a3", ACTF.Square, rc, None, "sq", 4),
-            "q0": ("vb", ACTF.Square, -1.0, B_1HB, "sq", 4),
-            "l0": ("vb", ACTF.Identity, -0.5, B_L2, "lin", 2),
-            "q1": ("vb", ACTF.Square, 1.0, B_HB, "sq", 4),
-            "l1": ("vb", ACTF.Identity, 0.5, B_L1, "lin", 2),
+            "s4": ("f1", ACTF.Square, r6, B_M2R6, "sq", 6),
+            "s6": ("f1", ACTF.Square, rc, None, "sq", 6),
+            "s3": ("a3", ACTF.Square, r6, B_M2R6, "sq", 6),
+            "s5": ("a3", ACTF.Square, rc, None, "sq", 6),
+            "q0": ("vb", ACTF.Square, -1.0, B_1HB, "sq", 6),
+            "l0": ("vb", ACTF.Identity, 0.5, B_L2, "lin", 2),
+            "q1": ("vb", ACTF.Square, 1.0, B_HB, "sq", 6),
+            "l1": ("vb", ACTF.Identity, -0.5, B_L1, "lin", 2),
         }
 
         def aops(c, names):
@@ -308,45 +327,34 @@ def tile_refiner_pa_kernel(tc, X, Y, Wx, bx, Wy, by, base_w, spline_w, spline_sc
             if plane is None:
                 cap = work.tile([P, CW], BF16, name="cap%d" % f, align_bytes=64)
                 st[c]["cap%d" % f] = cap
-                product(c, cap[:], in0, scalar, in1)
+                dst = cap[:]
             else:
                 key = "pl%d" % f
                 if key not in st[c]:
-                    st[c][key] = work.tile([P, 4, CW], BF16, name=key, tag="pl", bufs=3, align_bytes=64)
-                product(c, st[c][key][:, plane, :], in0, scalar, in1)
+                    st[c][key] = work.tile([P, 2, CW], BF16, name=key, align_bytes=64)
+                dst = st[c][key][:, plane, :]
+            for k, (s, o) in enumerate(halves(c, in0, dst)):
+                other = st[c][in1][:] if in0 != "x" else st[c][in1][:, 512 * k : 512 * k + 512]
+                nc.vector.scalar_tensor_tensor(out=o, in0=s, scalar=scalar, in1=other, op0=ALU.add, op1=ALU.mult)
 
-        def views(dst, planes):
-            return dst.rearrange("p (c i j) -> p c j i", i=4, j=4), planes.rearrange("p j (c i) -> p c j i", i=4)
+        def cap_arm(c, f):
+            p0 = st[c]["pl%d" % f][:, 0, :]
+            nc.vector.tensor_tensor(out=p0, in0=p0, in1=st[c]["cap%d" % f][:], op=ALU.max)
 
-        def cut(c):
-            return (CW - (ACT_W_LAST if c == NCH - 1 else ACT_W)) // 4
-
-        def neg(c, f):
-            pl = st[c]["pl%d" % f]
-            nc.vector.tensor_scalar(out=pl[:, 2:4, :], in0=pl[:, 0:2, :], scalar1=-1.0, scalar2=None, op0=ALU.mult)
-
-        def cap_min(c, f):
-            pl = st[c]["pl%d" % f]
-            nc.vector.tensor_tensor(
-                out=pl[:, 1:4, :],
-                in0=pl[:, 1:4, :],
-                in1=st[c]["cap%d" % f][:].unsqueeze(1).to_broadcast([P, 3, CW]),
-                op=ALU.min,
-            )
-
-        def fam_views(c, f):
+        def split(c, f, side):
             key = "fam%d" % f
             if key not in st[c]:
-                st[c][key] = work.tile([P, 4 * CW], BF16, name="fam", align_bytes=64)
-            return views(st[c][key][:], st[c]["pl%d" % f][:])
+                st[c][key] = work.tile([P, 4, CW], BF16, name="fam", tag="fam", bufs=2, align_bytes=64)
+            nc.vector.tensor_scalar(
+                out=st[c][key][:, 2 * side : 2 * side + 2, :], in0=st[c]["pl%d" % f][:],
+                scalar1=sgn[:, 1 - side : 2 - side], scalar2=0.0, op0=ALU.mult, op1=ALU.min,
+            )
 
-        def weave(c, f):
-            o, s = fam_views(c, f)
-            nc.vector.tensor_scalar(out=o[:, 0 : cut(c)], in0=s[:, 0 : cut(c)], scalar1=0.0, scalar2=None, op0=ALU.max)
-
-        def relu_share(c, f):
-            o, s = fam_views(c, f)
-            nc.scalar.activation(out=o[:, cut(c) : CW // 4], in_=s[:, cut(c) : CW // 4], func=ACTF.Relu)
+        def cap_rest(c, f):
+            rest = st[c]["fam%d" % f][:, 1:4:2, :]
+            nc.vector.tensor_tensor(
+                out=rest, in0=rest, in1=st[c]["cap%d" % f][:].unsqueeze(1).to_broadcast([P, 2, CW]), op=ALU.max
+            )
 
         def quant_family(c, f):
             if f == 0:
@@ -354,185 +362,187 @@ def tile_refiner_pa_kernel(tc, X, Y, Wx, bx, Wy, by, base_w, spline_w, spline_sc
                 st[c]["scl"] = work.tile([P, 2 * CW], U8, name="scl", align_bytes=64)
             cols = slice(CW * f, CW * f + CW)
             nc.vector.quantize_mx(
-                out=st[c]["codes"][:, cols].bitcast(FP8X4), scales=st[c]["scl"][:, cols], in_=st[c]["fam%d" % f][:]
+                out=st[c]["codes"][:, cols].bitcast(FP8X4), scales=st[c]["scl"][:, cols],
+                in_=st[c]["fam%d" % f][:].rearrange("p a w -> p (a w)"),
             )
 
         def silu(c):
-            sil = work.tile([P, CW], BF16, name="sil", bufs=4, align_bytes=64)
-            o, s = views(sil[:], st[c]["x"][:].rearrange("p (j m) -> p j m", j=4))
-            nc.scalar.activation(out=o, in_=s, func=ACTF.Silu)
+            sil = work.tile([P, CW], BF16, name="sil", bufs=2, align_bytes=64)
+            for s, o in halves(c, "x", sil[:]):
+                nc.scalar.activation(out=o, in_=s, func=ACTF.Silu)
             st[c]["sil"] = sil
 
         def quant_silu(c):
-            bc = work.tile([P, MC], U32, name="bc", bufs=4, align_bytes=64)
-            bs = work.tile([P, MC], U8, name="bs", bufs=4, align_bytes=64)
+            bc = work.tile([P, MC], U32, name="bc", bufs=2, align_bytes=64)
+            bs = work.tile([P, MC], U8, name="bs", bufs=2, align_bytes=64)
             nc.vector.quantize_mx(out=bc[:].bitcast(FP8X4), scales=bs[:], in_=st[c]["sil"][:])
             st[c]["bc"] = bc
             st[c]["bs"] = bs
 
         def mx2(c, mt, lhs, lhs_s, m0, q0, start, stop):
-            v = c % 2
             nc.tensor.matmul_mx(
-                out=acc[(c // 2, mt)][:, 0:P],
+                out=acc[(c, mt)][:, 0:P],
                 lhsT=lhs[:, m0 : m0 + P].bitcast(FP8X4),
                 lhsT_scale=lhs_s[:, m0 : m0 + P],
-                rhs=swc[v][:, q0 : q0 + P].bitcast(FP8X4),
-                rhs_scale=sws[v][:, q0 : q0 + P],
+                rhs=swc[:, q0 : q0 + P].bitcast(FP8X4),
+                rhs_scale=sws[:, q0 : q0 + P],
                 start=start,
                 stop=stop,
             )
 
-        def m2_spline(c, last):
-            if c % 2 == 0:
-                for mt in range(2):
-                    acc[(c // 2, mt)] = psum.tile([P, 512], F32, name="acc", tag="acc", bufs=4)
-            for f in range(2):
-                for mt in range(2):
-                    for j in range(4):
-                        mx2(
-                            c, mt, st[c]["codes"], st[c]["scl"], CW * f + MC * j + P * mt, P * (2 * j + f),
-                            c % 2 == 0 and f == 0 and j == 0, last and f == 1 and j == 3,
-                        )
-
-        def m2_base(c, last):
+        def m2_base(c):
             for mt in range(2):
-                mx2(c, mt, st[c]["bc"], st[c]["bs"], P * mt, 8 * P, False, last)
+                acc[(c, mt)] = psum.tile([P, 512], F32, name="acc", tag="acc", bufs=2)
+                mx2(c, mt, st[c]["bc"], st[c]["bs"], P * mt, 8 * P, True, False)
 
-        def store(g):
-            b, h = g // 2, g % 2
+        def m2_family(c, f):
             for mt in range(2):
-                ob = work.tile([P, 64], F32, name="ob", bufs=4)
-                nc.scalar.copy(out=ob[:], in_=acc[(g, mt)][:, 0:64])
-                r0 = MC * h + P * mt
-                nc.sync.dma_start(out=out[b, r0 : r0 + P, :], in_=ob[:])
+                for n in range(4):
+                    mx2(
+                        c, mt, st[c]["codes"], st[c]["scl"], CW * f + MC * n + P * mt, P * (4 * f + n),
+                        False, f == 1 and n == 3,
+                    )
 
+        def finish(c):
+            b, h, sg = where(c)
+            for mt in range(2):
+                if sg == 0:
+                    ob = work.tile([P, 64], F32, name="ob", bufs=4)
+                    nc.vector.tensor_copy(out=ob[:], in_=acc[(c, mt)][:, 0:64])
+                    obx[(c, mt)] = ob
+                else:
+                    res = work.tile([P, 64], F32, name="res", bufs=4)
+                    nc.vector.tensor_tensor(out=res[:], in0=acc[(c, mt)][:, 64:128], in1=obx[(c - 1, mt)][:], op=ALU.add)
+                    r0 = MC * h + P * mt
+                    nc.sync.dma_start(out=out[b, r0 : r0 + P, :], in_=res[:])
+
+        V, S = nc.vector.tensor_copy, nc.scalar.copy
+        w_raw[0] = load_w(Wx, "wxr")
         nc.sync.dma_start(out=brow[0:4, :], in_=bx.rearrange("(r c) -> r c", c=P))
         nc.sync.dma_start(out=brow[4:8, :], in_=by.rearrange("(r c) -> r c", c=P))
-        w_raw[0] = load_w(Wx, "wxr")
-        x_raw[(0, 0)] = raw_tile("x0r")
-        load_x(X, 0, x_raw[(0, 0)], 0, 4096)
-        w_raw[1] = load_w(Wy, "wyr")
+        x_raw[(0, 0)] = load_x(X, 0, "x0r")
         load_small()
+        sw_raw = load_sw()
+        w_raw[1] = load_w(Wy, "wyr")
+        x_raw[(1, 0)] = load_x(Y, 0, "y0r")
 
-        w_regroup(0)
-        x_raw[(1, 0)] = raw_tile("y0r")
-        load_x(Y, 0, x_raw[(1, 0)], 0, 4096)
+        for j in range(4):
+            w_regroup(0, j, S if j % 2 else V)
+        x_raw[(0, 1)] = load_x(X, 1, "x1r")
+        for j in range(4):
+            w_transpose(0, j)
         pb0 = bank("pb0", BF16)
         nc.tensor.transpose(pb0[:, 0:P], brow[:], ident_b[:])
         bias = keep.tile([P, 8], F32, name="bias")
-        nc.vector.tensor_copy(out=bias[:], in_=pb0[:, 0:8])
-        w_transpose(0, 0, 4)
+        w_evac(0, 0, S)
+        w_evac(0, 1, V)
+        x_copy(0, V)
+        w_evac(0, 2, S)
         w_quant(0, 0, 2)
-        x_copy(0)
-        w_quant(0, 2, 4)
+        w_evac(0, 3, V)
         x_quant(0)
+        nc.vector.tensor_copy(out=bias[:], in_=pb0[:, 0:8])
+        w_quant(0, 2, 4)
         m1(0)
-        tanh(0)
-        aops(0, ("a3", "f1", "s3", "g2", "s5", "s6", "vb", "s4", "q0", "l0", "q1", "l1"))
-        w_regroup(1)
-        sw_raw = load_sw()
-        w_transpose(1, 0, 4)
-        w_quant(1, 0, 4)
-        vop(0, "P3")
         sw_small()
-        vop(0, "L5")
-        x_copy(2)
-        vop(0, "L6")
+        tanh(0)
+        x_copy(2, V)
+        sw_regroup(sw_raw, V)
         x_quant(2)
-        vop(0, "P4")
-        x_copy(1)
-        vop(0, "C0")
-        x_quant(1)
-        m1(1)
+        weave(0)
+        sw_small_evac()
+        for j in range(4):
+            w_regroup(1, j, S)
+        sw_transpose(0)
         m1(2)
-        vop(0, "C1")
-        tanh(1)
-        tanh(2)
-        x_copy(3)
-        neg(0, 0)
-        x_quant(3)
-        m1(3)
-        tanh(3)
-        for k in range(4):
-            silu(k)
-        sw_regroup(sw_raw)
-        x_raw[(0, 1)] = raw_tile("x1r")
-        load_x(X, 1, x_raw[(0, 1)], 0, 4096)
-        cap_min(0, 0)
-        neg(0, 1)
-        for kk in range(4):
-            sw_transpose(kk)
-        weave(0, 0)
         sw_products(0)
-        cap_min(0, 1)
+        sw_transpose(1)
         sw_products(1)
-        weave(0, 1)
+        aops(0, ("f1", "a3", "s6", "s4"))
+        sw_transpose(2)
         sw_products(2)
+        x_copy(1, S)
+        sw_transpose(3)
         sw_products(3)
-        sw_finish(0)
-        sw_finish(1)
-        x_raw[(1, 1)] = raw_tile("y1r")
-        load_x(Y, 1, x_raw[(1, 1)], 0, 4096)
-        for k in range(4):
-            quant_silu(k)
+        for j in range(4):
+            w_transpose(1, j)
+            w_evac(1, j, S)
+        x_raw[(1, 1)] = load_x(Y, 1, "y1r")
+        silu(0)
+        x_quant(1)
+        bw_quant()
+        sw_quant()
+        aops(0, ("g2", "vb"))
+        w_quant(1, 0, 4)
+        m1(1)
+        vop(0, "L6")
+        aops(0, ("q0", "l0"))
+        vop(0, "P4")
+        tanh(1)
+        vop(0, "C0")
+        aops(0, ("s5", "s3"))
+        weave(1)
+        x_copy(3, V)
+        cap_arm(0, 0)
+        vop(0, "L5")
+        split(0, 0, 0)
+        aops(0, ("q1", "l1"))
+        vop(0, "P3")
+        split(0, 0, 1)
+        x_quant(3)
+        tanh(2)
+        cap_rest(0, 0)
+        vop(0, "C1")
+        quant_family(0, 0)
+        quant_silu(0)
+        m2_base(0)
+        m2_family(0, 0)
+        m1(3)
 
         for c in range(1, NCH + 1):
             p = c - 1
             live = c < NCH
             nxt = c + 3 < NCH
+            if c + 1 < NCH:
+                weave(c + 1)
             if live:
-                if c >= 4:
-                    tanh(c)
-                aops(c, ("f1", "a3", "g2", "s6", "vb", "s4"))
-            if c > 1:
-                neg(p, 0)
-            if live:
+                aops(c, ("f1", "a3", "s6", "s4"))
+                silu(c)
+                aops(c, ("g2", "vb"))
                 vop(c, "L6")
-            if c > 1:
-                cap_min(p, 0)
-            relu_share(p, 0)
+            cap_arm(p, 1)
             if live:
-                aops(c, ("s5", "q0", "s3", "l0"))
                 vop(c, "P4")
-            if c > 1:
-                weave(p, 0)
-                neg(p, 1)
+                aops(c, ("q0", "l0"))
+            split(p, 1, 0)
             if nxt:
-                x_copy(c + 3)
-            if c > 1:
-                cap_min(p, 1)
-            relu_share(p, 1)
-            if live:
-                aops(c, ("q1", "l1"))
-                vop(c, "L5")
-            if c > 1:
-                weave(p, 1)
-            if c == NCH:
-                for k in range(4, NCH):
-                    quant_silu(k)
-                m2_base(4, False)
-                m2_base(5, True)
-                store(2)
-                m2_base(6, False)
-                m2_base(7, False)
-            quant_family(p, 0)
-            if live:
-                vop(c, "P3")
-            if nxt:
-                x_quant(c + 3)
-                m1(c + 3)
+                x_copy(c + 3, V)
+            split(p, 1, 1)
             if live:
                 vop(c, "C0")
-            quant_family(p, 1)
-            m2_spline(p, c == NCH)
+                aops(c, ("s5", "s3"))
+            cap_rest(p, 1)
+            if nxt:
+                x_quant(c + 3)
             if live:
+                cap_arm(c, 0)
+            if c + 2 < NCH:
+                tanh(c + 2)
+            quant_family(p, 1)
+            m2_family(p, 1)
+            if live:
+                vop(c, "L5")
+                split(c, 0, 0)
+                aops(c, ("q1", "l1"))
+                vop(c, "P3")
+                split(c, 0, 1)
+                finish(p)
+                quant_silu(c)
+                cap_rest(c, 0)
                 vop(c, "C1")
-            if p in (1, 3):
-                m2_base(p - 1, False)
-                m2_base(p, True)
-            if p in (2, 4):
-                store((p - 1) // 2)
-            if c == NCH - 1:
-                for k in range(4, NCH):
-                    silu(k)
-        store(3)
+                quant_family(c, 0)
+                m2_base(c)
+                m2_family(c, 0)
+            if nxt:
+                m1(c + 3)
+        finish(NCH - 1)

@@ -77,17 +77,18 @@ def tile_refiner_pa_kernel(tc, X, Y, Wx, bx, Wy, by, base_w, spline_w, spline_sc
 
         def load_w(w, nm):
             wr = raw_tile(nm)
-            for j in range(4):
-                nc.sync.dma_start(out=wr[:, 1024 * j : 1024 * j + 1024], in_=w[P * j : P * j + P, :])
+            for jj in range(2):
+                nc.sync.dma_start(
+                    out=wr[:, 2048 * jj : 2048 * jj + 2048].rearrange("p (j k) -> p j k", j=2),
+                    in_=w[256 * jj : 256 * jj + 256, :].rearrange("(j p) k -> p j k", p=P),
+                )
             return wr
 
-        def load_x(x, b, nm):
-            xr = raw_tile(nm)
+        def load_x(x, b, xr, lo, hi):
             src = x[b].rearrange("(a c) n f -> c a (n f)", c=16)
             for cl in range(4):
                 for s in range(4):
-                    nc.sync.dma_start(out=xr[32 * cl + s : 32 * cl + 32 : 4, :], in_=src[4 * cl + s])
-            return xr
+                    nc.sync.dma_start(out=xr[32 * cl + s : 32 * cl + 32 : 4, lo:hi], in_=src[4 * cl + s][:, lo:hi])
 
         def load_sw():
             swr = raw_tile("swr")
@@ -167,11 +168,8 @@ def tile_refiner_pa_kernel(tc, X, Y, Wx, bx, Wy, by, base_w, spline_w, spline_sc
 
         def sw_small_evac():
             psc, pbw = sw_state["psc"], sw_state["pbw"]
-            nc.vector.tensor_scalar(
-                out=sct[:].rearrange("p (q j) -> p q j", j=4), in0=psc[:].rearrange("p (j q) -> p q j", j=4),
-                scalar1=-1.0, scalar2=None, op0=ALU.mult,
-            )
-            nc.vector.tensor_copy(out=bwt[:].rearrange("p (q j) -> p q j", j=4), in_=pbw[:].rearrange("p (j q) -> p q j", j=4))
+            nc.scalar.mul(sct[:].rearrange("p (q j) -> p q j", j=4), psc[:].rearrange("p (j q) -> p q j", j=4), -1.0)
+            nc.scalar.copy(out=bwt[:].rearrange("p (q j) -> p q j", j=4), in_=pbw[:].rearrange("p (j q) -> p q j", j=4))
 
         def sw_regroup(swr, copier):
             swg = grp_tile("swg", 2048, F32)
@@ -418,17 +416,22 @@ def tile_refiner_pa_kernel(tc, X, Y, Wx, bx, Wy, by, base_w, spline_w, spline_sc
 
         V, S = nc.vector.tensor_copy, nc.scalar.copy
         w_raw[0] = load_w(Wx, "wxr")
+        x_raw[(0, 0)] = raw_tile("x0r")
+        load_x(X, 0, x_raw[(0, 0)], 0, 2048)
         nc.sync.dma_start(out=brow[0:4, :], in_=bx.rearrange("(r c) -> r c", c=P))
         nc.sync.dma_start(out=brow[4:8, :], in_=by.rearrange("(r c) -> r c", c=P))
-        x_raw[(0, 0)] = load_x(X, 0, "x0r")
+        w_raw[1] = load_w(Wy, "wyr")
         load_small()
         sw_raw = load_sw()
-        w_raw[1] = load_w(Wy, "wyr")
-        x_raw[(1, 0)] = load_x(Y, 0, "y0r")
+        x_raw[(1, 0)] = raw_tile("y0r")
+        load_x(Y, 0, x_raw[(1, 0)], 0, 2048)
+        load_x(X, 0, x_raw[(0, 0)], 2048, 4096)
+        load_x(Y, 0, x_raw[(1, 0)], 2048, 4096)
 
         for j in range(4):
             w_regroup(0, j, S if j % 2 else V)
-        x_raw[(0, 1)] = load_x(X, 1, "x1r")
+        x_raw[(0, 1)] = raw_tile("x1r")
+        load_x(X, 1, x_raw[(0, 1)], 0, 4096)
         for j in range(4):
             w_transpose(0, j)
         pb0 = bank("pb0", BF16)
@@ -444,44 +447,51 @@ def tile_refiner_pa_kernel(tc, X, Y, Wx, bx, Wy, by, base_w, spline_w, spline_sc
         nc.vector.tensor_copy(out=bias[:], in_=pb0[:, 0:8])
         w_quant(0, 2, 4)
         m1(0)
+        for j in range(4):
+            w_regroup(1, j, S if j < 3 else V)
         sw_small()
         tanh(0)
-        x_copy(2, V)
-        sw_regroup(sw_raw, V)
-        x_quant(2)
+        for j in range(2):
+            w_transpose(1, j)
+        w_evac(1, 0, S)
+        w_evac(1, 1, V)
         weave(0)
         sw_small_evac()
-        for j in range(4):
-            w_regroup(1, j, S)
-        sw_transpose(0)
-        m1(2)
-        sw_products(0)
-        sw_transpose(1)
-        sw_products(1)
-        aops(0, ("f1", "a3", "s6", "s4"))
-        sw_transpose(2)
-        sw_products(2)
-        x_copy(1, S)
-        sw_transpose(3)
-        sw_products(3)
-        for j in range(4):
+        sw_regroup(sw_raw, V)
+        for j in range(2, 4):
             w_transpose(1, j)
-            w_evac(1, j, S)
-        x_raw[(1, 1)] = load_x(Y, 1, "y1r")
-        silu(0)
+        sw_transpose(0)
+        w_evac(1, 2, V)
+        x_copy(1, V)
+        w_evac(1, 3, V)
+        sw_transpose(1)
+        aops(0, ("f1", "a3"))
         x_quant(1)
-        bw_quant()
-        sw_quant()
-        aops(0, ("g2", "vb"))
         w_quant(1, 0, 4)
         m1(1)
+        aops(0, ("s6", "s4"))
+        silu(0)
+        sw_products(0)
+        sw_products(1)
+        sw_transpose(2)
+        x_copy(2, V)
+        aops(0, ("g2", "vb"))
         vop(0, "L6")
-        aops(0, ("q0", "l0"))
-        vop(0, "P4")
+        sw_transpose(3)
+        x_quant(2)
         tanh(1)
+        weave(1)
+        m1(2)
+        sw_products(2)
+        vop(0, "P4")
+        sw_products(3)
+        x_raw[(1, 1)] = raw_tile("y1r")
+        load_x(Y, 1, x_raw[(1, 1)], 0, 4096)
+        bw_quant()
+        aops(0, ("q0", "l0"))
+        sw_quant()
         vop(0, "C0")
         aops(0, ("s5", "s3"))
-        weave(1)
         x_copy(3, V)
         cap_arm(0, 0)
         vop(0, "L5")
@@ -516,7 +526,7 @@ def tile_refiner_pa_kernel(tc, X, Y, Wx, bx, Wy, by, base_w, spline_w, spline_sc
                 aops(c, ("q0", "l0"))
             split(p, 1, 0)
             if nxt:
-                x_copy(c + 3, V)
+                x_copy(c + 3, S if c > 1 else V)
             split(p, 1, 1)
             if live:
                 vop(c, "C0")

@@ -73,7 +73,7 @@ def tile_refiner_pa_kernel(tc, X, Y, Wx, bx, Wy, by, base_w, spline_w, spline_sc
         nc.vector.tensor_scalar(out=sgn[:, 1:2], in0=low[:], scalar1=-2.0, scalar2=1.0, op0=ALU.mult, op1=ALU.add)
 
         def raw_tile(nm):
-            return prep.tile([P, 4096], BF16, name=nm, tag="raw", bufs=5)
+            return prep.tile([P, 4096], BF16, name=nm, tag="raw", bufs=5, align_bytes=64)
 
         def load_w(w, nm):
             wr = raw_tile(nm)
@@ -84,11 +84,13 @@ def tile_refiner_pa_kernel(tc, X, Y, Wx, bx, Wy, by, base_w, spline_w, spline_sc
                 )
             return wr
 
-        def load_x(x, b, xr, lo, hi):
-            src = x[b].rearrange("(a c) n f -> c a (n f)", c=16)
+        def load_x(sg, b):
+            xr = prep.tile([P, 4096], BF16, name="xr%d%d" % (sg, b), tag="xr", bufs=2)
+            src = (X, Y)[sg][b].rearrange("(a c) n f -> c a (n f)", c=16)
             for cl in range(4):
                 for s in range(4):
-                    nc.sync.dma_start(out=xr[32 * cl + s : 32 * cl + 32 : 4, lo:hi], in_=src[4 * cl + s][:, lo:hi])
+                    nc.sync.dma_start(out=xr[32 * cl + s : 32 * cl + 32 : 4, :], in_=src[4 * cl + s])
+            x_raw[(sg, b)] = xr
 
         def load_sw():
             swr = raw_tile("swr")
@@ -107,7 +109,7 @@ def tile_refiner_pa_kernel(tc, X, Y, Wx, bx, Wy, by, base_w, spline_w, spline_sc
         w_scales = [None, None]
 
         def grp_tile(nm, cols, dt):
-            return prep.tile([P, cols], dt, name=nm, tag="grp", bufs=3, align_bytes=64)
+            return prep.tile([P, cols], dt, name=nm, tag="raw", bufs=5, align_bytes=64)
 
         def w_regroup(sg, j, copier):
             if w_grp[sg] is None:
@@ -168,8 +170,11 @@ def tile_refiner_pa_kernel(tc, X, Y, Wx, bx, Wy, by, base_w, spline_w, spline_sc
 
         def sw_small_evac():
             psc, pbw = sw_state["psc"], sw_state["pbw"]
-            nc.scalar.mul(sct[:].rearrange("p (q j) -> p q j", j=4), psc[:].rearrange("p (j q) -> p q j", j=4), -1.0)
-            nc.scalar.copy(out=bwt[:].rearrange("p (q j) -> p q j", j=4), in_=pbw[:].rearrange("p (j q) -> p q j", j=4))
+            nc.vector.tensor_scalar(
+                out=sct[:].rearrange("p (q j) -> p q j", j=4), in0=psc[:].rearrange("p (j q) -> p q j", j=4),
+                scalar1=-1.0, scalar2=None, op0=ALU.mult,
+            )
+            nc.vector.tensor_copy(out=bwt[:].rearrange("p (q j) -> p q j", j=4), in_=pbw[:].rearrange("p (j q) -> p q j", j=4))
 
         def sw_regroup(swr, copier):
             swg = grp_tile("swg", 2048, F32)
@@ -276,82 +281,99 @@ def tile_refiner_pa_kernel(tc, X, Y, Wx, bx, Wy, by, base_w, spline_w, spline_sc
                 )
                 st[c]["x"].append(xi)
 
+        def weave_first(c):
+            xi = work.tile([P, CW], F32, name="x", bufs=2)
+            nc.vector.tensor_copy(
+                out=xi[:].rearrange("p (c i j) -> p c j i", i=4, j=4),
+                in_=st[c]["xj"][:].rearrange("p (j c i) -> p c j i", i=4, j=4),
+            )
+            st[c]["x"] = xi
+
         def halves(c, src, dst):
             t = st[c][src]
-            if src != "x":
+            if src != "x" or c == 0:
                 return [(t[:], dst)]
             return [(t[half][:], dst[:, 512 * half : 512 * half + 512]) for half in range(2)]
 
-        def act(c, nm, src, func, scale, bi, tag, bufs):
-            t = work.tile([P, CW], F32, name=nm, tag=tag, bufs=bufs)
-            for s, o in halves(c, src, t[:]):
-                if bi is None:
-                    nc.scalar.activation(out=o, in_=s, func=func, scale=scale)
-                else:
-                    nc.scalar.activation(out=o, in_=s, func=func, bias=cbias(bi), scale=scale)
-            st[c][nm] = t
+        def pair(c, nm, tag, bufs):
+            if nm not in st[c]:
+                st[c][nm] = work.tile([P, 2, CW], F32, name=nm, tag=tag, bufs=bufs)
+            return st[c][nm]
 
-        A_OPS = {
-            "f1": ("x", ACTF.Abs, 2.5, B_M05, "f1", 2),
-            "a3": ("x", ACTF.Abs, 2.5, B_P05, "a3", 2),
-            "g2": ("f1", ACTF.Abs, 1.0, B_M2, "fold", 2),
-            "vb": ("g2", ACTF.Abs, 1.0, B_M1, "fold", 2),
-            "s4": ("f1", ACTF.Square, r6, B_M2R6, "sq", 6),
-            "s6": ("f1", ACTF.Square, rc, None, "sq", 6),
-            "s3": ("a3", ACTF.Square, r6, B_M2R6, "sq", 6),
-            "s5": ("a3", ACTF.Square, rc, None, "sq", 6),
-            "q0": ("vb", ACTF.Square, -1.0, B_1HB, "sq", 6),
-            "l0": ("vb", ACTF.Identity, 0.5, B_L2, "lin", 2),
-            "q1": ("vb", ACTF.Square, 1.0, B_HB, "sq", 6),
-            "l1": ("vb", ACTF.Identity, -0.5, B_L1, "lin", 2),
-        }
-
-        def aops(c, names):
-            for nm in names:
-                src, func, scale, bi, tag, bufs = A_OPS[nm]
-                act(c, nm, src, func, scale, bi, tag, bufs)
-
-        V_OPS = {
-            "P4": (0, 0, "f1", -2.0, "s4"),
-            "L6": (0, 1, "x", -0.2, "s6"),
-            "P3": (1, 0, "a3", -2.0, "s3"),
-            "L5": (1, 1, "x", 0.2, "s5"),
-            "C0": (0, None, "q0", cp, "l0"),
-            "C1": (1, None, "q1", cp, "l1"),
-        }
-
-        def vop(c, nm):
-            f, plane, in0, scalar, in1 = V_OPS[nm]
-            if plane is None:
-                cap = work.tile([P, CW], BF16, name="cap%d" % f, align_bytes=64)
-                st[c]["cap%d" % f] = cap
-                dst = cap[:]
+        def act(out_, in_, func, scale, bi):
+            if bi is None:
+                nc.scalar.activation(out=out_, in_=in_, func=func, scale=scale)
             else:
-                key = "pl%d" % f
-                if key not in st[c]:
-                    st[c][key] = work.tile([P, 2, CW], BF16, name=key, align_bytes=64)
-                dst = st[c][key][:, plane, :]
-            for k, (s, o) in enumerate(halves(c, in0, dst)):
-                other = st[c][in1][:] if in0 != "x" else st[c][in1][:, 512 * k : 512 * k + 512]
-                nc.vector.scalar_tensor_tensor(out=o, in0=s, scalar=scalar, in1=other, op0=ALU.add, op1=ALU.mult)
+                nc.scalar.activation(out=out_, in_=in_, func=func, bias=cbias(bi), scale=scale)
 
-        def cap_arm(c, f):
-            p0 = st[c]["pl%d" % f][:, 0, :]
-            nc.vector.tensor_tensor(out=p0, in0=p0, in1=st[c]["cap%d" % f][:], op=ALU.max)
+        def dist(c, f):
+            t = pair(c, "fa", "fa", 2)
+            for s, o in halves(c, "x", t[:, f, :]):
+                act(o, s, ACTF.Abs, 2.5, (B_M05, B_P05)[f])
 
-        def split(c, f, side):
-            key = "fam%d" % f
-            if key not in st[c]:
-                st[c][key] = work.tile([P, 4, CW], BF16, name="fam", tag="fam", bufs=2, align_bytes=64)
+        def fold(c, dst, src, bi):
+            t = work.tile([P, CW], F32, name=dst, tag="fold", bufs=2)
+            st[c][dst] = t
+            s = st[c]["fa"][:, 0, :] if src == "fa" else st[c][src][:]
+            act(t[:], s, ACTF.Abs, 1.0, bi)
+
+        def squares(c, nm, scale, bi, fs):
+            act(pair(c, nm, "sq", 4)[:, fs], st[c]["fa"][:, fs], ACTF.Square, scale, bi)
+
+        def cap_square(c, f):
+            act(pair(c, "q", "sq", 4)[:, f, :], st[c]["vb"][:], ACTF.Square, (-1.0, 1.0)[f], (B_1HB, B_HB)[f])
+
+        def cap_line(c, f):
+            act(pair(c, "l", "lin", 2)[:, f, :], st[c]["vb"][:], ACTF.Identity, (0.5, -0.5)[f], (B_L2, B_L1)[f])
+
+        def cap_line_v(c, f):
             nc.vector.tensor_scalar(
-                out=st[c][key][:, 2 * side : 2 * side + 2, :], in0=st[c]["pl%d" % f][:],
+                out=pair(c, "l", "lin", 2)[:, f, :], in0=st[c]["vb"][:], scalar1=(0.5, -0.5)[f],
+                scalar2=((a0 - 1.0) / 2.0, a0 / 2.0)[f], op0=ALU.mult, op1=ALU.add,
+            )
+
+        def arms(c):
+            if "arms" not in st[c]:
+                st[c]["arms"] = work.tile([P, 2, 2, CW], BF16, name="arms", align_bytes=64)
+            return st[c]["arms"]
+
+        def outer_arms(c, fs):
+            nc.vector.scalar_tensor_tensor(
+                out=arms(c)[:, 0, fs], in0=st[c]["fa"][:, fs], scalar=-2.0, in1=st[c]["sp"][:, fs], op0=ALU.add, op1=ALU.mult
+            )
+
+        def inner_arm(c, f):
+            sl = st[c]["sl"][:, f, :]
+            parts = halves(c, "x", arms(c)[:, 1, f, :])
+            w = CW // len(parts)
+            for k, (s, o) in enumerate(parts):
+                nc.vector.scalar_tensor_tensor(
+                    out=o, in0=s, scalar=(-0.2, 0.2)[f], in1=sl[:, w * k : w * k + w], op0=ALU.add, op1=ALU.mult
+                )
+
+        def caps(c, fs):
+            if "cap" not in st[c]:
+                st[c]["cap"] = work.tile([P, 2, CW], BF16, name="cap", align_bytes=64)
+            nc.vector.scalar_tensor_tensor(
+                out=st[c]["cap"][:, fs], in0=st[c]["q"][:, fs], scalar=cp, in1=st[c]["l"][:, fs], op0=ALU.add, op1=ALU.mult
+            )
+
+        def cap_arms(c, fs):
+            o = arms(c)[:, 0, fs]
+            nc.vector.tensor_tensor(out=o, in0=o, in1=st[c]["cap"][:, fs], op=ALU.max)
+
+        def split(c, side, fs):
+            if "fam" not in st[c]:
+                st[c]["fam"] = work.tile([P, 2, 4, CW], BF16, name="fam", bufs=1, align_bytes=64)
+            nc.vector.tensor_scalar(
+                out=st[c]["fam"][:, fs, 2 * side : 2 * side + 2, :], in0=arms(c)[:].rearrange("p k f w -> p f k w")[:, fs],
                 scalar1=sgn[:, 1 - side : 2 - side], scalar2=0.0, op0=ALU.mult, op1=ALU.min,
             )
 
-        def cap_rest(c, f):
-            rest = st[c]["fam%d" % f][:, 1:4:2, :]
+        def cap_rest(c, fs):
+            rest = st[c]["fam"][:, fs, 1:4:2, :]
             nc.vector.tensor_tensor(
-                out=rest, in0=rest, in1=st[c]["cap%d" % f][:].unsqueeze(1).to_broadcast([P, 2, CW]), op=ALU.max
+                out=rest, in0=rest, in1=st[c]["cap"][:, fs].unsqueeze(2).to_broadcast([P, fs.stop - fs.start, 2, CW]), op=ALU.max
             )
 
         def quant_family(c, f):
@@ -361,7 +383,7 @@ def tile_refiner_pa_kernel(tc, X, Y, Wx, bx, Wy, by, base_w, spline_w, spline_sc
             cols = slice(CW * f, CW * f + CW)
             nc.vector.quantize_mx(
                 out=st[c]["codes"][:, cols].bitcast(FP8X4), scales=st[c]["scl"][:, cols],
-                in_=st[c]["fam%d" % f][:].rearrange("p a w -> p (a w)"),
+                in_=st[c]["fam"][:, f].rearrange("p a w -> p (a w)"),
             )
 
         def silu(c):
@@ -377,61 +399,61 @@ def tile_refiner_pa_kernel(tc, X, Y, Wx, bx, Wy, by, base_w, spline_w, spline_sc
             st[c]["bc"] = bc
             st[c]["bs"] = bs
 
-        def mx2(c, mt, lhs, lhs_s, m0, q0, start, stop):
-            nc.tensor.matmul_mx(
-                out=acc[(c, mt)][:, 0:P],
-                lhsT=lhs[:, m0 : m0 + P].bitcast(FP8X4),
-                lhsT_scale=lhs_s[:, m0 : m0 + P],
-                rhs=swc[:, q0 : q0 + P].bitcast(FP8X4),
-                rhs_scale=sws[:, q0 : q0 + P],
-                start=start,
-                stop=stop,
-            )
-
-        def m2_base(c):
-            for mt in range(2):
-                acc[(c, mt)] = psum.tile([P, 512], F32, name="acc", tag="acc", bufs=2)
-                mx2(c, mt, st[c]["bc"], st[c]["bs"], P * mt, 8 * P, True, False)
-
-        def m2_family(c, f):
-            for mt in range(2):
+        def m2(c, mt, fams, first, last):
+            if first:
+                if c == NCH - 1 and mt == 1:
+                    acc[(c, mt)] = bank("acc1", F32)[:, 0:P]
+                else:
+                    if mt == 0:
+                        acc[c] = psum.tile([P, 512], F32, name="acc", tag="acc", bufs=2)
+                    acc[(c, mt)] = acc[c][:, P * mt : P * mt + P]
+            runs = [(st[c]["bc"], st[c]["bs"], P * mt, 8 * P)] if first else []
+            for f in fams:
                 for n in range(4):
-                    mx2(
-                        c, mt, st[c]["codes"], st[c]["scl"], CW * f + MC * n + P * mt, P * (4 * f + n),
-                        False, f == 1 and n == 3,
-                    )
+                    runs.append((st[c]["codes"], st[c]["scl"], CW * f + MC * n + P * mt, P * (4 * f + n)))
+            for k, (lhs, lhs_s, m0, q0) in enumerate(runs):
+                nc.tensor.matmul_mx(
+                    out=acc[(c, mt)],
+                    lhsT=lhs[:, m0 : m0 + P].bitcast(FP8X4),
+                    lhsT_scale=lhs_s[:, m0 : m0 + P],
+                    rhs=swc[:, q0 : q0 + P].bitcast(FP8X4),
+                    rhs_scale=sws[:, q0 : q0 + P],
+                    start=(first and k == 0),
+                    stop=(last and k == len(runs) - 1),
+                )
 
         def finish(c):
             b, h, sg = where(c)
-            for mt in range(2):
-                if sg == 0:
-                    ob = work.tile([P, 64], F32, name="ob", bufs=4)
-                    nc.vector.tensor_copy(out=ob[:], in_=acc[(c, mt)][:, 0:64])
-                    obx[(c, mt)] = ob
-                else:
-                    res = work.tile([P, 64], F32, name="res", bufs=4)
-                    nc.vector.tensor_tensor(out=res[:], in0=acc[(c, mt)][:, 64:128], in1=obx[(c - 1, mt)][:], op=ALU.add)
-                    r0 = MC * h + P * mt
-                    nc.sync.dma_start(out=out[b, r0 : r0 + P, :], in_=res[:])
+            cols = slice(64 * sg, 64 * sg + 64)
+            rows = out[b, MC * h : MC * h + MC, :].rearrange("(mt p) o -> p mt o", p=P)
+            if sg == 0:
+                ob = work.tile([P, 2, 64], F32, name="ob", bufs=2)
+                nc.vector.tensor_copy(out=ob[:], in_=acc[c][:, 0 : 2 * P].rearrange("p (mt q) -> p mt q", mt=2)[:, :, cols])
+                obx[c] = ob
+            elif c < NCH - 1:
+                res = work.tile([P, 2, 64], F32, name="res", bufs=2)
+                both = acc[c][:, 0 : 2 * P].rearrange("p (mt q) -> p mt q", mt=2)[:, :, cols]
+                nc.vector.tensor_tensor(out=res[:], in0=both, in1=obx[c - 1][:], op=ALU.add)
+                nc.sync.dma_start(out=rows, in_=res[:])
+            else:
+                for mt in range(2):
+                    res = work.tile([P, 64], F32, name="last", bufs=2)
+                    nc.vector.tensor_tensor(out=res[:], in0=acc[(c, mt)][:, cols], in1=obx[c - 1][:, mt, :], op=ALU.add)
+                    nc.sync.dma_start(out=rows[:, mt, :], in_=res[:])
 
         V, S = nc.vector.tensor_copy, nc.scalar.copy
+        BOTH, EVEN, ODD = slice(0, 2), slice(0, 1), slice(1, 2)
         w_raw[0] = load_w(Wx, "wxr")
-        x_raw[(0, 0)] = raw_tile("x0r")
-        load_x(X, 0, x_raw[(0, 0)], 0, 2048)
+        load_x(0, 0)
         nc.sync.dma_start(out=brow[0:4, :], in_=bx.rearrange("(r c) -> r c", c=P))
         nc.sync.dma_start(out=brow[4:8, :], in_=by.rearrange("(r c) -> r c", c=P))
         w_raw[1] = load_w(Wy, "wyr")
-        load_small()
         sw_raw = load_sw()
-        x_raw[(1, 0)] = raw_tile("y0r")
-        load_x(Y, 0, x_raw[(1, 0)], 0, 2048)
-        load_x(X, 0, x_raw[(0, 0)], 2048, 4096)
-        load_x(Y, 0, x_raw[(1, 0)], 2048, 4096)
+        load_small()
+        load_x(1, 0)
 
         for j in range(4):
             w_regroup(0, j, S if j % 2 else V)
-        x_raw[(0, 1)] = raw_tile("x1r")
-        load_x(X, 1, x_raw[(0, 1)], 0, 4096)
         for j in range(4):
             w_transpose(0, j)
         pb0 = bank("pb0", BF16)
@@ -439,120 +461,148 @@ def tile_refiner_pa_kernel(tc, X, Y, Wx, bx, Wy, by, base_w, spline_w, spline_sc
         bias = keep.tile([P, 8], F32, name="bias")
         w_evac(0, 0, S)
         w_evac(0, 1, V)
-        x_copy(0, V)
         w_evac(0, 2, S)
         w_quant(0, 0, 2)
         w_evac(0, 3, V)
-        x_quant(0)
         nc.vector.tensor_copy(out=bias[:], in_=pb0[:, 0:8])
         w_quant(0, 2, 4)
-        m1(0)
+        x_copy(0, V)
         for j in range(4):
             w_regroup(1, j, S if j < 3 else V)
-        sw_small()
-        tanh(0)
+        x_quant(0)
+        m1(0)
+        x_copy(2, V)
         for j in range(2):
             w_transpose(1, j)
+        tanh(0)
         w_evac(1, 0, S)
-        w_evac(1, 1, V)
-        weave(0)
-        sw_small_evac()
+        sw_small()
+        x_quant(2)
         sw_regroup(sw_raw, V)
+        weave_first(0)
+        sw_transpose(0)
+        w_evac(1, 1, V)
+        sw_small_evac()
+        dist(0, 0)
+        dist(0, 1)
+        sw_transpose(1)
         for j in range(2, 4):
             w_transpose(1, j)
-        sw_transpose(0)
-        w_evac(1, 2, V)
-        x_copy(1, V)
-        w_evac(1, 3, V)
-        sw_transpose(1)
-        aops(0, ("f1", "a3"))
-        x_quant(1)
-        w_quant(1, 0, 4)
-        m1(1)
-        aops(0, ("s6", "s4"))
-        silu(0)
         sw_products(0)
         sw_products(1)
+        w_evac(1, 2, V)
+        w_evac(1, 3, V)
         sw_transpose(2)
-        x_copy(2, V)
-        aops(0, ("g2", "vb"))
-        vop(0, "L6")
+        squares(0, "sl", rc, None, BOTH)
+        silu(0)
+        x_copy(1, V)
+        w_quant(1, 0, 4)
+        x_quant(1)
+        m1(1)
         sw_transpose(3)
-        x_quant(2)
+        squares(0, "sp", r6, B_M2R6, BOTH)
+        inner_arm(0, 0)
         tanh(1)
         weave(1)
-        m1(2)
+        inner_arm(0, 1)
         sw_products(2)
-        vop(0, "P4")
         sw_products(3)
-        x_raw[(1, 1)] = raw_tile("y1r")
-        load_x(Y, 1, x_raw[(1, 1)], 0, 4096)
+        m1(2)
+        load_x(0, 1)
         bw_quant()
-        aops(0, ("q0", "l0"))
-        sw_quant()
-        vop(0, "C0")
-        aops(0, ("s5", "s3"))
+        fold(0, "g2", "fa", B_M2)
+        fold(0, "vb", "g2", B_M1)
+        outer_arms(0, BOTH)
         x_copy(3, V)
-        cap_arm(0, 0)
-        vop(0, "L5")
-        split(0, 0, 0)
-        aops(0, ("q1", "l1"))
-        vop(0, "P3")
-        split(0, 0, 1)
-        x_quant(3)
+        sw_quant()
+        for f in range(2):
+            cap_line_v(0, f)
+            cap_square(0, f)
         tanh(2)
-        cap_rest(0, 0)
-        vop(0, "C1")
-        quant_family(0, 0)
-        quant_silu(0)
-        m2_base(0)
-        m2_family(0, 0)
-        m1(3)
+        load_x(1, 1)
+        caps(0, BOTH)
 
-        for c in range(1, NCH + 1):
+        for c in range(1, NCH - 1):
             p = c - 1
-            live = c < NCH
             nxt = c + 3 < NCH
-            if c + 1 < NCH:
-                weave(c + 1)
-            if live:
-                aops(c, ("f1", "a3", "s6", "s4"))
-                silu(c)
-                aops(c, ("g2", "vb"))
-                vop(c, "L6")
-            cap_arm(p, 1)
-            if live:
-                vop(c, "P4")
-                aops(c, ("q0", "l0"))
-            split(p, 1, 0)
+            weave(c + 1)
+            dist(c, 0)
+            dist(c, 1)
+            silu(c)
+            squares(c, "sl", rc, None, BOTH)
+            squares(c, "sp", r6, B_M2R6, BOTH)
+            cap_arms(p, BOTH)
+            quant_silu(p)
+            if c + 2 < NCH:
+                x_quant(c + 2)
+                m1(c + 2)
+            split(p, 0, BOTH)
+            fold(c, "g2", "fa", B_M2)
+            fold(c, "vb", "g2", B_M1)
+            split(p, 1, BOTH)
+            inner_arm(c, 0)
+            inner_arm(c, 1)
+            for f in range(2):
+                cap_square(c, f)
+                cap_line(c, f)
             if nxt:
-                x_copy(c + 3, S if c > 1 else V)
-            split(p, 1, 1)
-            if live:
-                vop(c, "C0")
-                aops(c, ("s5", "s3"))
-            cap_rest(p, 1)
-            if nxt:
-                x_quant(c + 3)
-            if live:
-                cap_arm(c, 0)
+                x_copy(c + 3, S if c > 3 else V)
             if c + 2 < NCH:
                 tanh(c + 2)
+            if p > 0:
+                finish(p - 1)
+            cap_rest(p, BOTH)
+            outer_arms(c, BOTH)
+            quant_family(p, 0)
+            caps(c, BOTH)
             quant_family(p, 1)
-            m2_family(p, 1)
-            if live:
-                vop(c, "L5")
-                split(c, 0, 0)
-                aops(c, ("q1", "l1"))
-                vop(c, "P3")
-                split(c, 0, 1)
-                finish(p)
-                quant_silu(c)
-                cap_rest(c, 0)
-                vop(c, "C1")
-                quant_family(c, 0)
-                m2_base(c)
-                m2_family(c, 0)
-            if nxt:
-                m1(c + 3)
-        finish(NCH - 1)
+            for mt in range(2):
+                m2(p, mt, (0, 1), True, True)
+
+        p, c = NCH - 2, NCH - 1
+        dist(c, 0)
+        dist(c, 1)
+        silu(c)
+        squares(c, "sl", rc, None, EVEN)
+        squares(c, "sp", r6, B_M2R6, EVEN)
+        fold(c, "g2", "fa", B_M2)
+        fold(c, "vb", "g2", B_M1)
+        cap_square(c, 0)
+        cap_line(c, 0)
+        squares(c, "sl", rc, None, ODD)
+        squares(c, "sp", r6, B_M2R6, ODD)
+        cap_square(c, 1)
+        cap_line(c, 1)
+        cap_arms(p, BOTH)
+        quant_silu(p)
+        split(p, 0, BOTH)
+        inner_arm(c, 0)
+        split(p, 1, BOTH)
+        outer_arms(c, EVEN)
+        finish(p - 1)
+        cap_rest(p, BOTH)
+        caps(c, EVEN)
+        quant_family(p, 0)
+        cap_arms(c, EVEN)
+        quant_family(p, 1)
+        for mt in range(2):
+            m2(p, mt, (0, 1), True, True)
+        split(c, 0, EVEN)
+        inner_arm(c, 1)
+        split(c, 1, EVEN)
+        outer_arms(c, ODD)
+        quant_silu(c)
+        cap_rest(c, EVEN)
+        caps(c, ODD)
+        quant_family(c, 0)
+        for mt in range(2):
+            m2(c, mt, (0,), True, False)
+        cap_arms(c, ODD)
+        finish(p)
+        split(c, 0, ODD)
+        split(c, 1, ODD)
+        cap_rest(c, ODD)
+        quant_family(c, 1)
+        for mt in range(2):
+            m2(c, mt, (1,), False, True)
+        finish(c)

@@ -61,6 +61,11 @@ def tile_refiner_pa_kernel(tc, X, Y, Wx, bx, Wy, by, base_w, spline_w, spline_sc
         for i, v in enumerate(bias_vals):
             nc.scalar.activation(out=cb[:, i : i + 1], in_=ones[:, 0:1], func=ACTF.Copy, scale=v)
 
+        def keep_warm(n):
+            pw = bank("pw", BF16)
+            for k in range(n):
+                nc.tensor.transpose(pw[:, 0:P], ident_b[:], ident_b[:])
+
         def cbias(i):
             return cb[:, i : i + 1]
 
@@ -75,22 +80,25 @@ def tile_refiner_pa_kernel(tc, X, Y, Wx, bx, Wy, by, base_w, spline_w, spline_sc
         def raw_tile(nm):
             return prep.tile([P, 4096], BF16, name=nm, tag="raw", bufs=5, align_bytes=64)
 
-        def load_w(w, nm):
-            wr = raw_tile(nm)
-            for jj in range(2):
+        def load_w(sg, parts):
+            w = (Wx, Wy)[sg]
+            if w_raw[sg] is None:
+                w_raw[sg] = raw_tile("wr%d" % sg)
+            wr = w_raw[sg]
+            for jj in parts:
                 nc.sync.dma_start(
                     out=wr[:, 2048 * jj : 2048 * jj + 2048].rearrange("p (j k) -> p j k", j=2),
                     in_=w[256 * jj : 256 * jj + 256, :].rearrange("(j p) k -> p j k", p=P),
                 )
-            return wr
 
-        def load_x(sg, b):
-            xr = prep.tile([P, 4096], BF16, name="xr%d%d" % (sg, b), tag="xr", bufs=2)
+        def load_x(sg, b, lo=0, hi=16):
+            if lo == 0:
+                x_raw[(sg, b)] = prep.tile([P, 4096], BF16, name="xr%d%d" % (sg, b), tag="xr", bufs=2)
+            xr = x_raw[(sg, b)]
             src = (X, Y)[sg][b].rearrange("(a c) n f -> c a (n f)", c=16)
-            for cl in range(4):
-                for s in range(4):
-                    nc.sync.dma_start(out=xr[32 * cl + s : 32 * cl + 32 : 4, :], in_=src[4 * cl + s])
-            x_raw[(sg, b)] = xr
+            for k in range(lo, hi):
+                p0 = 32 * (k // 4) + k % 4
+                nc.sync.dma_start(out=xr[p0 : p0 + 32 - k % 4 : 4, :], in_=src[k])
 
         def load_sw():
             swr = raw_tile("swr")
@@ -220,7 +228,7 @@ def tile_refiner_pa_kernel(tc, X, Y, Wx, bx, Wy, by, base_w, spline_w, spline_sc
 
         def x_copy(c, copier):
             b, h, sg = where(c)
-            xg = work.tile([P, 2048], BF16, name="xg", bufs=1, align_bytes=64)
+            xg = work.tile([P, 2048], BF16, name="xg", bufs=2, align_bytes=64)
             st[c]["xg"] = xg
             copier(
                 out=xg[:].bitcast(F32).rearrange("p (h n w) -> p h n w", h=2, w=2),
@@ -443,17 +451,18 @@ def tile_refiner_pa_kernel(tc, X, Y, Wx, bx, Wy, by, base_w, spline_w, spline_sc
 
         V, S = nc.vector.tensor_copy, nc.scalar.copy
         BOTH, EVEN, ODD = slice(0, 2), slice(0, 1), slice(1, 2)
-        w_raw[0] = load_w(Wx, "wxr")
-        load_x(0, 0)
+        load_w(0, (0, 1))
+        load_x(0, 0, 0, 16)
         nc.sync.dma_start(out=brow[0:4, :], in_=bx.rearrange("(r c) -> r c", c=P))
         nc.sync.dma_start(out=brow[4:8, :], in_=by.rearrange("(r c) -> r c", c=P))
-        w_raw[1] = load_w(Wy, "wyr")
+        load_w(1, (0, 1))
         sw_raw = load_sw()
         load_small()
         load_x(1, 0)
 
         for j in range(4):
             w_regroup(0, j, S if j % 2 else V)
+        keep_warm(18)
         for j in range(4):
             w_transpose(0, j)
         pb0 = bank("pb0", BF16)
@@ -464,14 +473,15 @@ def tile_refiner_pa_kernel(tc, X, Y, Wx, bx, Wy, by, base_w, spline_w, spline_sc
         w_evac(0, 2, S)
         w_quant(0, 0, 2)
         w_evac(0, 3, V)
-        nc.vector.tensor_copy(out=bias[:], in_=pb0[:, 0:8])
         w_quant(0, 2, 4)
         x_copy(0, V)
+        nc.vector.tensor_copy(out=bias[:], in_=pb0[:, 0:8])
+        x_copy(2, S)
+        x_quant(0)
         for j in range(4):
             w_regroup(1, j, S if j < 3 else V)
-        x_quant(0)
+        keep_warm(28)
         m1(0)
-        x_copy(2, V)
         for j in range(2):
             w_transpose(1, j)
         tanh(0)

@@ -203,14 +203,13 @@ def tile_refiner_pa_kernel(tc, X, Y, Wx, bx, Wy, by, base_w, spline_w, spline_sc
         def sw_products(kk):
             if kk == 0:
                 sw_state["swt"] = grp_tile("swt", 4096, BF16)
-            pairs = sw_state[kk][:].bitcast(BF16).rearrange("p (j q e) -> p e q j", j=4, e=2)
-            for e in range(2):
-                k = 2 * kk + e
-                plane = 4 * (k % 2) + KFAM[k % 2].index(k)
-                nc.vector.tensor_tensor(
-                    out=sw_state["swt"][:, 512 * plane : 512 * plane + 512].rearrange("p (q j) -> p q j", j=4),
-                    in0=pairs[:, e], in1=sct[:].rearrange("p (q j) -> p q j", j=4), op=ALU.mult,
-                )
+            first = KFAM[0].index(2 * kk)
+            second = 4 + KFAM[1].index(2 * kk + 1)
+            nc.vector.tensor_tensor(
+                out=sw_state["swt"][:].rearrange("p (a q j) -> p a q j", a=8, j=4)[:, first : second + 1 : second - first],
+                in0=sw_state[kk][:].bitcast(BF16).rearrange("p (j q e) -> p e q j", j=4, e=2),
+                in1=sct[:].rearrange("p (q j) -> p q j", j=4).unsqueeze(1).to_broadcast([P, 2, P, 4]), op=ALU.mult,
+            )
 
         def sw_quant():
             nc.vector.quantize_mx(out=swc[:, 0:1024].bitcast(FP8X4), scales=sws[:, 0:1024], in_=sw_state["swt"][:])
@@ -319,11 +318,11 @@ def tile_refiner_pa_kernel(tc, X, Y, Wx, bx, Wy, by, base_w, spline_w, spline_sc
             for s, o in halves(c, "x", t[:, f, :]):
                 act(o, s, ACTF.Abs, 2.5, (B_M05, B_P05)[f])
 
-        def fold(c, dst, src, bi):
-            t = work.tile([P, CW], F32, name=dst, tag="fold", bufs=2)
-            st[c][dst] = t
-            s = st[c]["fa"][:, 0, :] if src == "fa" else st[c][src][:]
-            act(t[:], s, ACTF.Abs, 1.0, bi)
+        def folds(c):
+            t = work.tile([P, CW], F32, name="vb", bufs=1)
+            act(t[:], st[c]["fa"][:, 0, :], ACTF.Abs, 1.0, B_M2)
+            act(t[:], t[:], ACTF.Abs, 1.0, B_M1)
+            st[c]["vb"] = t
 
         def squares(c, nm, scale, bi, fs):
             act(pair(c, nm, "sq", 4)[:, fs], st[c]["fa"][:, fs], ACTF.Square, scale, bi)
@@ -395,17 +394,18 @@ def tile_refiner_pa_kernel(tc, X, Y, Wx, bx, Wy, by, base_w, spline_w, spline_sc
             )
 
         def silu(c):
-            sil = work.tile([P, CW], BF16, name="sil", bufs=2, align_bytes=64)
-            for s, o in halves(c, "x", sil[:]):
+            if c % 2 == 0:
+                st[c]["sil"] = work.tile([P, 2, CW], BF16, name="sil", bufs=2, align_bytes=64)
+            sil = st[c - c % 2]["sil"]
+            for s, o in halves(c, "x", sil[:, c % 2, :]):
                 nc.scalar.activation(out=o, in_=s, func=ACTF.Silu)
-            st[c]["sil"] = sil
 
         def quant_silu(c):
-            bc = work.tile([P, MC], U32, name="bc", bufs=2, align_bytes=64)
-            bs = work.tile([P, MC], U8, name="bs", bufs=2, align_bytes=64)
-            nc.vector.quantize_mx(out=bc[:].bitcast(FP8X4), scales=bs[:], in_=st[c]["sil"][:])
-            st[c]["bc"] = bc
-            st[c]["bs"] = bs
+            bc = work.tile([P, 2 * MC], U32, name="bc", bufs=1, align_bytes=64)
+            bs = work.tile([P, 2 * MC], U8, name="bs", bufs=1, align_bytes=64)
+            nc.vector.quantize_mx(out=bc[:].bitcast(FP8X4), scales=bs[:], in_=st[c]["sil"][:].rearrange("p k w -> p (k w)"))
+            for k in range(2):
+                st[c + k]["bc"], st[c + k]["bs"] = bc[:, MC * k : MC * k + MC], bs[:, MC * k : MC * k + MC]
 
         def m2(c, mt, fams, first, last):
             if first:
@@ -436,7 +436,7 @@ def tile_refiner_pa_kernel(tc, X, Y, Wx, bx, Wy, by, base_w, spline_w, spline_sc
             rows = out[b, MC * h : MC * h + MC, :].rearrange("(mt p) o -> p mt o", p=P)
             if sg == 0:
                 ob = work.tile([P, 2, 64], F32, name="ob", bufs=2)
-                nc.vector.tensor_copy(out=ob[:], in_=acc[c][:, 0 : 2 * P].rearrange("p (mt q) -> p mt q", mt=2)[:, :, cols])
+                nc.scalar.copy(out=ob[:], in_=acc[c][:, 0 : 2 * P].rearrange("p (mt q) -> p mt q", mt=2)[:, :, cols])
                 obx[c] = ob
             elif c < NCH - 1:
                 res = work.tile([P, 2, 64], F32, name="res", bufs=2)
@@ -520,8 +520,7 @@ def tile_refiner_pa_kernel(tc, X, Y, Wx, bx, Wy, by, base_w, spline_w, spline_sc
         m1(2)
         load_x(0, 1)
         bw_quant()
-        fold(0, "g2", "fa", B_M2)
-        fold(0, "vb", "g2", B_M1)
+        folds(0)
         outer_arms(0, BOTH)
         x_copy(3, V)
         sw_quant()
@@ -532,87 +531,59 @@ def tile_refiner_pa_kernel(tc, X, Y, Wx, bx, Wy, by, base_w, spline_w, spline_sc
         load_x(1, 1)
         caps(0, BOTH)
 
-        for c in range(1, NCH - 1):
+        for c in range(1, NCH):
             p = c - 1
-            nxt = c + 3 < NCH
-            weave(c + 1)
+            if c % 2 and c > 2:
+                finish(c - 3)
+            if c + 1 < NCH:
+                weave(c + 1)
             dist(c, 0)
             dist(c, 1)
             silu(c)
             squares(c, "sl", rc, None, BOTH)
             squares(c, "sp", r6, B_M2R6, BOTH)
             cap_arms(p, BOTH)
-            quant_silu(p)
             if c + 2 < NCH:
                 x_quant(c + 2)
                 m1(c + 2)
+            else:
+                inner_arm(c, 0)
             split(p, 0, BOTH)
-            fold(c, "g2", "fa", B_M2)
-            fold(c, "vb", "g2", B_M1)
+            folds(c)
             split(p, 1, BOTH)
-            inner_arm(c, 0)
+            if c + 2 < NCH:
+                inner_arm(c, 0)
             inner_arm(c, 1)
             for f in range(2):
                 cap_square(c, f)
                 cap_line(c, f)
-            if nxt:
-                x_copy(c + 3, S if c > 3 else V)
+            if c + 3 < NCH:
+                x_copy(c + 3, V)
             if c + 2 < NCH:
                 tanh(c + 2)
-            if p > 0:
+            if p > 0 and p % 2 == 0:
                 finish(p - 1)
             cap_rest(p, BOTH)
             outer_arms(c, BOTH)
+            if c % 2:
+                quant_silu(p)
             quant_family(p, 0)
             caps(c, BOTH)
             quant_family(p, 1)
             for mt in range(2):
                 m2(p, mt, (0, 1), True, True)
 
-        p, c = NCH - 2, NCH - 1
-        dist(c, 0)
-        dist(c, 1)
-        silu(c)
-        squares(c, "sl", rc, None, EVEN)
-        squares(c, "sp", r6, B_M2R6, EVEN)
-        fold(c, "g2", "fa", B_M2)
-        fold(c, "vb", "g2", B_M1)
-        cap_square(c, 0)
-        cap_line(c, 0)
-        squares(c, "sl", rc, None, ODD)
-        squares(c, "sp", r6, B_M2R6, ODD)
-        cap_square(c, 1)
-        cap_line(c, 1)
-        cap_arms(p, BOTH)
-        quant_silu(p)
-        split(p, 0, BOTH)
-        inner_arm(c, 0)
-        split(p, 1, BOTH)
-        outer_arms(c, EVEN)
+        p = NCH - 1
         finish(p - 1)
-        cap_rest(p, BOTH)
-        caps(c, EVEN)
+        cap_arms(p, BOTH)
+        split(p, 0, BOTH)
+        split(p, 1, BOTH)
+        cap_rest(p, EVEN)
+        cap_rest(p, ODD)
         quant_family(p, 0)
-        cap_arms(c, EVEN)
+        for mt in range(2):
+            m2(p, mt, (0,), True, False)
         quant_family(p, 1)
         for mt in range(2):
-            m2(p, mt, (0, 1), True, True)
-        split(c, 0, EVEN)
-        inner_arm(c, 1)
-        split(c, 1, EVEN)
-        outer_arms(c, ODD)
-        quant_silu(c)
-        cap_rest(c, EVEN)
-        caps(c, ODD)
-        quant_family(c, 0)
-        for mt in range(2):
-            m2(c, mt, (0,), True, False)
-        cap_arms(c, ODD)
+            m2(p, mt, (1,), False, True)
         finish(p)
-        split(c, 0, ODD)
-        split(c, 1, ODD)
-        cap_rest(c, ODD)
-        quant_family(c, 1)
-        for mt in range(2):
-            m2(c, mt, (1,), False, True)
-        finish(c)

@@ -122,9 +122,9 @@ def tile_refiner_pa_kernel(tc, X, Y, Wx, bx, Wy, by, base_w, spline_w, spline_sc
         def w_regroup(sg, j, copier):
             if w_grp[sg] is None:
                 w_grp[sg] = grp_tile("wg%d" % sg, 2048, F32)
-            wrw = w_raw[sg][:].bitcast(F32).rearrange("p (j a c s f) -> p j f c a s", j=4, a=8, c=4, s=4, f=4)
+            wrw = w_raw[sg][:].bitcast(F32).rearrange("p (j a c s f) -> p j c a s f", j=4, a=8, c=4, s=4, f=4)
             copier(
-                out=w_grp[sg][:, 512 * j : 512 * j + 512].rearrange("p (f c a s) -> p f c a s", f=4, c=4, a=8, s=4),
+                out=w_grp[sg][:, 512 * j : 512 * j + 512].rearrange("p (f c a s) -> p c a s f", f=4, c=4, a=8, s=4),
                 in_=wrw[:, j],
             )
 
@@ -186,11 +186,11 @@ def tile_refiner_pa_kernel(tc, X, Y, Wx, bx, Wy, by, base_w, spline_w, spline_sc
 
         def sw_regroup(swr, copier):
             swg = grp_tile("swg", 2048, F32)
-            o = swg[:].rearrange("p (k g e r) -> p e k g r", k=4, e=2, r=4)
-            s = swr[:].bitcast(F32).rearrange("p (g e r k) -> p e k g r", e=2, r=4, k=4)
+            o = swg[:].rearrange("p (k g e r) -> p e g r k", k=4, e=2, r=4)
+            s = swr[:].bitcast(F32).rearrange("p (g e r k) -> p e g r k", e=2, r=4, k=4)
             copier(out=o[:, 0], in_=s[:, 0])
-            copier(out=o[:, 1, 0:2], in_=s[:, 1, 2:4])
-            copier(out=o[:, 1, 2:4], in_=s[:, 1, 0:2])
+            copier(out=o[:, 1, :, :, 0:2], in_=s[:, 1, :, :, 2:4])
+            copier(out=o[:, 1, :, :, 2:4], in_=s[:, 1, :, :, 0:2])
             sw_state["swg"] = swg
 
         def sw_transpose(kk):
@@ -230,8 +230,8 @@ def tile_refiner_pa_kernel(tc, X, Y, Wx, bx, Wy, by, base_w, spline_w, spline_sc
             xg = work.tile([P, 2048], BF16, name="xg", bufs=2, align_bytes=64)
             st[c]["xg"] = xg
             copier(
-                out=xg[:].bitcast(F32).rearrange("p (h n w) -> p h n w", h=2, w=2),
-                in_=x_raw[(sg, b)][:].bitcast(F32).rearrange("p (n h w) -> p h n w", h=2, w=2)[:, :, MC * h : MC * h + MC, :],
+                out=xg[:].bitcast(F32).rearrange("p (h n w) -> p n h w", h=2, w=2),
+                in_=x_raw[(sg, b)][:].bitcast(F32).rearrange("p (n h w) -> p n h w", h=2, w=2)[:, MC * h : MC * h + MC],
             )
 
         def x_quant(c):
@@ -491,7 +491,7 @@ def tile_refiner_pa_kernel(tc, X, Y, Wx, bx, Wy, by, base_w, spline_w, spline_sc
         sw_regroup(sw_raw, V)
         weave_first(0)
         sw_transpose(0)
-        w_evac(1, 1, V)
+        w_evac(1, 1, S)
         sw_small_evac()
         dist(0, 0)
         dist(0, 1)
@@ -500,8 +500,8 @@ def tile_refiner_pa_kernel(tc, X, Y, Wx, bx, Wy, by, base_w, spline_w, spline_sc
             w_transpose(1, j)
         sw_products(0)
         sw_products(1)
-        w_evac(1, 2, V)
-        w_evac(1, 3, V)
+        w_evac(1, 2, S)
+        w_evac(1, 3, S)
         sw_transpose(2)
         squares(0, "sl", rc, None, BOTH)
         silu(0)
@@ -546,13 +546,10 @@ def tile_refiner_pa_kernel(tc, X, Y, Wx, bx, Wy, by, base_w, spline_w, spline_sc
             if c + 2 < NCH:
                 x_quant(c + 2)
                 m1(c + 2)
-            else:
-                inner_arm(c, 0)
             split(p, 0, BOTH)
             folds(c)
             split(p, 1, BOTH)
-            if c + 2 < NCH:
-                inner_arm(c, 0)
+            inner_arm(c, 0)
             inner_arm(c, 1)
             for f in range(2):
                 cap_square(c, f)

@@ -51,6 +51,10 @@ def tile_refiner_pa_kernel(tc, X, Y, Wx, bx, Wy, by, base_w, spline_w, spline_sc
         make_identity(nc, ident_f[:])
         ident_b = keep.tile([P, P], BF16, name="ident_b")
         make_identity(nc, ident_b[:])
+        perm = keep.tile([P, P], BF16, name="perm")
+        nc.vector.tensor_copy(
+            out=perm[:].rearrange("p (c a s) -> p c a s", c=4, a=8), in_=ident_b[:].rearrange("p (a c s) -> p c a s", a=8, c=4)
+        )
         ones = keep.tile([P, 8], F32, name="ones")
         nc.vector.memset(ones[:], 1.0)
         brow = keep.tile([P, P], BF16, name="brow")
@@ -78,27 +82,31 @@ def tile_refiner_pa_kernel(tc, X, Y, Wx, bx, Wy, by, base_w, spline_w, spline_sc
         nc.vector.tensor_scalar(out=sgn[:, 1:2], in0=low[:], scalar1=-2.0, scalar2=1.0, op0=ALU.mult, op1=ALU.add)
 
         def raw_tile(nm):
-            return prep.tile([P, 4096], BF16, name=nm, tag="raw", bufs=5, align_bytes=64)
+            return prep.tile([P, 4096], BF16, name=nm, tag="raw", bufs=4, align_bytes=64)
 
         def load_w(sg, parts):
             w = (Wx, Wy)[sg]
             if w_raw[sg] is None:
                 w_raw[sg] = raw_tile("wr%d" % sg)
             wr = w_raw[sg]
-            for jj in parts:
-                nc.sync.dma_start(
-                    out=wr[:, 2048 * jj : 2048 * jj + 2048].rearrange("p (j k) -> p j k", j=2),
-                    in_=w[256 * jj : 256 * jj + 256, :].rearrange("(j p) k -> p j k", p=P),
-                )
+            for j in parts:
+                nc.sync.dma_start(out=wr[:, 1024 * j : 1024 * j + 1024], in_=w[P * j : P * j + P, :])
 
-        def load_x(sg, b, lo=0, hi=16):
-            if lo == 0:
-                x_raw[(sg, b)] = prep.tile([P, 4096], BF16, name="xr%d%d" % (sg, b), tag="xr", bufs=2)
-            xr = x_raw[(sg, b)]
+        def load_x_first():
+            xn = prep.tile([P, 8 * MC], BF16, name="xn", tag="half", bufs=2)
+            nc.sync.dma_start(out=xn[:], in_=X[0][:, 0:MC].rearrange("t n f -> t (n f)"))
+            return xn
+
+        def load_x(sg, b, n0=0):
+            if n0:
+                xr = prep.tile([P, 8 * (512 - n0)], BF16, name="xb", tag="half", bufs=2)
+            else:
+                xr = prep.tile([P, 4096], BF16, name="xr%d%d" % (sg, b), tag="xr", bufs=2)
             src = (X, Y)[sg][b].rearrange("(a c) n f -> c a (n f)", c=16)
-            for k in range(lo, hi):
+            for k in range(16):
                 p0 = 32 * (k // 4) + k % 4
-                nc.sync.dma_start(out=xr[p0 : p0 + 32 - k % 4 : 4, :], in_=src[k])
+                nc.sync.dma_start(out=xr[p0 : 32 * (k // 4) + 32 : 4, :], in_=src[k][:, 8 * n0 : 4096])
+            x_raw[(sg, b)] = xr, n0
 
         def load_sw():
             swr = raw_tile("swr")
@@ -117,7 +125,7 @@ def tile_refiner_pa_kernel(tc, X, Y, Wx, bx, Wy, by, base_w, spline_w, spline_sc
         w_scales = [None, None]
 
         def grp_tile(nm, cols, dt):
-            return prep.tile([P, cols], dt, name=nm, tag="raw", bufs=5, align_bytes=64)
+            return prep.tile([P, cols], dt, name=nm, tag="raw", bufs=4, align_bytes=64)
 
         def w_regroup(sg, j, copier):
             if w_grp[sg] is None:
@@ -227,12 +235,29 @@ def tile_refiner_pa_kernel(tc, X, Y, Wx, bx, Wy, by, base_w, spline_w, spline_sc
 
         def x_copy(c, copier):
             b, h, sg = where(c)
+            xr, n0 = x_raw[(sg, b)]
             xg = work.tile([P, 2048], BF16, name="xg", bufs=2, align_bytes=64)
             st[c]["xg"] = xg
             copier(
                 out=xg[:].bitcast(F32).rearrange("p (h n w) -> p n h w", h=2, w=2),
-                in_=x_raw[(sg, b)][:].bitcast(F32).rearrange("p (n h w) -> p n h w", h=2, w=2)[:, MC * h : MC * h + MC],
+                in_=xr[:].bitcast(F32).rearrange("p (n h w) -> p n h w", h=2, w=2)[:, MC * h - n0 : MC * h - n0 + MC],
             )
+
+        def x_permute(xn):
+            st[0]["xp"] = []
+            for h in range(2):
+                xp = psum.tile([P, 1024], BF16, name="xp", tag="s1", bufs=6)
+                for k in range(2):
+                    nc.tensor.matmul(
+                        out=xp[:, 512 * k : 512 * k + 512], lhsT=perm[:],
+                        rhs=xn[:].rearrange("p (k n h f) -> p k h n f", k=2, h=2, f=4)[:, k, h], start=True, stop=True,
+                    )
+                st[0]["xp"].append(xp)
+
+        def x_evac(h, copier):
+            if h == 0:
+                st[0]["xg"] = work.tile([P, 2048], BF16, name="xg", bufs=2, align_bytes=64)
+            copier(out=st[0]["xg"][:, 1024 * h : 1024 * h + 1024], in_=st[0]["xp"][h][:])
 
         def x_quant(c):
             xg = st[c]["xg"]
@@ -451,20 +476,22 @@ def tile_refiner_pa_kernel(tc, X, Y, Wx, bx, Wy, by, base_w, spline_w, spline_sc
 
         V, S = nc.vector.tensor_copy, nc.scalar.copy
         BOTH, EVEN, ODD = slice(0, 2), slice(0, 1), slice(1, 2)
-        load_w(0, (0, 1))
-        load_x(0, 0, 0, 16)
+        load_w(0, (0, 1, 2, 3))
+        xn = load_x_first()
         nc.sync.dma_start(out=brow[0:4, :], in_=bx.rearrange("(r c) -> r c", c=P))
         nc.sync.dma_start(out=brow[4:8, :], in_=by.rearrange("(r c) -> r c", c=P))
-        load_w(1, (0, 1))
+        load_w(1, (0, 1, 2, 3))
         sw_raw = load_sw()
         load_small()
         load_x(1, 0)
+        load_x(0, 0, MC)
 
         for j in range(4):
             w_regroup(0, j, S if j % 2 else V)
         keep_warm(18)
         for j in range(4):
             w_transpose(0, j)
+        x_permute(xn)
         pb0 = bank("pb0", BF16)
         nc.tensor.transpose(pb0[:, 0:P], brow[:], ident_b[:])
         bias = keep.tile([P, 8], F32, name="bias")
@@ -473,21 +500,19 @@ def tile_refiner_pa_kernel(tc, X, Y, Wx, bx, Wy, by, base_w, spline_w, spline_sc
         w_evac(0, 2, S)
         w_quant(0, 0, 2)
         w_evac(0, 3, V)
+        x_evac(0, S)
+        x_evac(1, V)
         w_quant(0, 2, 4)
-        x_copy(0, V)
-        nc.vector.tensor_copy(out=bias[:], in_=pb0[:, 0:8])
-        x_copy(2, S)
         x_quant(0)
-        for j in range(4):
-            w_regroup(1, j, S if j < 3 else V)
-        keep_warm(28)
+        nc.vector.tensor_copy(out=bias[:], in_=pb0[:, 0:8])
         m1(0)
+        for j in range(4):
+            w_regroup(1, j, S if j < 2 else V)
+        tanh(0)
         for j in range(2):
             w_transpose(1, j)
-        tanh(0)
         w_evac(1, 0, S)
         sw_small()
-        x_quant(2)
         sw_regroup(sw_raw, V)
         weave_first(0)
         sw_transpose(0)
@@ -505,29 +530,30 @@ def tile_refiner_pa_kernel(tc, X, Y, Wx, bx, Wy, by, base_w, spline_w, spline_sc
         sw_transpose(2)
         squares(0, "sl", rc, None, BOTH)
         silu(0)
-        x_copy(1, V)
+        sw_transpose(3)
         w_quant(1, 0, 4)
+        sw_products(2)
+        x_copy(1, V)
+        sw_products(3)
         x_quant(1)
         m1(1)
-        sw_transpose(3)
         squares(0, "sp", r6, B_M2R6, BOTH)
         inner_arm(0, 0)
         tanh(1)
         weave(1)
         inner_arm(0, 1)
-        sw_products(2)
-        sw_products(3)
-        m1(2)
         load_x(0, 1)
         bw_quant()
         folds(0)
         outer_arms(0, BOTH)
-        x_copy(3, V)
+        x_copy(2, V)
         sw_quant()
+        x_quant(2)
+        m1(2)
         for f in range(2):
             cap_line_v(0, f)
             cap_square(0, f)
-        tanh(2)
+        x_copy(3, V)
         load_x(1, 1)
         caps(0, BOTH)
 
@@ -535,12 +561,15 @@ def tile_refiner_pa_kernel(tc, X, Y, Wx, bx, Wy, by, base_w, spline_w, spline_sc
             p = c - 1
             if c % 2 and c > 2:
                 finish(c - 3)
-            if c + 1 < NCH:
+            if 1 < c < NCH - 1:
                 weave(c + 1)
             dist(c, 0)
             dist(c, 1)
             silu(c)
             squares(c, "sl", rc, None, BOTH)
+            if c == 1:
+                tanh(2)
+                weave(2)
             squares(c, "sp", r6, B_M2R6, BOTH)
             cap_arms(p, BOTH)
             if c + 2 < NCH:

@@ -355,18 +355,17 @@ def tile_refiner_pa_kernel(tc, X, Y, Wx, bx, Wy, by, base_w, spline_w, spline_sc
         def cap_square(c, f):
             act(pair(c, "q", "sq", 4)[:, f, :], st[c]["vb"][:], ACTF.Square, (-1.0, 1.0)[f], (B_1HB, B_HB)[f])
 
-        def cap_line(c, f):
-            act(pair(c, "l", "lin", 2)[:, f, :], st[c]["vb"][:], ACTF.Identity, (0.5, -0.5)[f], (B_L2, B_L1)[f])
-
-        def cap_line_v(c, f):
-            nc.vector.tensor_scalar(
-                out=pair(c, "l", "lin", 2)[:, f, :], in0=st[c]["vb"][:], scalar1=(0.5, -0.5)[f],
+        def cap_line(c, f, engine):
+            if "l" not in st[c]:
+                st[c]["l"] = work.tile([P, 2, CW], F32, name="l", tag="arms", bufs=3, align_bytes=64)
+            engine.tensor_scalar(
+                out=st[c]["l"][:, f, :], in0=st[c]["vb"][:], scalar1=(0.5, -0.5)[f],
                 scalar2=((a0 - 1.0) / 2.0, a0 / 2.0)[f], op0=ALU.mult, op1=ALU.add,
             )
 
         def arms(c):
             if "arms" not in st[c]:
-                st[c]["arms"] = work.tile([P, 2, 2, CW], BF16, name="arms", align_bytes=64)
+                st[c]["arms"] = work.tile([P, 2, 2, CW], BF16, name="arms", tag="arms", bufs=3, align_bytes=64)
             return st[c]["arms"]
 
         def outer_arms(c, fs):
@@ -551,7 +550,7 @@ def tile_refiner_pa_kernel(tc, X, Y, Wx, bx, Wy, by, base_w, spline_w, spline_sc
         x_quant(2)
         m1(2)
         for f in range(2):
-            cap_line_v(0, f)
+            cap_line(0, f, nc.vector)
             cap_square(0, f)
         x_copy(3, V)
         load_x(1, 1)
@@ -582,7 +581,7 @@ def tile_refiner_pa_kernel(tc, X, Y, Wx, bx, Wy, by, base_w, spline_w, spline_sc
             inner_arm(c, 1)
             for f in range(2):
                 cap_square(c, f)
-                cap_line(c, f)
+                cap_line(c, f, nc.gpsimd)
             if c + 3 < NCH:
                 x_copy(c + 3, V)
             if c + 2 < NCH:

@@ -34,8 +34,8 @@ def tile_refiner_pa_kernel(tc, X, Y, Wx, bx, Wy, by, base_w, spline_w, spline_sc
     a0, hb, cp = central_constants()
     r6 = 1.0 / math.sqrt(6.0)
     rc = math.sqrt(2.5 / 6.0)
-    bias_vals = (-0.5, 0.5, -2.0, -1.0, -2.0 * r6, hb, 1.0 + hb, a0 / 2.0, (a0 - 1.0) / 2.0)
-    (B_M05, B_P05, B_M2, B_M1, B_M2R6, B_HB, B_1HB, B_L1, B_L2) = range(9)
+    bias_vals = (-0.5, 0.5, -2.0, -1.0, -2.0 * r6, hb, 1.0 + hb)
+    (B_M05, B_P05, B_M2, B_M1, B_M2R6, B_HB, B_1HB) = range(7)
 
     with ExitStack() as ctx:
         keep = ctx.enter_context(tc.tile_pool(name="keep", bufs=1))
@@ -64,6 +64,10 @@ def tile_refiner_pa_kernel(tc, X, Y, Wx, bx, Wy, by, base_w, spline_w, spline_sc
         nc.scalar.activation(out=warm[:, 0:1], in_=ones[:, 0:1], func=ACTF.Silu)
         for i, v in enumerate(bias_vals):
             nc.scalar.activation(out=cb[:, i : i + 1], in_=ones[:, 0:1], func=ACTF.Copy, scale=v)
+
+        lines = keep.tile([P, 4], F32, name="lines")
+        for i, v in enumerate((0.5, -0.5, (a0 - 1.0) / 2.0, a0 / 2.0)):
+            nc.scalar.activation(out=lines[:, i : i + 1], in_=ones[:, 0:1], func=ACTF.Copy, scale=v)
 
         def keep_warm(n):
             pw = bank("pw", BF16)
@@ -343,11 +347,11 @@ def tile_refiner_pa_kernel(tc, X, Y, Wx, bx, Wy, by, base_w, spline_w, spline_sc
             for s, o in halves(c, "x", t[:, f, :]):
                 act(o, s, ACTF.Abs, 2.5, (B_M05, B_P05)[f])
 
-        def folds(c):
-            t = work.tile([P, CW], F32, name="vb", bufs=1)
-            act(t[:], st[c]["fa"][:, 0, :], ACTF.Abs, 1.0, B_M2)
-            act(t[:], t[:], ACTF.Abs, 1.0, B_M1)
-            st[c]["vb"] = t
+        def fold(c, k):
+            if k == 0:
+                st[c]["vb"] = work.tile([P, CW], F32, name="vb", bufs=1)
+            t = st[c]["vb"]
+            act(t[:], st[c]["fa"][:, 0, :] if k == 0 else t[:], ACTF.Abs, 1.0, (B_M2, B_M1)[k])
 
         def squares(c, nm, scale, bi, fs):
             act(pair(c, nm, "sq", 4)[:, fs], st[c]["fa"][:, fs], ACTF.Square, scale, bi)
@@ -355,17 +359,20 @@ def tile_refiner_pa_kernel(tc, X, Y, Wx, bx, Wy, by, base_w, spline_w, spline_sc
         def cap_square(c, f):
             act(pair(c, "q", "sq", 4)[:, f, :], st[c]["vb"][:], ACTF.Square, (-1.0, 1.0)[f], (B_1HB, B_HB)[f])
 
-        def cap_line(c, f, engine):
-            if "l" not in st[c]:
-                st[c]["l"] = work.tile([P, 2, CW], F32, name="l", tag="arms", bufs=3, align_bytes=64)
+        def let_gpsimd():
+            go = work.tile([P, 4], F32, name="go", bufs=2)
+            nc.vector.tensor_copy(out=go[:], in_=lines[:])
+            return go
+
+        def cap_line(c, f, engine, consts):
             engine.tensor_scalar(
-                out=st[c]["l"][:, f, :], in0=st[c]["vb"][:], scalar1=(0.5, -0.5)[f],
-                scalar2=((a0 - 1.0) / 2.0, a0 / 2.0)[f], op0=ALU.mult, op1=ALU.add,
+                out=pair(c, "l", "lin", 2)[:, f, :], in0=st[c]["vb"][:], scalar1=consts[:, f : f + 1],
+                scalar2=consts[:, 2 + f : 3 + f], op0=ALU.mult, op1=ALU.add,
             )
 
         def arms(c):
             if "arms" not in st[c]:
-                st[c]["arms"] = work.tile([P, 2, 2, CW], BF16, name="arms", tag="arms", bufs=3, align_bytes=64)
+                st[c]["arms"] = work.tile([P, 2, 2, CW], BF16, name="arms", align_bytes=64)
             return st[c]["arms"]
 
         def outer_arms(c, fs):
@@ -543,14 +550,15 @@ def tile_refiner_pa_kernel(tc, X, Y, Wx, bx, Wy, by, base_w, spline_w, spline_sc
         inner_arm(0, 1)
         load_x(0, 1)
         bw_quant()
-        folds(0)
+        fold(0, 0)
+        fold(0, 1)
         outer_arms(0, BOTH)
         x_copy(2, V)
         sw_quant()
         x_quant(2)
         m1(2)
         for f in range(2):
-            cap_line(0, f, nc.vector)
+            cap_line(0, f, nc.vector, lines)
             cap_square(0, f)
         x_copy(3, V)
         load_x(1, 1)
@@ -564,8 +572,10 @@ def tile_refiner_pa_kernel(tc, X, Y, Wx, bx, Wy, by, base_w, spline_w, spline_sc
                 weave(c + 1)
             dist(c, 0)
             dist(c, 1)
-            silu(c)
+            fold(c, 0)
             squares(c, "sl", rc, None, BOTH)
+            fold(c, 1)
+            silu(c)
             if c == 1:
                 tanh(2)
                 weave(2)
@@ -575,15 +585,16 @@ def tile_refiner_pa_kernel(tc, X, Y, Wx, bx, Wy, by, base_w, spline_w, spline_sc
                 x_quant(c + 2)
                 m1(c + 2)
             split(p, 0, BOTH)
-            folds(c)
+            go = let_gpsimd()
             split(p, 1, BOTH)
+            for f in range(2):
+                cap_line(c, f, nc.gpsimd, go)
             inner_arm(c, 0)
             inner_arm(c, 1)
             for f in range(2):
                 cap_square(c, f)
-                cap_line(c, f, nc.gpsimd)
             if c + 3 < NCH:
-                x_copy(c + 3, V)
+                x_copy(c + 3, S)
             if c + 2 < NCH:
                 tanh(c + 2)
             if p > 0 and p % 2 == 0:

@@ -167,7 +167,7 @@ def tile_refiner_pa_kernel(tc, X, Y, Wx, bx, Wy, by, base_w, spline_w, spline_sc
 
         scr = prep.tile([P, 512], BF16, name="scr")
         bwr = prep.tile([P, 512], BF16, name="bwr")
-        sct = prep.tile([P, 512], BF16, name="sct")
+        sct = prep.tile([P, 3 * 512], BF16, name="sct")
         bwt = prep.tile([P, 512], BF16, name="bwt", align_bytes=64)
         swc = keep.tile([P, 9 * P], U32, name="swc", align_bytes=64)
         sws = keep.tile([P, 9 * P], U8, name="sws", align_bytes=64)
@@ -191,10 +191,12 @@ def tile_refiner_pa_kernel(tc, X, Y, Wx, bx, Wy, by, base_w, spline_w, spline_sc
         def sw_small_evac():
             psc, pbw = sw_state["psc"], sw_state["pbw"]
             nc.vector.tensor_scalar(
-                out=sct[:].rearrange("p (q j) -> p q j", j=4), in0=psc[:].rearrange("p (j q) -> p q j", j=4),
+                out=sct[:, 512:1024].rearrange("p (q j) -> p q j", j=4), in0=psc[:].rearrange("p (j q) -> p q j", j=4),
                 scalar1=-1.0, scalar2=None, op0=ALU.mult,
             )
             nc.vector.tensor_copy(out=bwt[:].rearrange("p (q j) -> p q j", j=4), in_=pbw[:].rearrange("p (j q) -> p q j", j=4))
+            for k in (0, 1024):
+                nc.vector.tensor_scalar(out=sct[:, k : k + 512], in0=sct[:, 512:1024], scalar1=-1.0, scalar2=None, op0=ALU.mult)
 
         def sw_regroup(swr, copier):
             swg = grp_tile("swg", 2048, F32)
@@ -220,7 +222,7 @@ def tile_refiner_pa_kernel(tc, X, Y, Wx, bx, Wy, by, base_w, spline_w, spline_sc
             nc.vector.tensor_tensor(
                 out=sw_state["swt"][:].rearrange("p (a q j) -> p a q j", a=8, j=4)[:, first : second + 1 : second - first],
                 in0=sw_state[kk][:].bitcast(BF16).rearrange("p (j q e) -> p e q j", j=4, e=2),
-                in1=sct[:].rearrange("p (q j) -> p q j", j=4).unsqueeze(1).to_broadcast([P, 2, P, 4]), op=ALU.mult,
+                in1=sct[:, 512 * (kk % 2) : 512 * (kk % 2) + 1024].rearrange("p (e q j) -> p e q j", e=2, j=4), op=ALU.mult,
             )
 
         def sw_quant():
@@ -306,9 +308,10 @@ def tile_refiner_pa_kernel(tc, X, Y, Wx, bx, Wy, by, base_w, spline_w, spline_sc
                 )
             st[c]["xj"] = x
 
-        def weave(c):
-            st[c]["x"] = []
-            for half in range(2):
+        def weave(c, parts=(0, 1)):
+            if parts[0] == 0:
+                st[c]["x"] = []
+            for half in parts:
                 xi = bank("xi", F32)
                 nc.tensor.matmul(
                     out=xi[:], lhsT=ident_f[:],
@@ -317,19 +320,8 @@ def tile_refiner_pa_kernel(tc, X, Y, Wx, bx, Wy, by, base_w, spline_w, spline_sc
                 )
                 st[c]["x"].append(xi)
 
-        def weave_first(c):
-            xi = work.tile([P, CW], F32, name="x", bufs=2)
-            nc.vector.tensor_copy(
-                out=xi[:].rearrange("p (c i j) -> p c j i", i=4, j=4),
-                in_=st[c]["xj"][:].rearrange("p (j c i) -> p c j i", i=4, j=4),
-            )
-            st[c]["x"] = xi
-
         def halves(c, src, dst):
-            t = st[c][src]
-            if src != "x" or c == 0:
-                return [(t[:], dst)]
-            return [(t[half][:], dst[:, 512 * half : 512 * half + 512]) for half in range(2)]
+            return [(st[c][src][half][:], dst[:, 512 * half : 512 * half + 512]) for half in range(2)]
 
         def pair(c, nm, tag, bufs):
             if nm not in st[c]:
@@ -342,10 +334,12 @@ def tile_refiner_pa_kernel(tc, X, Y, Wx, bx, Wy, by, base_w, spline_w, spline_sc
             else:
                 nc.scalar.activation(out=out_, in_=in_, func=func, bias=cbias(bi), scale=scale)
 
-        def dist(c, f):
+        def dist(c):
             t = pair(c, "fa", "fa", 2)
-            for s, o in halves(c, "x", t[:, f, :]):
-                act(o, s, ACTF.Abs, 2.5, (B_M05, B_P05)[f])
+            for half in range(2):
+                for f in range(2):
+                    s, o = halves(c, "x", t[:, f, :])[half]
+                    act(o, s, ACTF.Abs, 2.5, (B_M05, B_P05)[f])
 
         def fold(c, k):
             if k == 0:
@@ -370,6 +364,12 @@ def tile_refiner_pa_kernel(tc, X, Y, Wx, bx, Wy, by, base_w, spline_w, spline_sc
                 scalar2=consts[:, 2 + f : 3 + f], op0=ALU.mult, op1=ALU.add,
             )
 
+        def cap_line_s(c, f):
+            nc.scalar.activation(
+                out=pair(c, "l", "lin", 2)[:, f, :], in_=st[c]["vb"][:], func=ACTF.Identity,
+                bias=lines[:, 2 + f : 3 + f], scale=(0.5, -0.5)[f],
+            )
+
         def arms(c):
             if "arms" not in st[c]:
                 st[c]["arms"] = work.tile([P, 2, 2, CW], BF16, name="arms", align_bytes=64)
@@ -391,7 +391,7 @@ def tile_refiner_pa_kernel(tc, X, Y, Wx, bx, Wy, by, base_w, spline_w, spline_sc
 
         def caps(c, fs):
             if "cap" not in st[c]:
-                st[c]["cap"] = work.tile([P, 2, CW], BF16, name="cap", align_bytes=64)
+                st[c]["cap"] = work.tile([P, 2, CW], BF16, name="cap", bufs=1, align_bytes=64)
             nc.vector.scalar_tensor_tensor(
                 out=st[c]["cap"][:, fs], in0=st[c]["q"][:, fs], scalar=cp, in1=st[c]["l"][:, fs], op0=ALU.add, op1=ALU.mult
             )
@@ -400,12 +400,22 @@ def tile_refiner_pa_kernel(tc, X, Y, Wx, bx, Wy, by, base_w, spline_w, spline_sc
             o = arms(c)[:, 0, fs]
             nc.vector.tensor_tensor(out=o, in0=o, in1=st[c]["cap"][:, fs], op=ALU.max)
 
-        def split(c, side, fs):
+        def plane(c, fs, n):
             if "fam" not in st[c]:
                 st[c]["fam"] = work.tile([P, 2, 4, CW], BF16, name="fam", bufs=1, align_bytes=64)
+            return st[c]["fam"][:, fs, n, :]
+
+        def split_outer(c, side, fs, scalar=False):
+            o, i, sign = plane(c, fs, 2 * side), arms(c)[:, 0, fs], sgn[:, side : side + 1]
+            if scalar:
+                nc.scalar.activation(out=o, in_=i, func=ACTF.Relu, scale=sign)
+            else:
+                nc.vector.tensor_scalar(out=o, in0=i, scalar1=sign, scalar2=0.0, op0=ALU.mult, op1=ALU.max)
+
+        def split_inner(c, side, fs):
             nc.vector.tensor_scalar(
-                out=st[c]["fam"][:, fs, 2 * side : 2 * side + 2, :], in0=arms(c)[:].rearrange("p k f w -> p f k w")[:, fs],
-                scalar1=sgn[:, 1 - side : 2 - side], scalar2=0.0, op0=ALU.mult, op1=ALU.min,
+                out=plane(c, fs, 2 * side + 1), in0=arms(c)[:, 1, fs], scalar1=sgn[:, 1 - side : 2 - side], scalar2=0.0,
+                op0=ALU.mult, op1=ALU.min,
             )
 
         def cap_rest(c, fs):
@@ -414,15 +424,18 @@ def tile_refiner_pa_kernel(tc, X, Y, Wx, bx, Wy, by, base_w, spline_w, spline_sc
                 out=rest, in0=rest, in1=st[c]["cap"][:, fs].unsqueeze(2).to_broadcast([P, fs.stop - fs.start, 2, CW]), op=ALU.max
             )
 
-        def quant_family(c, f):
-            if f == 0:
+        def quant_planes(c, f, a0_, a1_):
+            if "codes" not in st[c]:
                 st[c]["codes"] = work.tile([P, 2 * CW], U32, name="codes", align_bytes=64)
                 st[c]["scl"] = work.tile([P, 2 * CW], U8, name="scl", align_bytes=64)
-            cols = slice(CW * f, CW * f + CW)
+            cols = slice(CW * f + MC * a0_, CW * f + MC * a1_)
             nc.vector.quantize_mx(
                 out=st[c]["codes"][:, cols].bitcast(FP8X4), scales=st[c]["scl"][:, cols],
-                in_=st[c]["fam"][:, f].rearrange("p a w -> p (a w)"),
+                in_=st[c]["fam"][:, f, a0_:a1_].rearrange("p a w -> p (a w)"),
             )
+
+        def quant_family(c, f):
+            quant_planes(c, f, 0, 4)
 
         def silu(c):
             if c % 2 == 0:
@@ -438,7 +451,7 @@ def tile_refiner_pa_kernel(tc, X, Y, Wx, bx, Wy, by, base_w, spline_w, spline_sc
             for k in range(2):
                 st[c + k]["bc"], st[c + k]["bs"] = bc[:, MC * k : MC * k + MC], bs[:, MC * k : MC * k + MC]
 
-        def m2(c, mt, fams, first, last):
+        def m2(c, mt, planes, first, last):
             if first:
                 if c == NCH - 1 and mt == 1:
                     acc[(c, mt)] = bank("acc1", F32)[:, 0:P]
@@ -447,9 +460,8 @@ def tile_refiner_pa_kernel(tc, X, Y, Wx, bx, Wy, by, base_w, spline_w, spline_sc
                         acc[c] = psum.tile([P, 512], F32, name="acc", tag="acc", bufs=2)
                     acc[(c, mt)] = acc[c][:, P * mt : P * mt + P]
             runs = [(st[c]["bc"], st[c]["bs"], P * mt, 8 * P)] if first else []
-            for f in fams:
-                for n in range(4):
-                    runs.append((st[c]["codes"], st[c]["scl"], CW * f + MC * n + P * mt, P * (4 * f + n)))
+            for n in planes:
+                runs.append((st[c]["codes"], st[c]["scl"], MC * n + P * mt, P * n))
             for k, (lhs, lhs_s, m0, q0) in enumerate(runs):
                 nc.tensor.matmul_mx(
                     out=acc[(c, mt)],
@@ -517,48 +529,50 @@ def tile_refiner_pa_kernel(tc, X, Y, Wx, bx, Wy, by, base_w, spline_w, spline_sc
         tanh(0)
         for j in range(2):
             w_transpose(1, j)
-        w_evac(1, 0, S)
         sw_small()
+        weave(0, (0,))
         sw_regroup(sw_raw, V)
-        weave_first(0)
-        sw_transpose(0)
-        w_evac(1, 1, S)
         sw_small_evac()
-        dist(0, 0)
-        dist(0, 1)
+        bw_quant()
+        sw_transpose(0)
+        weave(0, (1,))
+        w_evac(1, 0, S)
+        w_evac(1, 1, S)
         sw_transpose(1)
-        for j in range(2, 4):
-            w_transpose(1, j)
+        dist(0)
         sw_products(0)
         sw_products(1)
+        for j in range(2, 4):
+            w_transpose(1, j)
+        sw_transpose(2)
+        fold(0, 0)
+        squares(0, "sl", rc, None, BOTH)
+        sw_transpose(3)
+        sw_products(2)
+        sw_products(3)
         w_evac(1, 2, S)
         w_evac(1, 3, S)
-        sw_transpose(2)
-        squares(0, "sl", rc, None, BOTH)
-        silu(0)
-        sw_transpose(3)
-        w_quant(1, 0, 4)
-        sw_products(2)
+        fold(0, 1)
         x_copy(1, V)
-        sw_products(3)
+        sw_quant()
         x_quant(1)
+        w_quant(1, 0, 4)
         m1(1)
-        squares(0, "sp", r6, B_M2R6, BOTH)
+        go = let_gpsimd()
+        for f in range(2):
+            cap_line(0, f, nc.gpsimd, go)
         inner_arm(0, 0)
+        inner_arm(0, 1)
+        squares(0, "sp", r6, B_M2R6, BOTH)
         tanh(1)
         weave(1)
-        inner_arm(0, 1)
         load_x(0, 1)
-        bw_quant()
-        fold(0, 0)
-        fold(0, 1)
-        outer_arms(0, BOTH)
+        silu(0)
         x_copy(2, V)
-        sw_quant()
+        outer_arms(0, BOTH)
         x_quant(2)
         m1(2)
         for f in range(2):
-            cap_line(0, f, nc.vector, lines)
             cap_square(0, f)
         x_copy(3, V)
         load_x(1, 1)
@@ -570,12 +584,10 @@ def tile_refiner_pa_kernel(tc, X, Y, Wx, bx, Wy, by, base_w, spline_w, spline_sc
                 finish(c - 3)
             if 1 < c < NCH - 1:
                 weave(c + 1)
-            dist(c, 0)
-            dist(c, 1)
+            dist(c)
             fold(c, 0)
             squares(c, "sl", rc, None, BOTH)
             fold(c, 1)
-            silu(c)
             if c == 1:
                 tanh(2)
                 weave(2)
@@ -584,15 +596,30 @@ def tile_refiner_pa_kernel(tc, X, Y, Wx, bx, Wy, by, base_w, spline_w, spline_sc
             if c + 2 < NCH:
                 x_quant(c + 2)
                 m1(c + 2)
-            split(p, 0, BOTH)
-            go = let_gpsimd()
-            split(p, 1, BOTH)
-            for f in range(2):
-                cap_line(c, f, nc.gpsimd, go)
-            inner_arm(c, 0)
+                split_inner(p, 0, BOTH)
+                split_inner(p, 1, BOTH)
+                split_outer(p, 0, BOTH)
+                go = let_gpsimd()
+                split_outer(p, 1, BOTH)
+                for f in range(2):
+                    cap_line(c, f, nc.gpsimd, go)
+                inner_arm(c, 0)
+            else:
+                inner_arm(c, 0)
+                split_inner(p, 0, BOTH)
+                split_inner(p, 1, BOTH)
+                if c < NCH - 1:
+                    split_outer(p, 0, BOTH)
+                    split_outer(p, 1, BOTH)
             inner_arm(c, 1)
             for f in range(2):
                 cap_square(c, f)
+                if c + 2 >= NCH:
+                    cap_line_s(c, f)
+            silu(c)
+            if c == NCH - 1:
+                for side in range(2):
+                    split_outer(p, side, BOTH, scalar=True)
             if c + 3 < NCH:
                 x_copy(c + 3, S)
             if c + 2 < NCH:
@@ -601,25 +628,35 @@ def tile_refiner_pa_kernel(tc, X, Y, Wx, bx, Wy, by, base_w, spline_w, spline_sc
                 finish(p - 1)
             cap_rest(p, BOTH)
             outer_arms(c, BOTH)
-            if c % 2:
+            if c < NCH - 1:
+                quant_family(p, 0)
+                caps(c, BOTH)
+                quant_family(p, 1)
+                if c % 2:
+                    quant_silu(p)
+            else:
+                caps(c, BOTH)
                 quant_silu(p)
-            quant_family(p, 0)
-            caps(c, BOTH)
-            quant_family(p, 1)
+                cap_arms(c, EVEN)
+                cap_arms(c, ODD)
+                quant_family(p, 0)
+                quant_family(p, 1)
             for mt in range(2):
-                m2(p, mt, (0, 1), True, True)
+                m2(p, mt, range(8), True, True)
 
         p = NCH - 1
+        for fs in (EVEN, ODD):
+            for side in range(2):
+                split_inner(p, side, fs)
+                split_outer(p, side, fs, scalar=True)
         finish(p - 1)
-        cap_arms(p, BOTH)
-        split(p, 0, BOTH)
-        split(p, 1, BOTH)
         cap_rest(p, EVEN)
         cap_rest(p, ODD)
         quant_family(p, 0)
         for mt in range(2):
-            m2(p, mt, (0,), True, False)
-        quant_family(p, 1)
-        for mt in range(2):
-            m2(p, mt, (1,), False, True)
+            m2(p, mt, range(4), True, False)
+        for a in (0, 2):
+            quant_planes(p, 1, a, a + 2)
+            for mt in range(2):
+                m2(p, mt, (4 + a, 5 + a), False, a == 2)
         finish(p)

@@ -149,7 +149,7 @@ def tile_refiner_pa_kernel(tc, X, Y, Wx, bx, Wy, by, base_w, spline_w, spline_sc
 
         def w_evac(sg, j, copier):
             if w_tg[sg] is None:
-                w_tg[sg] = grp_tile("wtg%d" % sg, 4096, BF16)
+                w_tg[sg] = work.tile([P, 4096], BF16, name="wtg%d" % sg, tag="fam", bufs=1, align_bytes=64)
             copier(
                 out=w_tg[sg][:].bitcast(F32)[:, 512 * j : 512 * j + 512].rearrange("p (h i e) -> p h i e", h=2, e=2),
                 in_=w_pt[(sg, j)][:].rearrange("p (h e i) -> p h i e", h=2, e=2),
@@ -402,7 +402,7 @@ def tile_refiner_pa_kernel(tc, X, Y, Wx, bx, Wy, by, base_w, spline_w, spline_sc
 
         def plane(c, fs, n):
             if "fam" not in st[c]:
-                st[c]["fam"] = work.tile([P, 2, 4, CW], BF16, name="fam", bufs=1, align_bytes=64)
+                st[c]["fam"] = work.tile([P, 2, 4, CW], BF16, name="fam", tag="fam", bufs=1, align_bytes=64)
             return st[c]["fam"][:, fs, n, :]
 
         def split_outer(c, side, fs, scalar=False):
@@ -494,89 +494,88 @@ def tile_refiner_pa_kernel(tc, X, Y, Wx, bx, Wy, by, base_w, spline_w, spline_sc
 
         V, S = nc.vector.tensor_copy, nc.scalar.copy
         BOTH, EVEN, ODD = slice(0, 2), slice(0, 1), slice(1, 2)
-        load_w(0, (0, 1, 2, 3))
+        load_w(0, (0, 1))
         xn = load_x_first()
+        load_w(0, (2, 3))
         nc.sync.dma_start(out=brow[0:4, :], in_=bx.rearrange("(r c) -> r c", c=P))
         nc.sync.dma_start(out=brow[4:8, :], in_=by.rearrange("(r c) -> r c", c=P))
-        load_w(1, (0, 1, 2, 3))
-        sw_raw = load_sw()
         load_small()
+        sw_raw = load_sw()
+        load_w(1, (0, 1, 2, 3))
         load_x(1, 0)
         load_x(0, 0, MC)
 
-        for j in range(4):
-            w_regroup(0, j, S if j % 2 else V)
         keep_warm(18)
-        for j in range(4):
+        for j in range(2):
+            w_regroup(0, j, V)
             w_transpose(0, j)
         x_permute(xn)
+        w_evac(0, 0, S)
+        w_evac(0, 1, S)
+        for j in range(2, 4):
+            w_regroup(0, j, V)
+            w_transpose(0, j)
         pb0 = bank("pb0", BF16)
         nc.tensor.transpose(pb0[:, 0:P], brow[:], ident_b[:])
         bias = keep.tile([P, 8], F32, name="bias")
-        w_evac(0, 0, S)
-        w_evac(0, 1, V)
-        w_evac(0, 2, S)
-        w_quant(0, 0, 2)
-        w_evac(0, 3, V)
         x_evac(0, S)
         x_evac(1, V)
-        w_quant(0, 2, 4)
+        w_quant(0, 0, 2)
+        w_evac(0, 2, S)
+        w_evac(0, 3, S)
         x_quant(0)
+        w_quant(0, 2, 4)
         nc.vector.tensor_copy(out=bias[:], in_=pb0[:, 0:8])
-        m1(0)
-        for j in range(4):
-            w_regroup(1, j, S if j < 2 else V)
-        tanh(0)
-        for j in range(2):
-            w_transpose(1, j)
         sw_small()
-        weave(0, (0,))
-        sw_regroup(sw_raw, V)
+        m1(0)
+        tanh(0)
         sw_small_evac()
         bw_quant()
+        sw_regroup(sw_raw, V)
+        weave(0, (0,))
         sw_transpose(0)
         weave(0, (1,))
-        w_evac(1, 0, S)
-        w_evac(1, 1, S)
         sw_transpose(1)
+        for j in range(4):
+            w_regroup(1, j, V if j else S)
         dist(0)
         sw_products(0)
         sw_products(1)
-        for j in range(2, 4):
-            w_transpose(1, j)
         sw_transpose(2)
+        sw_transpose(3)
+        for j in range(4):
+            w_transpose(1, j)
         fold(0, 0)
         squares(0, "sl", rc, None, BOTH)
-        sw_transpose(3)
         sw_products(2)
         sw_products(3)
-        w_evac(1, 2, S)
-        w_evac(1, 3, S)
         fold(0, 1)
-        x_copy(1, V)
+        for j in range(4):
+            w_evac(1, j, S)
         sw_quant()
+        x_copy(1, V)
         x_quant(1)
-        w_quant(1, 0, 4)
-        m1(1)
         go = let_gpsimd()
         for f in range(2):
             cap_line(0, f, nc.gpsimd, go)
         inner_arm(0, 0)
         inner_arm(0, 1)
         squares(0, "sp", r6, B_M2R6, BOTH)
-        tanh(1)
-        weave(1)
-        load_x(0, 1)
-        silu(0)
+        w_quant(1, 0, 4)
+        m1(1)
         x_copy(2, V)
         outer_arms(0, BOTH)
-        x_quant(2)
-        m1(2)
         for f in range(2):
             cap_square(0, f)
+        tanh(1)
+        weave(1)
+        silu(0)
+        load_x(0, 1)
+        x_quant(2)
+        m1(2)
+        caps(0, BOTH)
         x_copy(3, V)
         load_x(1, 1)
-        caps(0, BOTH)
 
         for c in range(1, NCH):
             p = c - 1
@@ -599,8 +598,9 @@ def tile_refiner_pa_kernel(tc, X, Y, Wx, bx, Wy, by, base_w, spline_w, spline_sc
                 split_inner(p, 0, BOTH)
                 split_inner(p, 1, BOTH)
                 split_outer(p, 0, BOTH)
-                go = let_gpsimd()
                 split_outer(p, 1, BOTH)
+                go = let_gpsimd()
+                cap_rest(p, BOTH)
                 for f in range(2):
                     cap_line(c, f, nc.gpsimd, go)
                 inner_arm(c, 0)
@@ -612,21 +612,23 @@ def tile_refiner_pa_kernel(tc, X, Y, Wx, bx, Wy, by, base_w, spline_w, spline_sc
                     split_outer(p, 0, BOTH)
                     split_outer(p, 1, BOTH)
             inner_arm(c, 1)
+            if c + 2 >= NCH:
+                cap_rest(p, BOTH)
             for f in range(2):
                 cap_square(c, f)
                 if c + 2 >= NCH:
                     cap_line_s(c, f)
-            silu(c)
             if c == NCH - 1:
-                for side in range(2):
-                    split_outer(p, side, BOTH, scalar=True)
+                for fs in (EVEN, ODD):
+                    for side in range(2):
+                        split_outer(p, side, fs, scalar=True)
+            silu(c)
             if c + 3 < NCH:
                 x_copy(c + 3, S)
             if c + 2 < NCH:
                 tanh(c + 2)
             if p > 0 and p % 2 == 0:
                 finish(p - 1)
-            cap_rest(p, BOTH)
             outer_arms(c, BOTH)
             if c < NCH - 1:
                 quant_family(p, 0)
@@ -636,11 +638,11 @@ def tile_refiner_pa_kernel(tc, X, Y, Wx, bx, Wy, by, base_w, spline_w, spline_sc
                     quant_silu(p)
             else:
                 caps(c, BOTH)
-                quant_silu(p)
+                quant_family(p, 0)
                 cap_arms(c, EVEN)
                 cap_arms(c, ODD)
-                quant_family(p, 0)
                 quant_family(p, 1)
+                quant_silu(p)
             for mt in range(2):
                 m2(p, mt, range(8), True, True)
 

@@ -47,6 +47,10 @@ def tile_refiner_pa_kernel(tc, X, Y, Wx, bx, Wy, by, base_w, spline_w, spline_sc
         def bank(nm, dt):
             return psum.tile([P, 512], dt, name=nm, tag="s1", bufs=6)
 
+        w_codes = [keep.tile([P, 1024], U32, name="wc%d" % sg, align_bytes=64) for sg in range(2)]
+        w_scales = [keep.tile([P, 1024], U8, name="ws%d" % sg, align_bytes=64) for sg in range(2)]
+        nc.vector.memset(w_codes[0][:, 0:512], 0)
+        nc.vector.memset(w_scales[0][:, 0:512].bitcast(U32), 0)
         ident_f = keep.tile([P, P], F32, name="ident_f")
         make_identity(nc, ident_f[:])
         ident_b = keep.tile([P, P], BF16, name="ident_b")
@@ -69,10 +73,13 @@ def tile_refiner_pa_kernel(tc, X, Y, Wx, bx, Wy, by, base_w, spline_w, spline_sc
         for i, v in enumerate((0.5, -0.5, (a0 - 1.0) / 2.0, a0 / 2.0)):
             nc.scalar.activation(out=lines[:, i : i + 1], in_=ones[:, 0:1], func=ACTF.Copy, scale=v)
 
-        def keep_warm(n):
-            pw = bank("pw", BF16)
+        def keep_clock(n, codes, scales, tag, bufs):
+            idle = psum.tile([P, 512], F32, name="idle", tag=tag, bufs=bufs)
             for k in range(n):
-                nc.tensor.transpose(pw[:, 0:P], ident_b[:], ident_b[:])
+                nc.tensor.matmul_mx(
+                    out=idle[:], lhsT=codes[:, 0:P].bitcast(FP8X4), lhsT_scale=scales[:, 0:P],
+                    rhs=codes[:, 0:512].bitcast(FP8X4), rhs_scale=scales[:, 0:512], start=True, stop=True,
+                )
 
         def cbias(i):
             return cb[:, i : i + 1]
@@ -125,8 +132,6 @@ def tile_refiner_pa_kernel(tc, X, Y, Wx, bx, Wy, by, base_w, spline_w, spline_sc
         w_grp = [None, None]
         w_tg = [None, None]
         w_pt = {}
-        w_codes = [None, None]
-        w_scales = [None, None]
 
         def grp_tile(nm, cols, dt):
             return prep.tile([P, cols], dt, name=nm, tag="raw", bufs=4, align_bytes=64)
@@ -156,9 +161,6 @@ def tile_refiner_pa_kernel(tc, X, Y, Wx, bx, Wy, by, base_w, spline_w, spline_sc
             )
 
         def w_quant(sg, lo, hi):
-            if lo == 0:
-                w_codes[sg] = keep.tile([P, 1024], U32, name="wc%d" % sg, align_bytes=64)
-                w_scales[sg] = keep.tile([P, 1024], U8, name="ws%d" % sg, align_bytes=64)
             nc.vector.quantize_mx(
                 out=w_codes[sg][:, 256 * lo : 256 * hi].bitcast(FP8X4),
                 scales=w_scales[sg][:, 256 * lo : 256 * hi],
@@ -190,11 +192,13 @@ def tile_refiner_pa_kernel(tc, X, Y, Wx, bx, Wy, by, base_w, spline_w, spline_sc
 
         def sw_small_evac():
             psc, pbw = sw_state["psc"], sw_state["pbw"]
-            nc.vector.tensor_scalar(
-                out=sct[:, 512:1024].rearrange("p (q j) -> p q j", j=4), in0=psc[:].rearrange("p (j q) -> p q j", j=4),
-                scalar1=-1.0, scalar2=None, op0=ALU.mult,
+            nc.scalar.activation(
+                out=sct[:, 512:1024].rearrange("p (q j) -> p q j", j=4), in_=psc[:].rearrange("p (j q) -> p q j", j=4),
+                func=ACTF.Copy, scale=-1.0,
             )
-            nc.vector.tensor_copy(out=bwt[:].rearrange("p (q j) -> p q j", j=4), in_=pbw[:].rearrange("p (j q) -> p q j", j=4))
+            nc.scalar.copy(out=bwt[:].rearrange("p (q j) -> p q j", j=4), in_=pbw[:].rearrange("p (j q) -> p q j", j=4))
+
+        def sw_positive():
             for k in (0, 1024):
                 nc.vector.tensor_scalar(out=sct[:, k : k + 512], in0=sct[:, 512:1024], scalar1=-1.0, scalar2=None, op0=ALU.mult)
 
@@ -496,16 +500,16 @@ def tile_refiner_pa_kernel(tc, X, Y, Wx, bx, Wy, by, base_w, spline_w, spline_sc
         BOTH, EVEN, ODD = slice(0, 2), slice(0, 1), slice(1, 2)
         load_w(0, (0, 1))
         xn = load_x_first()
-        load_w(0, (2, 3))
         nc.sync.dma_start(out=brow[0:4, :], in_=bx.rearrange("(r c) -> r c", c=P))
         nc.sync.dma_start(out=brow[4:8, :], in_=by.rearrange("(r c) -> r c", c=P))
-        load_small()
+        load_w(0, (2, 3))
         sw_raw = load_sw()
+        load_small()
         load_w(1, (0, 1, 2, 3))
         load_x(1, 0)
         load_x(0, 0, MC)
 
-        keep_warm(18)
+        keep_clock(5, w_codes[0], w_scales[0], "acc", 2)
         for j in range(2):
             w_regroup(0, j, V)
             w_transpose(0, j)
@@ -521,23 +525,26 @@ def tile_refiner_pa_kernel(tc, X, Y, Wx, bx, Wy, by, base_w, spline_w, spline_sc
         x_evac(0, S)
         x_evac(1, V)
         w_quant(0, 0, 2)
+        keep_clock(2, w_codes[0], w_scales[0], "acc", 2)
         w_evac(0, 2, S)
         w_evac(0, 3, S)
         x_quant(0)
         w_quant(0, 2, 4)
         nc.vector.tensor_copy(out=bias[:], in_=pb0[:, 0:8])
-        sw_small()
         m1(0)
-        tanh(0)
-        sw_small_evac()
-        bw_quant()
         sw_regroup(sw_raw, V)
-        weave(0, (0,))
+        sw_small()
+        tanh(0)
         sw_transpose(0)
+        weave(0, (0,))
+        sw_small_evac()
+        for j in range(2):
+            w_regroup(1, j, V)
         weave(0, (1,))
         sw_transpose(1)
-        for j in range(4):
-            w_regroup(1, j, V if j else S)
+        w_regroup(1, 2, V)
+        sw_positive()
+        w_regroup(1, 3, V)
         dist(0)
         sw_products(0)
         sw_products(1)
@@ -560,6 +567,7 @@ def tile_refiner_pa_kernel(tc, X, Y, Wx, bx, Wy, by, base_w, spline_w, spline_sc
             cap_line(0, f, nc.gpsimd, go)
         inner_arm(0, 0)
         inner_arm(0, 1)
+        bw_quant()
         squares(0, "sp", r6, B_M2R6, BOTH)
         w_quant(1, 0, 4)
         m1(1)
@@ -647,6 +655,7 @@ def tile_refiner_pa_kernel(tc, X, Y, Wx, bx, Wy, by, base_w, spline_w, spline_sc
                 m2(p, mt, range(8), True, True)
 
         p = NCH - 1
+        keep_clock(4, swc, sws, "s1", 6)
         for fs in (EVEN, ODD):
             for side in range(2):
                 split_inner(p, side, fs)

@@ -47,10 +47,6 @@ def tile_refiner_pa_kernel(tc, X, Y, Wx, bx, Wy, by, base_w, spline_w, spline_sc
         def bank(nm, dt):
             return psum.tile([P, 512], dt, name=nm, tag="s1", bufs=6)
 
-        w_codes = [keep.tile([P, 1024], U32, name="wc%d" % sg, align_bytes=64) for sg in range(2)]
-        w_scales = [keep.tile([P, 1024], U8, name="ws%d" % sg, align_bytes=64) for sg in range(2)]
-        nc.vector.memset(w_codes[0][:, 0:512], 0)
-        nc.vector.memset(w_scales[0][:, 0:512].bitcast(U32), 0)
         ident_f = keep.tile([P, P], F32, name="ident_f")
         make_identity(nc, ident_f[:])
         ident_b = keep.tile([P, P], BF16, name="ident_b")
@@ -73,13 +69,10 @@ def tile_refiner_pa_kernel(tc, X, Y, Wx, bx, Wy, by, base_w, spline_w, spline_sc
         for i, v in enumerate((0.5, -0.5, (a0 - 1.0) / 2.0, a0 / 2.0)):
             nc.scalar.activation(out=lines[:, i : i + 1], in_=ones[:, 0:1], func=ACTF.Copy, scale=v)
 
-        def keep_clock(n, codes, scales, tag, bufs):
-            idle = psum.tile([P, 512], F32, name="idle", tag=tag, bufs=bufs)
+        def keep_warm(n):
+            pw = bank("pw", BF16)
             for k in range(n):
-                nc.tensor.matmul_mx(
-                    out=idle[:], lhsT=codes[:, 0:P].bitcast(FP8X4), lhsT_scale=scales[:, 0:P],
-                    rhs=codes[:, 0:512].bitcast(FP8X4), rhs_scale=scales[:, 0:512], start=True, stop=True,
-                )
+                nc.tensor.transpose(pw[:, 0:P], ident_b[:], ident_b[:])
 
         def cbias(i):
             return cb[:, i : i + 1]
@@ -132,6 +125,8 @@ def tile_refiner_pa_kernel(tc, X, Y, Wx, bx, Wy, by, base_w, spline_w, spline_sc
         w_grp = [None, None]
         w_tg = [None, None]
         w_pt = {}
+        w_codes = [None, None]
+        w_scales = [None, None]
 
         def grp_tile(nm, cols, dt):
             return prep.tile([P, cols], dt, name=nm, tag="raw", bufs=4, align_bytes=64)
@@ -161,6 +156,9 @@ def tile_refiner_pa_kernel(tc, X, Y, Wx, bx, Wy, by, base_w, spline_w, spline_sc
             )
 
         def w_quant(sg, lo, hi):
+            if lo == 0:
+                w_codes[sg] = keep.tile([P, 1024], U32, name="wc%d" % sg, align_bytes=64)
+                w_scales[sg] = keep.tile([P, 1024], U8, name="ws%d" % sg, align_bytes=64)
             nc.vector.quantize_mx(
                 out=w_codes[sg][:, 256 * lo : 256 * hi].bitcast(FP8X4),
                 scales=w_scales[sg][:, 256 * lo : 256 * hi],
@@ -509,7 +507,7 @@ def tile_refiner_pa_kernel(tc, X, Y, Wx, bx, Wy, by, base_w, spline_w, spline_sc
         load_x(1, 0)
         load_x(0, 0, MC)
 
-        keep_clock(5, w_codes[0], w_scales[0], "acc", 2)
+        keep_warm(18)
         for j in range(2):
             w_regroup(0, j, V)
             w_transpose(0, j)
@@ -525,7 +523,6 @@ def tile_refiner_pa_kernel(tc, X, Y, Wx, bx, Wy, by, base_w, spline_w, spline_sc
         x_evac(0, S)
         x_evac(1, V)
         w_quant(0, 0, 2)
-        keep_clock(2, w_codes[0], w_scales[0], "acc", 2)
         w_evac(0, 2, S)
         w_evac(0, 3, S)
         x_quant(0)
@@ -595,38 +592,27 @@ def tile_refiner_pa_kernel(tc, X, Y, Wx, bx, Wy, by, base_w, spline_w, spline_sc
             fold(c, 0)
             squares(c, "sl", rc, None, BOTH)
             fold(c, 1)
+            squares(c, "sp", r6, B_M2R6, BOTH)
             if c == 1:
                 tanh(2)
                 weave(2)
-            squares(c, "sp", r6, B_M2R6, BOTH)
+            for side in range(2):
+                split_inner(p, side, BOTH)
             cap_arms(p, BOTH)
             if c + 2 < NCH:
                 x_quant(c + 2)
                 m1(c + 2)
-                split_inner(p, 0, BOTH)
-                split_inner(p, 1, BOTH)
-                split_outer(p, 0, BOTH)
-                split_outer(p, 1, BOTH)
-                go = let_gpsimd()
-                cap_rest(p, BOTH)
-                for f in range(2):
-                    cap_line(c, f, nc.gpsimd, go)
-                inner_arm(c, 0)
-            else:
-                inner_arm(c, 0)
-                split_inner(p, 0, BOTH)
-                split_inner(p, 1, BOTH)
-                if c < NCH - 1:
-                    split_outer(p, 0, BOTH)
-                    split_outer(p, 1, BOTH)
-            inner_arm(c, 1)
-            if c + 2 >= NCH:
-                cap_rest(p, BOTH)
+            if p < 5:
+                for side in range(2):
+                    split_outer(p, side, BOTH)
+            go = let_gpsimd()
+            cap_rest(p, BOTH)
+            for f in range(2):
+                cap_line(c, f, nc.gpsimd, go)
+                inner_arm(c, f)
             for f in range(2):
                 cap_square(c, f)
-                if c + 2 >= NCH:
-                    cap_line_s(c, f)
-            if c == NCH - 1:
+            if p >= 5:
                 for fs in (EVEN, ODD):
                     for side in range(2):
                         split_outer(p, side, fs, scalar=True)
@@ -655,7 +641,6 @@ def tile_refiner_pa_kernel(tc, X, Y, Wx, bx, Wy, by, base_w, spline_w, spline_sc
                 m2(p, mt, range(8), True, True)
 
         p = NCH - 1
-        keep_clock(4, swc, sws, "s1", 6)
         for fs in (EVEN, ODD):
             for side in range(2):
                 split_inner(p, side, fs)

@@ -116,7 +116,7 @@ def tile_refiner_pa_kernel(tc, X, Y, Wx, bx, Wy, by, base_w, spline_w, spline_sc
             swr = raw_tile("swr")
             for sg in range(2):
                 nc.sync.dma_start(
-                    out=swr[64 * sg : 64 * sg + 64, :],
+                    out=swr[sg : P : 2, :],
                     in_=spline_w[:, 512 * sg : 512 * sg + 512, :].rearrange("o i k -> o (i k)"),
                 )
             return swr
@@ -175,7 +175,7 @@ def tile_refiner_pa_kernel(tc, X, Y, Wx, bx, Wy, by, base_w, spline_w, spline_sc
 
         def load_small():
             for sg in range(2):
-                rows = slice(64 * sg, 64 * sg + 64)
+                rows = slice(sg, P, 2)
                 cols = slice(512 * sg, 512 * sg + 512)
                 nc.sync.dma_start(out=scr[rows, :], in_=spline_scaler[:, cols])
                 nc.sync.dma_start(out=bwr[rows, :], in_=base_w[:, cols])
@@ -366,12 +366,6 @@ def tile_refiner_pa_kernel(tc, X, Y, Wx, bx, Wy, by, base_w, spline_w, spline_sc
                 scalar2=consts[:, 2 + f : 3 + f], op0=ALU.mult, op1=ALU.add,
             )
 
-        def cap_line_s(c, f):
-            nc.scalar.activation(
-                out=pair(c, "l", "lin", 2)[:, f, :], in_=st[c]["vb"][:], func=ACTF.Identity,
-                bias=lines[:, 2 + f : 3 + f], scale=(0.5, -0.5)[f],
-            )
-
         def arms(c):
             if "arms" not in st[c]:
                 st[c]["arms"] = work.tile([P, 2, 2, CW], BF16, name="arms", align_bytes=64)
@@ -477,7 +471,7 @@ def tile_refiner_pa_kernel(tc, X, Y, Wx, bx, Wy, by, base_w, spline_w, spline_sc
 
         def finish(c):
             b, h, sg = where(c)
-            cols = slice(64 * sg, 64 * sg + 64)
+            cols = slice(sg, P, 2)
             rows = out[b, MC * h : MC * h + MC, :].rearrange("(mt p) o -> p mt o", p=P)
             if sg == 0:
                 ob = work.tile([P, 2, 64], F32, name="ob", bufs=2)

@@ -53,7 +53,7 @@ def tile_refiner_pa_kernel(tc, X, Y, Wx, bx, Wy, by, base_w, spline_w, spline_sc
         make_identity(nc, ident_b[:])
         perm = keep.tile([P, P], BF16, name="perm")
         nc.vector.tensor_copy(
-            out=perm[:].rearrange("p (c a s) -> p c a s", c=4, a=8), in_=ident_b[:].rearrange("p (a c s) -> p c a s", a=8, c=4)
+            out=perm[:].rearrange("p (g i a) -> p g i a", g=2, i=16), in_=ident_b[:].rearrange("p (g a i) -> p g i a", g=2, a=4)
         )
         ones = keep.tile([P, 8], F32, name="ones")
         nc.vector.memset(ones[:], 1.0)
@@ -106,10 +106,10 @@ def tile_refiner_pa_kernel(tc, X, Y, Wx, bx, Wy, by, base_w, spline_w, spline_sc
                 xr = prep.tile([P, 8 * (512 - n0)], BF16, name="xb", tag="half", bufs=2)
             else:
                 xr = prep.tile([P, 4096], BF16, name="xr%d%d" % (sg, b), tag="xr", bufs=2)
-            src = (X, Y)[sg][b].rearrange("(a c) n f -> c a (n f)", c=16)
-            for k in range(16):
-                p0 = 32 * (k // 4) + k % 4
-                nc.sync.dma_start(out=xr[p0 : 32 * (k // 4) + 32 : 4, :], in_=src[k][:, 8 * n0 : 4096])
+            src = (X, Y)[sg][b].rearrange("(k i) n f -> k i (n f)", i=16)
+            for k in range(8):
+                g = k // 4
+                nc.sync.dma_start(out=xr[64 * g + k % 4 : 64 * g + 64 : 4, :], in_=src[k][:, 8 * n0 : 4096])
             x_raw[(sg, b)] = xr, n0
 
         def load_sw():
@@ -134,9 +134,9 @@ def tile_refiner_pa_kernel(tc, X, Y, Wx, bx, Wy, by, base_w, spline_w, spline_sc
         def w_regroup(sg, j, copier):
             if w_grp[sg] is None:
                 w_grp[sg] = grp_tile("wg%d" % sg, 2048, F32)
-            wrw = w_raw[sg][:].bitcast(F32).rearrange("p (j a c s f) -> p j c a s f", j=4, a=8, c=4, s=4, f=4)
+            wrw = w_raw[sg][:].bitcast(F32).rearrange("p (j g a i f) -> p j g i a f", j=4, g=2, a=4, i=16, f=4)
             copier(
-                out=w_grp[sg][:, 512 * j : 512 * j + 512].rearrange("p (f c a s) -> p c a s f", f=4, c=4, a=8, s=4),
+                out=w_grp[sg][:, 512 * j : 512 * j + 512].rearrange("p (f g i a) -> p g i a f", f=4, g=2, i=16, a=4),
                 in_=wrw[:, j],
             )
 
@@ -531,34 +531,33 @@ def tile_refiner_pa_kernel(tc, X, Y, Wx, bx, Wy, by, base_w, spline_w, spline_sc
         sw_small_evac()
         for j in range(2):
             w_regroup(1, j, V)
-        weave(0, (1,))
         sw_transpose(1)
-        w_regroup(1, 2, V)
+        weave(0, (1,))
         sw_positive()
-        w_regroup(1, 3, V)
         dist(0)
         sw_products(0)
         sw_products(1)
         sw_transpose(2)
         sw_transpose(3)
-        for j in range(4):
-            w_transpose(1, j)
         fold(0, 0)
         squares(0, "sl", rc, None, BOTH)
         sw_products(2)
         sw_products(3)
         fold(0, 1)
+        for j in range(2, 4):
+            w_regroup(1, j, V)
         for j in range(4):
+            w_transpose(1, j)
             w_evac(1, j, S)
         sw_quant()
         x_copy(1, V)
+        bw_quant()
         x_quant(1)
         go = let_gpsimd()
         for f in range(2):
             cap_line(0, f, nc.gpsimd, go)
         inner_arm(0, 0)
         inner_arm(0, 1)
-        bw_quant()
         squares(0, "sp", r6, B_M2R6, BOTH)
         w_quant(1, 0, 4)
         m1(1)

@@ -47,6 +47,10 @@ def tile_refiner_pa_kernel(tc, X, Y, Wx, bx, Wy, by, base_w, spline_w, spline_sc
         def bank(nm, dt):
             return psum.tile([P, 512], dt, name=nm, tag="s1", bufs=6)
 
+        w_codes = [keep.tile([P, 1024], U32, name="wc%d" % sg, align_bytes=64) for sg in range(2)]
+        w_scales = [keep.tile([P, 1024], U8, name="ws%d" % sg, align_bytes=64) for sg in range(2)]
+        nc.vector.memset(w_codes[0][:, 0:512], 0)
+        nc.vector.memset(w_scales[0][:, 0:512].bitcast(U32), 0)
         ident_f = keep.tile([P, P], F32, name="ident_f")
         make_identity(nc, ident_f[:])
         ident_b = keep.tile([P, P], BF16, name="ident_b")
@@ -69,10 +73,13 @@ def tile_refiner_pa_kernel(tc, X, Y, Wx, bx, Wy, by, base_w, spline_w, spline_sc
         for i, v in enumerate((0.5, -0.5, (a0 - 1.0) / 2.0, a0 / 2.0)):
             nc.scalar.activation(out=lines[:, i : i + 1], in_=ones[:, 0:1], func=ACTF.Copy, scale=v)
 
-        def keep_warm(n):
-            pw = bank("pw", BF16)
+        def keep_clock(n, codes, scales, tag, bufs):
+            idle = psum.tile([P, 512], F32, name="idle", tag=tag, bufs=bufs)
             for k in range(n):
-                nc.tensor.transpose(pw[:, 0:P], ident_b[:], ident_b[:])
+                nc.tensor.matmul_mx(
+                    out=idle[:], lhsT=codes[:, 0:P].bitcast(FP8X4), lhsT_scale=scales[:, 0:P],
+                    rhs=codes[:, 0:512].bitcast(FP8X4), rhs_scale=scales[:, 0:512], start=True, stop=True,
+                )
 
         def cbias(i):
             return cb[:, i : i + 1]
@@ -114,19 +121,13 @@ def tile_refiner_pa_kernel(tc, X, Y, Wx, bx, Wy, by, base_w, spline_w, spline_sc
 
         def load_sw():
             swr = raw_tile("swr")
-            for sg in range(2):
-                nc.sync.dma_start(
-                    out=swr[sg : P : 2, :],
-                    in_=spline_w[:, 512 * sg : 512 * sg + 512, :].rearrange("o i k -> o (i k)"),
-                )
+            nc.sync.dma_start(out=swr[:], in_=spline_w.rearrange("o (s i) k -> (o s) (i k)", s=2))
             return swr
 
         w_raw = [None, None]
         w_grp = [None, None]
         w_tg = [None, None]
         w_pt = {}
-        w_codes = [None, None]
-        w_scales = [None, None]
 
         def grp_tile(nm, cols, dt):
             return prep.tile([P, cols], dt, name=nm, tag="raw", bufs=4, align_bytes=64)
@@ -156,9 +157,6 @@ def tile_refiner_pa_kernel(tc, X, Y, Wx, bx, Wy, by, base_w, spline_w, spline_sc
             )
 
         def w_quant(sg, lo, hi):
-            if lo == 0:
-                w_codes[sg] = keep.tile([P, 1024], U32, name="wc%d" % sg, align_bytes=64)
-                w_scales[sg] = keep.tile([P, 1024], U8, name="ws%d" % sg, align_bytes=64)
             nc.vector.quantize_mx(
                 out=w_codes[sg][:, 256 * lo : 256 * hi].bitcast(FP8X4),
                 scales=w_scales[sg][:, 256 * lo : 256 * hi],
@@ -174,11 +172,8 @@ def tile_refiner_pa_kernel(tc, X, Y, Wx, bx, Wy, by, base_w, spline_w, spline_sc
         sw_state = {}
 
         def load_small():
-            for sg in range(2):
-                rows = slice(sg, P, 2)
-                cols = slice(512 * sg, 512 * sg + 512)
-                nc.sync.dma_start(out=scr[rows, :], in_=spline_scaler[:, cols])
-                nc.sync.dma_start(out=bwr[rows, :], in_=base_w[:, cols])
+            nc.sync.dma_start(out=scr[:], in_=spline_scaler.rearrange("o (s i) -> (o s) i", s=2))
+            nc.sync.dma_start(out=bwr[:], in_=base_w.rearrange("o (s i) -> (o s) i", s=2))
 
         def sw_small():
             sw_state["psc"] = psc = bank("psc", BF16)
@@ -501,7 +496,7 @@ def tile_refiner_pa_kernel(tc, X, Y, Wx, bx, Wy, by, base_w, spline_w, spline_sc
         load_x(1, 0)
         load_x(0, 0, MC)
 
-        keep_warm(18)
+        keep_clock(5, w_codes[0], w_scales[0], "acc", 2)
         for j in range(2):
             w_regroup(0, j, V)
             w_transpose(0, j)
@@ -515,13 +510,14 @@ def tile_refiner_pa_kernel(tc, X, Y, Wx, bx, Wy, by, base_w, spline_w, spline_sc
         nc.tensor.transpose(pb0[:, 0:P], brow[:], ident_b[:])
         bias = keep.tile([P, 8], F32, name="bias")
         x_evac(0, S)
-        x_evac(1, V)
+        x_evac(1, S)
         w_quant(0, 0, 2)
+        keep_clock(2, w_codes[0], w_scales[0], "acc", 2)
         w_evac(0, 2, S)
         w_evac(0, 3, S)
         x_quant(0)
-        w_quant(0, 2, 4)
         nc.vector.tensor_copy(out=bias[:], in_=pb0[:, 0:8])
+        w_quant(0, 2, 4)
         m1(0)
         sw_regroup(sw_raw, V)
         sw_small()
@@ -634,6 +630,7 @@ def tile_refiner_pa_kernel(tc, X, Y, Wx, bx, Wy, by, base_w, spline_w, spline_sc
                 m2(p, mt, range(8), True, True)
 
         p = NCH - 1
+        keep_clock(4, swc, sws, "s1", 6)
         for fs in (EVEN, ODD):
             for side in range(2):
                 split_inner(p, side, fs)

import math
from contextlib import ExitStack

import concourse.mybir as mybir
from concourse.masks import make_identity

F32 = mybir.dt.float32
BF16 = mybir.dt.bfloat16
U32 = mybir.dt.uint32
U8 = mybir.dt.uint8
FP8X4 = mybir.dt.float8_e4m3fn_x4
ACTF = mybir.ActivationFunctionType
ALU = mybir.AluOpType
AX = mybir.AxisListType

P = 128
FLOPS = 2 * 2 * 1024 * 1024 * 512 + 2 * 1024 * 64 * (1024 + 8192)
MC = 256
CW = 4 * MC
NCH = 8
KFAM = ((0, 6, 4, 2), (7, 5, 3, 1))


def central_constants():
    a0 = -0.7
    for i in range(80):
        a0 = a0 - (a0 ** 3 - 2.0 * a0 ** 2 + 4.0 / 3.0) / (3.0 * a0 ** 2 - 4.0 * a0)
    b = a0 - 2.0
    return a0, b / 2.0, a0 * b - b * b / 4.0


def tile_refiner_pa_kernel(tc, X, Y, Wx, bx, Wy, by, base_w, spline_w, spline_scaler, out):
    nc = tc.nc
    a0, hb, cp = central_constants()
    r6 = 1.0 / math.sqrt(6.0)
    rc = math.sqrt(2.5 / 6.0)
    bias_vals = (-0.5, 0.5, -2.0, -1.0, -2.0 * r6, hb, 1.0 + hb)
    (B_M05, B_P05, B_M2, B_M1, B_M2R6, B_HB, B_1HB) = range(7)

    with ExitStack() as ctx:
        keep = ctx.enter_context(tc.tile_pool(name="keep", bufs=1))
        prep = ctx.enter_context(tc.tile_pool(name="prep", bufs=1))
        work = ctx.enter_context(tc.tile_pool(name="work", bufs=2))
        psum = ctx.enter_context(tc.psum_pool(name="psum", bufs=1))
        ctx.enter_context(tc.manual_schedule())

        def bank(nm, dt):
            return psum.tile([P, 512], dt, name=nm, tag="s1", bufs=6)

        w_codes = [keep.tile([P, 1024], U32, name="wc%d" % sg, align_bytes=64) for sg in range(2)]
        w_scales = [keep.tile([P, 1024], U8, name="ws%d" % sg, align_bytes=64) for sg in range(2)]
        nc.vector.memset(w_codes[0][:, 0:512], 0)
        nc.vector.memset(w_scales[0][:, 0:512].bitcast(U32), 0)
        ident_f = keep.tile([P, P], F32, name="ident_f")
        make_identity(nc, ident_f[:])
        ident_b = keep.tile([P, P], BF16, name="ident_b")
        make_identity(nc, ident_b[:])
        perm = keep.tile([P, P], BF16, name="perm")
        nc.vector.tensor_copy(
            out=perm[:].rearrange("p (g i a) -> p g i a", g=2, i=16), in_=ident_b[:].rearrange("p (g a i) -> p g i a", g=2, a=4)
        )
        ones = keep.tile([P, 8], F32, name="ones")
        nc.vector.memset(ones[:], 1.0)
        brow = keep.tile([P, P], BF16, name="brow")
        nc.vector.memset(brow[:], 0.0)
        cb = keep.tile([P, 16], F32, name="cb")
        warm = keep.tile([P, 8], F32, name="warm")
        nc.scalar.activation(out=warm[:, 0:1], in_=ones[:, 0:1], func=ACTF.Silu)
        for i, v in enumerate(bias_vals):
            nc.scalar.activation(out=cb[:, i : i + 1], in_=ones[:, 0:1], func=ACTF.Copy, scale=v)

        lines = keep.tile([P, 4], F32, name="lines")
        for i, v in enumerate((0.5, -0.5, (a0 - 1.0) / 2.0, a0 / 2.0)):
            nc.scalar.activation(out=lines[:, i : i + 1], in_=ones[:, 0:1], func=ACTF.Copy, scale=v)

        def keep_clock(n, codes, scales, tag, bufs):
            idle = psum.tile([P, 512], F32, name="idle", tag=tag, bufs=bufs)
            for k in range(n):
                nc.tensor.matmul_mx(
                    out=idle[:], lhsT=codes[:, 0:P].bitcast(FP8X4), lhsT_scale=scales[:, 0:P],
                    rhs=codes[:, 0:512].bitcast(FP8X4), rhs_scale=scales[:, 0:512], start=True, stop=True,
                )

        def cbias(i):
            return cb[:, i : i + 1]

        low = keep.tile([P, 1], F32, name="low")
        nc.vector.tensor_reduce(
            out=low[:], in_=ident_f[:].rearrange("p (g e r) -> p e g r", e=2, r=4)[:, 0], axis=AX.XY, op=ALU.add
        )
        sgn = keep.tile([P, 2], F32, name="sgn")
        nc.vector.tensor_scalar(out=sgn[:, 0:1], in0=low[:], scalar1=2.0, scalar2=-1.0, op0=ALU.mult, op1=ALU.add)
        nc.vector.tensor_scalar(out=sgn[:, 1:2], in0=low[:], scalar1=-2.0, scalar2=1.0, op0=ALU.mult, op1=ALU.add)

        def raw_tile(nm):
            return prep.tile([P, 4096], BF16, name=nm, tag="raw", bufs=4, align_bytes=64)

        def load_w(sg, parts):
            w = (Wx, Wy)[sg]
            if w_raw[sg] is None:
                w_raw[sg] = raw_tile("wr%d" % sg)
            wr = w_raw[sg]
            for j in parts:
                nc.sync.dma_start(out=wr[:, 1024 * j : 1024 * j + 1024], in_=w[P * j : P * j + P, :])

        def load_x_first():
            xn = prep.tile([P, 8 * MC], BF16, name="xn", tag="half", bufs=2)
            nc.sync.dma_start(out=xn[:], in_=X[0][:, 0:MC].rearrange("t n f -> t (n f)"))
            return xn

        def load_x(sg, b, n0=0):
            if n0:
                xr = prep.tile([P, 8 * (512 - n0)], BF16, name="xb", tag="half", bufs=2)
            else:
                xr = prep.tile([P, 4096], BF16, name="xr%d%d" % (sg, b), tag="xr", bufs=2)
            src = (X, Y)[sg][b].rearrange("(k i) n f -> k i (n f)", i=16)
            for k in range(8):
                g = k // 4
                nc.sync.dma_start(out=xr[64 * g + k % 4 : 64 * g + 64 : 4, :], in_=src[k][:, 8 * n0 : 4096])
            x_raw[(sg, b)] = xr, n0

        def load_sw():
            swr = raw_tile("swr")
            nc.sync.dma_start(out=swr[:], in_=spline_w.rearrange("o (s i) k -> (o s) (i k)", s=2))
            return swr

        w_raw = [None, None]
        w_grp = [None, None]
        w_tg = [None, None]
        w_pt = {}

        def grp_tile(nm, cols, dt):
            return prep.tile([P, cols], dt, name=nm, tag="raw", bufs=4, align_bytes=64)

        def w_regroup(sg, j, copier):
            if w_grp[sg] is None:
                w_grp[sg] = grp_tile("wg%d" % sg, 2048, F32)
            wrw = w_raw[sg][:].bitcast(F32).rearrange("p (j g a i f) -> p j g i a f", j=4, g=2, a=4, i=16, f=4)
            copier(
                out=w_grp[sg][:, 512 * j : 512 * j + 512].rearrange("p (f g i a) -> p g i a f", f=4, g=2, i=16, a=4),
                in_=wrw[:, j],
            )

        def w_transpose(sg, j):
            wg = w_grp[sg]
            pt = bank("ptw%d%d" % (sg, j), F32)
            for f in range(4):
                nc.tensor.transpose(pt[:, P * f : P * f + P], wg[:, 512 * j + P * f : 512 * j + P * f + P], ident_f[:])
            w_pt[(sg, j)] = pt

        def w_evac(sg, j, copier):
            if w_tg[sg] is None:
                w_tg[sg] = work.tile([P, 4096], BF16, name="wtg%d" % sg, tag="fam", bufs=1, align_bytes=64)
            copier(
                out=w_tg[sg][:].bitcast(F32)[:, 512 * j : 512 * j + 512].rearrange("p (h i e) -> p h i e", h=2, e=2),
                in_=w_pt[(sg, j)][:].rearrange("p (h e i) -> p h i e", h=2, e=2),
            )

        def w_quant(sg, lo, hi):
            nc.vector.quantize_mx(
                out=w_codes[sg][:, 256 * lo : 256 * hi].bitcast(FP8X4),
                scales=w_scales[sg][:, 256 * lo : 256 * hi],
                in_=w_tg[sg][:, 1024 * lo : 1024 * hi],
            )

        scr = prep.tile([P, 512], BF16, name="scr")
        bwr = prep.tile([P, 512], BF16, name="bwr")
        sct = prep.tile([P, 3 * 512], BF16, name="sct")
        bwt = prep.tile([P, 512], BF16, name="bwt", align_bytes=64)
        swc = keep.tile([P, 9 * P], U32, name="swc", align_bytes=64)
        sws = keep.tile([P, 9 * P], U8, name="sws", align_bytes=64)
        sw_state = {}

        def load_small():
            nc.sync.dma_start(out=scr[:], in_=spline_scaler.rearrange("o (s i) -> (o s) i", s=2))
            nc.sync.dma_start(out=bwr[:], in_=base_w.rearrange("o (s i) -> (o s) i", s=2))

        def sw_small():
            sw_state["psc"] = psc = bank("psc", BF16)
            sw_state["pbw"] = pbw = bank("pbw", BF16)
            for j in range(4):
                nc.tensor.transpose(psc[:, P * j : P * j + P], scr[:, P * j : P * j + P], ident_b[:])
            for j in range(4):
                nc.tensor.transpose(pbw[:, P * j : P * j + P], bwr[:, P * j : P * j + P], ident_b[:])

        def sw_small_evac():
            psc, pbw = sw_state["psc"], sw_state["pbw"]
            nc.scalar.activation(
                out=sct[:, 512:1024].rearrange("p (q j) -> p q j", j=4), in_=psc[:].rearrange("p (j q) -> p q j", j=4),
                func=ACTF.Copy, scale=-1.0,
            )
            nc.scalar.copy(out=bwt[:].rearrange("p (q j) -> p q j", j=4), in_=pbw[:].rearrange("p (j q) -> p q j", j=4))

        def sw_positive():
            for k in (0, 1024):
                nc.vector.tensor_scalar(out=sct[:, k : k + 512], in0=sct[:, 512:1024], scalar1=-1.0, scalar2=None, op0=ALU.mult)

        def sw_regroup(swr, copier):
            swg = grp_tile("swg", 2048, F32)
            o = swg[:].rearrange("p (k g e r) -> p e g r k", k=4, e=2, r=4)
            s = swr[:].bitcast(F32).rearrange("p (g e r k) -> p e g r k", e=2, r=4, k=4)
            copier(out=o[:, 0], in_=s[:, 0])
            copier(out=o[:, 1, :, :, 0:2], in_=s[:, 1, :, :, 2:4])
            copier(out=o[:, 1, :, :, 2:4], in_=s[:, 1, :, :, 0:2])
            sw_state["swg"] = swg

        def sw_transpose(kk):
            swg = sw_state["swg"]
            pt = bank("pts%d" % kk, F32)
            for j in range(4):
                nc.tensor.transpose(pt[:, P * j : P * j + P], swg[:, 512 * kk + P * j : 512 * kk + P * j + P], ident_f[:])
            sw_state[kk] = pt

        def sw_products(kk):
            if kk == 0:
                sw_state["swt"] = grp_tile("swt", 4096, BF16)
            first = KFAM[0].index(2 * kk)
            second = 4 + KFAM[1].index(2 * kk + 1)
            nc.vector.tensor_tensor(
                out=sw_state["swt"][:].rearrange("p (a q j) -> p a q j", a=8, j=4)[:, first : second + 1 : second - first],
                in0=sw_state[kk][:].bitcast(BF16).rearrange("p (j q e) -> p e q j", j=4, e=2),
                in1=sct[:, 512 * (kk % 2) : 512 * (kk % 2) + 1024].rearrange("p (e q j) -> p e q j", e=2, j=4), op=ALU.mult,
            )

        def sw_quant():
            nc.vector.quantize_mx(out=swc[:, 0:1024].bitcast(FP8X4), scales=sws[:, 0:1024], in_=sw_state["swt"][:])

        def bw_quant():
            nc.vector.quantize_mx(out=swc[:, 1024:1152].bitcast(FP8X4), scales=sws[:, 1024:1152], in_=bwt[:])

        x_raw = {}
        st = [{} for c in range(NCH)]
        acc = {}
        obx = {}

        def where(c):
            return c // 4, (c // 2) % 2, c % 2

        def x_copy(c, copier):
            b, h, sg = where(c)
            xr, n0 = x_raw[(sg, b)]
            xg = work.tile([P, 2048], BF16, name="xg", bufs=2, align_bytes=64)
            st[c]["xg"] = xg
            copier(
                out=xg[:].bitcast(F32).rearrange("p (h n w) -> p n h w", h=2, w=2),
                in_=xr[:].bitcast(F32).rearrange("p (n h w) -> p n h w", h=2, w=2)[:, MC * h - n0 : MC * h - n0 + MC],
            )

        def x_permute(xn):
            st[0]["xp"] = []
            for h in range(2):
                xp = psum.tile([P, 1024], BF16, name="xp", tag="s1", bufs=6)
                for k in range(2):
                    nc.tensor.matmul(
                        out=xp[:, 512 * k : 512 * k + 512], lhsT=perm[:],
                        rhs=xn[:].rearrange("p (k n h f) -> p k h n f", k=2, h=2, f=4)[:, k, h], start=True, stop=True,
                    )
                st[0]["xp"].append(xp)

        def x_evac(h, copier):
            if h == 0:
                st[0]["xg"] = work.tile([P, 2048], BF16, name="xg", bufs=2, align_bytes=64)
            copier(out=st[0]["xg"][:, 1024 * h : 1024 * h + 1024], in_=st[0]["xp"][h][:])

        def x_quant(c):
            xg = st[c]["xg"]
            xc = work.tile([P, 512], U32, name="xc", bufs=2, align_bytes=64)
            xs = work.tile([P, 512], U8, name="xs", bufs=2, align_bytes=64)
            nc.vector.quantize_mx(out=xc[:].bitcast(FP8X4), scales=xs[:], in_=xg[:])
            st[c]["xc"] = xc
            st[c]["xs"] = xs

        def m1(c):
            sg = c % 2
            xc, xs = st[c]["xc"], st[c]["xs"]
            st[c]["ps"] = []
            for jj in range(2):
                ps = bank("ps1", F32)
                for j2 in range(2):
                    j = 2 * jj + j2
                    for half in range(2):
                        wcol = slice(256 * j + P * half, 256 * j + P * half + P)
                        xcol = slice(MC * half, MC * half + MC)
                        nc.tensor.matmul_mx(
                            out=ps[:, MC * j2 : MC * j2 + MC],
                            lhsT=w_codes[sg][:, wcol].bitcast(FP8X4),
                            lhsT_scale=w_scales[sg][:, wcol],
                            rhs=xc[:, xcol].bitcast(FP8X4),
                            rhs_scale=xs[:, xcol],
                            start=(half == 0),
                            stop=(half == 1),
                        )
                st[c]["ps"].append(ps)

        def tanh(c):
            sg = c % 2
            x = work.tile([P, CW], F32, name="x", bufs=2)
            for j in range(4):
                nc.scalar.activation(
                    out=x[:, MC * j : MC * j + MC],
                    in_=st[c]["ps"][j // 2][:, MC * (j % 2) : MC * (j % 2) + MC],
                    func=ACTF.Tanh,
                    bias=bias[:, 4 * sg + j : 4 * sg + j + 1],
                    scale=1.0,
                )
            st[c]["xj"] = x

        def weave(c, parts=(0, 1)):
            if parts[0] == 0:
                st[c]["x"] = []
            for half in parts:
                xi = bank("xi", F32)
                nc.tensor.matmul(
                    out=xi[:], lhsT=ident_f[:],
                    rhs=st[c]["xj"][:].rearrange("p (j h m) -> p h m j", j=4, h=2)[:, half],
                    start=True, stop=True,
                )
                st[c]["x"].append(xi)

        def halves(c, src, dst):
            return [(st[c][src][half][:], dst[:, 512 * half : 512 * half + 512]) for half in range(2)]

        def pair(c, nm, tag, bufs):
            if nm not in st[c]:
                st[c][nm] = work.tile([P, 2, CW], F32, name=nm, tag=tag, bufs=bufs)
            return st[c][nm]

        def act(out_, in_, func, scale, bi):
            if bi is None:
                nc.scalar.activation(out=out_, in_=in_, func=func, scale=scale)
            else:
                nc.scalar.activation(out=out_, in_=in_, func=func, bias=cbias(bi), scale=scale)

        def dist(c):
            t = pair(c, "fa", "fa", 2)
            for half in range(2):
                for f in range(2):
                    s, o = halves(c, "x", t[:, f, :])[half]
                    act(o, s, ACTF.Abs, 2.5, (B_M05, B_P05)[f])

        def fold(c, k):
            if k == 0:
                st[c]["vb"] = work.tile([P, CW], F32, name="vb", bufs=1)
            t = st[c]["vb"]
            act(t[:], st[c]["fa"][:, 0, :] if k == 0 else t[:], ACTF.Abs, 1.0, (B_M2, B_M1)[k])

        def squares(c, nm, scale, bi, fs):
            act(pair(c, nm, "sq", 4)[:, fs], st[c]["fa"][:, fs], ACTF.Square, scale, bi)

        def cap_square(c, f):
            act(pair(c, "q", "sq", 4)[:, f, :], st[c]["vb"][:], ACTF.Square, (-1.0, 1.0)[f], (B_1HB, B_HB)[f])

        def let_gpsimd():
            go = work.tile([P, 4], F32, name="go", bufs=2)
            nc.vector.tensor_copy(out=go[:], in_=lines[:])
            return go

        def cap_line(c, f, engine, consts):
            engine.tensor_scalar(
                out=pair(c, "l", "lin", 2)[:, f, :], in0=st[c]["vb"][:], scalar1=consts[:, f : f + 1],
                scalar2=consts[:, 2 + f : 3 + f], op0=ALU.mult, op1=ALU.add,
            )

        def arms(c):
            if "arms" not in st[c]:
                st[c]["arms"] = work.tile([P, 2, 2, CW], BF16, name="arms", align_bytes=64)
            return st[c]["arms"]

        def outer_arms(c, fs):
            nc.vector.scalar_tensor_tensor(
                out=arms(c)[:, 0, fs], in0=st[c]["fa"][:, fs], scalar=-2.0, in1=st[c]["sp"][:, fs], op0=ALU.add, op1=ALU.mult
            )

        def inner_arm(c, f):
            sl = st[c]["sl"][:, f, :]
            parts = halves(c, "x", arms(c)[:, 1, f, :])
            w = CW // len(parts)
            for k, (s, o) in enumerate(parts):
                nc.vector.scalar_tensor_tensor(
                    out=o, in0=s, scalar=(-0.2, 0.2)[f], in1=sl[:, w * k : w * k + w], op0=ALU.add, op1=ALU.mult
                )

        def caps(c, fs):
            if "cap" not in st[c]:
                st[c]["cap"] = work.tile([P, 2, CW], BF16, name="cap", bufs=1, align_bytes=64)
            nc.vector.scalar_tensor_tensor(
                out=st[c]["cap"][:, fs], in0=st[c]["q"][:, fs], scalar=cp, in1=st[c]["l"][:, fs], op0=ALU.add, op1=ALU.mult
            )

        def cap_arms(c, fs):
            o = arms(c)[:, 0, fs]
            nc.vector.tensor_tensor(out=o, in0=o, in1=st[c]["cap"][:, fs], op=ALU.max)

        def plane(c, fs, n):
            if "fam" not in st[c]:
                st[c]["fam"] = work.tile([P, 2, 4, CW], BF16, name="fam", tag="fam", bufs=1, align_bytes=64)
            return st[c]["fam"][:, fs, n, :]

        def split_outer(c, side, fs, scalar=False):
            o, i, sign = plane(c, fs, 2 * side), arms(c)[:, 0, fs], sgn[:, side : side + 1]
            if scalar:
                nc.scalar.activation(out=o, in_=i, func=ACTF.Relu, scale=sign)
            else:
                nc.vector.tensor_scalar(out=o, in0=i, scalar1=sign, scalar2=0.0, op0=ALU.mult, op1=ALU.max)

        def split_inner(c, side, fs):
            nc.vector.tensor_scalar(
                out=plane(c, fs, 2 * side + 1), in0=arms(c)[:, 1, fs], scalar1=sgn[:, 1 - side : 2 - side], scalar2=0.0,
                op0=ALU.mult, op1=ALU.min,
            )

        def cap_rest(c, fs):
            rest = st[c]["fam"][:, fs, 1:4:2, :]
            nc.vector.tensor_tensor(
                out=rest, in0=rest, in1=st[c]["cap"][:, fs].unsqueeze(2).to_broadcast([P, fs.stop - fs.start, 2, CW]), op=ALU.max
            )

        def quant_planes(c, f, a0_, a1_):
            if "codes" not in st[c]:
                st[c]["codes"] = work.tile([P, 2 * CW], U32, name="codes", align_bytes=64)
                st[c]["scl"] = work.tile([P, 2 * CW], U8, name="scl", align_bytes=64)
            cols = slice(CW * f + MC * a0_, CW * f + MC * a1_)
            nc.vector.quantize_mx(
                out=st[c]["codes"][:, cols].bitcast(FP8X4), scales=st[c]["scl"][:, cols],
                in_=st[c]["fam"][:, f, a0_:a1_].rearrange("p a w -> p (a w)"),
            )

        def quant_family(c, f):
            quant_planes(c, f, 0, 4)

        def silu(c):
            if c % 2 == 0:
                st[c]["sil"] = work.tile([P, 2, CW], BF16, name="sil", bufs=2, align_bytes=64)
            sil = st[c - c % 2]["sil"]
            for s, o in halves(c, "x", sil[:, c % 2, :]):
                nc.scalar.activation(out=o, in_=s, func=ACTF.Silu)

        def quant_silu(c):
            bc = work.tile([P, 2 * MC], U32, name="bc", bufs=1, align_bytes=64)
            bs = work.tile([P, 2 * MC], U8, name="bs", bufs=1, align_bytes=64)
            nc.vector.quantize_mx(out=bc[:].bitcast(FP8X4), scales=bs[:], in_=st[c]["sil"][:].rearrange("p k w -> p (k w)"))
            for k in range(2):
                st[c + k]["bc"], st[c + k]["bs"] = bc[:, MC * k : MC * k + MC], bs[:, MC * k : MC * k + MC]

        def m2(c, mt, planes, first, last):
            if first:
                if c == NCH - 1 and mt == 1:
                    acc[(c, mt)] = bank("acc1", F32)[:, 0:P]
                else:
                    if mt == 0:
                        acc[c] = psum.tile([P, 512], F32, name="acc", tag="acc", bufs=2)
                    acc[(c, mt)] = acc[c][:, P * mt : P * mt + P]
            runs = [(st[c]["bc"], st[c]["bs"], P * mt, 8 * P)] if first else []
            for n in planes:
                runs.append((st[c]["codes"], st[c]["scl"], MC * n + P * mt, P * n))
            for k, (lhs, lhs_s, m0, q0) in enumerate(runs):
                nc.tensor.matmul_mx(
                    out=acc[(c, mt)],
                    lhsT=lhs[:, m0 : m0 + P].bitcast(FP8X4),
                    lhsT_scale=lhs_s[:, m0 : m0 + P],
                    rhs=swc[:, q0 : q0 + P].bitcast(FP8X4),
                    rhs_scale=sws[:, q0 : q0 + P],
                    start=(first and k == 0),
                    stop=(last and k == len(runs) - 1),
                )

        def finish(c):
            b, h, sg = where(c)
            cols = slice(sg, P, 2)
            rows = out[b, MC * h : MC * h + MC, :].rearrange("(mt p) o -> p mt o", p=P)
            if sg == 0:
                ob = work.tile([P, 2, 64], F32, name="ob", bufs=2)
                nc.scalar.copy(out=ob[:], in_=acc[c][:, 0 : 2 * P].rearrange("p (mt q) -> p mt q", mt=2)[:, :, cols])
                obx[c] = ob
            elif c < NCH - 1:
                res = work.tile([P, 2, 64], F32, name="res", bufs=2)
                both = acc[c][:, 0 : 2 * P].rearrange("p (mt q) -> p mt q", mt=2)[:, :, cols]
                nc.vector.tensor_tensor(out=res[:], in0=both, in1=obx[c - 1][:], op=ALU.add)
                nc.sync.dma_start(out=rows, in_=res[:])
            else:
                for mt in range(2):
                    res = work.tile([P, 64], F32, name="last", bufs=2)
                    nc.vector.tensor_tensor(out=res[:], in0=acc[(c, mt)][:, cols], in1=obx[c - 1][:, mt, :], op=ALU.add)
                    nc.sync.dma_start(out=rows[:, mt, :], in_=res[:])

        V, S = nc.vector.tensor_copy, nc.scalar.copy
        BOTH, EVEN, ODD = slice(0, 2), slice(0, 1), slice(1, 2)
        load_w(0, (0, 1))
        xn = load_x_first()
        nc.sync.dma_start(out=brow[0:4, :], in_=bx.rearrange("(r c) -> r c", c=P))
        nc.sync.dma_start(out=brow[4:8, :], in_=by.rearrange("(r c) -> r c", c=P))
        load_w(0, (2, 3))
        sw_raw = load_sw()
        load_small()
        load_w(1, (0, 1, 2, 3))
        load_x(1, 0)
        load_x(0, 0, MC)

        keep_clock(5, w_codes[0], w_scales[0], "acc", 2)
        for j in range(2):
            w_regroup(0, j, V)
            w_transpose(0, j)
        x_permute(xn)
        w_evac(0, 0, S)
        w_evac(0, 1, S)
        for j in range(2, 4):
            w_regroup(0, j, V)
            w_transpose(0, j)
        pb0 = bank("pb0", BF16)
        nc.tensor.transpose(pb0[:, 0:P], brow[:], ident_b[:])
        bias = keep.tile([P, 8], F32, name="bias")
        x_evac(0, S)
        x_evac(1, S)
        w_quant(0, 0, 2)
        keep_clock(2, w_codes[0], w_scales[0], "acc", 2)
        w_evac(0, 2, S)
        w_evac(0, 3, S)
        x_quant(0)
        nc.vector.tensor_copy(out=bias[:], in_=pb0[:, 0:8])
        w_quant(0, 2, 4)
        m1(0)
        sw_regroup(sw_raw, V)
        sw_small()
        tanh(0)
        sw_transpose(0)
        weave(0, (0,))
        sw_small_evac()
        for j in range(2):
            w_regroup(1, j, V)
        sw_transpose(1)
        weave(0, (1,))
        sw_positive()
        dist(0)
        sw_products(0)
        sw_products(1)
        sw_transpose(2)
        sw_transpose(3)
        fold(0, 0)
        squares(0, "sl", rc, None, BOTH)
        sw_products(2)
        sw_products(3)
        fold(0, 1)
        for j in range(2, 4):
            w_regroup(1, j, V)
        for j in range(4):
            w_transpose(1, j)
            w_evac(1, j, S)
        sw_quant()
        x_copy(1, V)
        bw_quant()
        x_quant(1)
        go = let_gpsimd()
        for f in range(2):
            cap_line(0, f, nc.gpsimd, go)
        inner_arm(0, 0)
        inner_arm(0, 1)
        squares(0, "sp", r6, B_M2R6, BOTH)
        w_quant(1, 0, 4)
        m1(1)
        x_copy(2, V)
        outer_arms(0, BOTH)
        for f in range(2):
            cap_square(0, f)
        tanh(1)
        weave(1)
        silu(0)
        load_x(0, 1)
        x_quant(2)
        m1(2)
        caps(0, BOTH)
        x_copy(3, V)
        load_x(1, 1)

        for c in range(1, NCH):
            p = c - 1
            if c % 2 and c > 2:
                finish(c - 3)
            if 1 < c < NCH - 1:
                weave(c + 1)
            dist(c)
            fold(c, 0)
            squares(c, "sl", rc, None, BOTH)
            fold(c, 1)
            squares(c, "sp", r6, B_M2R6, BOTH)
            if c == 1:
                tanh(2)
                weave(2)
            for side in range(2):
                split_inner(p, side, BOTH)
            cap_arms(p, BOTH)
            if c + 2 < NCH:
                x_quant(c + 2)
                m1(c + 2)
            if p < 5:
                for side in range(2):
                    split_outer(p, side, BOTH)
            go = let_gpsimd()
            cap_rest(p, BOTH)
            for f in range(2):
                cap_line(c, f, nc.gpsimd, go)
                inner_arm(c, f)
            for f in range(2):
                cap_square(c, f)
            if p >= 5:
                for fs in (EVEN, ODD):
                    for side in range(2):
                        split_outer(p, side, fs, scalar=True)
            silu(c)
            if c + 3 < NCH:
                x_copy(c + 3, S)
            if c + 2 < NCH:
                tanh(c + 2)
            if p > 0 and p % 2 == 0:
                finish(p - 1)
            outer_arms(c, BOTH)
            if c < NCH - 1:
                quant_family(p, 0)
                caps(c, BOTH)
                quant_family(p, 1)
                if c % 2:
                    quant_silu(p)
            else:
                caps(c, BOTH)
                quant_family(p, 0)
                cap_arms(c, EVEN)
                cap_arms(c, ODD)
                quant_family(p, 1)
                quant_silu(p)
            for mt in range(2):
                m2(p, mt, range(8), True, True)

        p = NCH - 1
        keep_clock(4, swc, sws, "s1", 6)
        for fs in (EVEN, ODD):
            for side in range(2):
                split_inner(p, side, fs)
                split_outer(p, side, fs, scalar=True)
        finish(p - 1)
        cap_rest(p, EVEN)
        cap_rest(p, ODD)
        quant_family(p, 0)
        for mt in range(2):
            m2(p, mt, range(4), True, False)
        for a in (0, 2):
            quant_planes(p, 1, a, a + 2)
            for mt in range(2):
                m2(p, mt, (4 + a, 5 + a), False, a == 2)
        finish(p)
